import numpy as np
import ml_dtypes


def mxq(x, axis, fmt="e4m3"):
    dtype, down = {"e4m3": (ml_dtypes.float8_e4m3fn, 7), "e5m2": (ml_dtypes.float8_e5m2, 14)}[fmt]
    v = np.moveaxis(np.asarray(x, np.float32).astype(ml_dtypes.bfloat16).astype(np.float64), axis, -1)
    blocks = v.reshape(v.shape[:-1] + (-1, 32))
    amax = np.abs(blocks).max(-1, keepdims=True)
    byte = np.maximum(np.where(amax > 0, np.frexp(amax)[1] - 1 + 127, 0) - down, 1)
    scale = np.exp2(byte - 127.0)
    codes = (blocks / scale).astype(np.float32).astype(dtype).astype(np.float64)
    return np.moveaxis((codes * scale).reshape(v.shape), -1, axis)


WIDE = False


def mx_kscale(k):
    if not WIDE:
        return np.ones(k)
    levels = np.array([10, -10, 5, -5, 0])
    a = np.random.permutation(np.resize(levels, k // 512 * 4)).reshape(k // 512, 4)
    idx = np.arange(k)
    return np.exp2(a[idx // 512, idx % 128 // 32])


BF16 = ml_dtypes.bfloat16


def bf(x):
    return np.asarray(x, np.float32).astype(BF16)


def f64(x):
    return np.asarray(x).astype(np.float64)


B, S, P, D, H, HD = 1, 512, 1024, 2048, 16, 128
T = P + S


def heads(t):
    return t.reshape(B, -1, H, HD).transpose(0, 2, 1, 3)


def setup_inputs():
    s = mx_kscale(D)
    return {
        "x": bf(np.random.standard_normal((B, S, D)) * s),
        "q": bf(np.random.standard_normal((B, H, S, HD)) * 1.5),
        "k_new": bf(np.random.standard_normal((B, H, S, HD)) * 1.5),
        "past_k": bf(np.random.standard_normal((B, H, P, HD)) * 1.5),
        "past_v": bf(np.random.standard_normal((B, H, P, HD))),
        "Wv": bf(np.random.standard_normal((D, D)) / np.sqrt(D) / s[None, :]),
        "bv": bf(np.random.standard_normal(D) * 0.3),
    }


def reference(x, q, k_new, past_k, past_v, Wv, bv):
    v_new = heads((mxq(f64(x), 2, "e4m3") @ mxq(f64(Wv), 1, "e4m3").T) + f64(bv))
    v_cached = np.concatenate([f64(past_v), v_new], axis=2)
    qf = f64(q)
    scores = np.concatenate([qf @ f64(past_k).transpose(0, 1, 3, 2), qf @ f64(k_new).transpose(0, 1, 3, 2)], axis=3) * (1.0 / np.sqrt(HD))
    q_pos = np.arange(T - S, T)[:, None]
    k_pos = np.arange(T)[None, :]
    scores = np.where(q_pos >= k_pos, scores, -np.inf)
    e = np.exp(scores - scores.max(-1, keepdims=True))
    out = (mxq(e, 3, "e4m3") @ mxq(v_cached, 2, "e4m3")) / e.sum(-1, keepdims=True)
    return out.transpose(0, 2, 1, 3).reshape(B, S, D)

@@ -1,0 +1,343 @@
+import math
+from contextlib import ExitStack
+
+import concourse.mybir as mybir
+from concourse.masks import make_identity
+
+F32 = mybir.dt.float32
+BF16 = mybir.dt.bfloat16
+U32 = mybir.dt.uint32
+U8 = mybir.dt.uint8
+FP8X4 = mybir.dt.float8_e4m3fn_x4
+ALU = mybir.AluOpType
+ACTF = mybir.ActivationFunctionType
+AX = mybir.AxisListType
+
+P = 128
+S, PAST, D, H, HD = 512, 1024, 2048, 16, 128
+NT = S // P
+SCALE = 1.0 / math.sqrt(HD)
+MASKED = -1.0e30
+FLOPS = 2 * S * D * D + 2 * 2 * H * S * (PAST + S) * HD
+
+MANUAL = True
+R2 = False
+SPLIT = 4
+V_REGROUP = "gpsimd"
+
+
+def tile_flashattentionmodule_pa_kernel(tc, x, q, k_new, past_k, past_v, Wv, bv, out):
+    nc = tc.nc
+    with ExitStack() as ctx:
+        const = ctx.enter_context(tc.tile_pool(name="const", bufs=1))
+        ld = ctx.enter_context(tc.tile_pool(name="ld", bufs=3))
+        hd = ctx.enter_context(tc.tile_pool(name="hd", bufs=2))
+        tl = ctx.enter_context(tc.tile_pool(name="tl", bufs=3))
+        ps_s = ctx.enter_context(tc.psum_pool(name="ps_s", bufs=3))
+        ps_t = ctx.enter_context(tc.psum_pool(name="ps_t", bufs=5))
+        ps_o = ps_t
+        one = ctx.enter_context(tc.tile_pool(name="one", bufs=1))
+        if MANUAL:
+            ctx.enter_context(tc.manual_schedule())
+
+        NTILES = H * NT
+        Q_SB, KN_SB, PK_SB, PV_SB, W_SB = {}, {}, {}, {}, {}
+        QKT, WG, WC, WS, VG, VC, VS, EC, ES, Y_PS = {}, {}, {}, {}, {}, {}, {}, {}, {}, {}
+        S_PS, S_SB, E_SB, T_PS, ETG = {}, {}, {}, {}, {}
+
+        def load_qk(h):
+            Q_SB[h] = ld.tile([P, NT, HD], BF16, name="q_sb", tag="q_sb")
+            nc.sync.dma_start(out=Q_SB[h][:], in_=q[0, h].rearrange("(a p) d -> p a d", p=P))
+            KN_SB[h] = ld.tile([P, NT, HD], BF16, name="kn_sb", tag="kn_sb")
+            nc.sync.dma_start(out=KN_SB[h][:], in_=k_new[0, h].rearrange("(a p) d -> p a d", p=P))
+            PK_SB[h] = ld.tile([P, 8, HD], BF16, name="pk_sb", tag="pk_sb")
+            nc.sync.dma_start(out=PK_SB[h][:], in_=past_k[0, h].rearrange("(p r) d -> p r d", r=8))
+
+        def load_wv(h):
+            W_SB[h] = ld.tile([P, D], BF16, name="w_sb", tag="w_sb")
+            nc.sync.dma_start(out=W_SB[h][:], in_=Wv[h * HD:(h + 1) * HD, :])
+            PV_SB[h] = ld.tile([P, 8, HD], BF16, name="pv_sb", tag="pv_sb")
+            nc.sync.dma_start(out=PV_SB[h][:], in_=past_v[0, h].rearrange("(p r) d -> p r d", r=8))
+
+        load_qk(0)
+        x_sb = const.tile([P, NT, D], BF16, name="x_sb")
+        nc.sync.dma_start(out=x_sb[:], in_=x[0].rearrange("(a p) k -> p a k", p=P))
+        load_wv(0)
+        load_qk(1)
+        bvb = const.tile([P, D], BF16, name="bvb")
+        nc.sync.dma_start(out=bvb[:], in_=bv.partition_broadcast(P))
+
+        ident_bf = const.tile([P, P], BF16, name="ident_bf")
+        make_identity(nc, ident_bf[:])
+        ident_f = const.tile([P, P], F32, name="ident_f")
+        make_identity(nc, ident_f[:])
+        mask_f = const.tile([P, P], F32, name="mask_f")
+        nc.gpsimd.memset(mask_f[:], 0.0)
+        nc.gpsimd.affine_select(out=mask_f[:], in_=mask_f[:], compare_op=ALU.is_ge, fill=MASKED, base=0,
+                                pattern=[[-1, P]], channel_multiplier=1)
+        mask_bf = const.tile([P, P], BF16, name="mask_bf")
+        nc.vector.tensor_copy(out=mask_bf[:], in_=mask_f[:])
+        ENG = []
+        for i in range(2):
+            eng = const.tile([P, NT * P * 4], BF16, name="eng%d" % i, align_bytes=64)
+            nc.gpsimd.memset(eng[:], 0.0)
+            ENG.append(eng)
+        mn3 = const.tile([P, NTILES * 4], F32, name="mn3")
+        nm = const.tile([P, NTILES], F32, name="nm")
+        sums = const.tile([P, NTILES], F32, name="sums")
+        rinv = const.tile([P, NTILES], F32, name="rinv")
+        xg = const.tile([P, 4 * S * 4], BF16, name="xg", align_bytes=64)
+        x_codes = const.tile([P, 4 * S], U32, name="x_codes", align_bytes=64)
+        x_scales = const.tile([P, 4 * S], U8, name="x_scales", align_bytes=64)
+
+        def evac(eng_name, out_ap, in_ap):
+            if eng_name == "v":
+                nc.vector.tensor_copy(out=out_ap, in_=in_ap)
+            else:
+                nc.scalar.copy(out=out_ap, in_=in_ap)
+
+        def x_part(a, gp, e):
+            xw = x_sb[:, a, :].bitcast(F32)
+            tx = ps_t.tile([P, 4, P], F32, name="tx", tag="t")
+            for j in range(4):
+                wb = gp * 4 + j
+                nc.tensor.transpose(tx[:, j, :], xw[:, wb * P:(wb + 1) * P], ident_f[:])
+            xgw = xg[:].bitcast(F32).rearrange("p (g k u) -> p g k u", g=4, u=2)
+            evac(e, xgw[:, 2 * gp:2 * gp + 2, a * P:(a + 1) * P, :], tx[:].rearrange("p (g u) k -> p g k u", u=2))
+
+        def x_quant(i):
+            nc.vector.quantize_mx(out=x_codes[:, i * 1024:(i + 1) * 1024].bitcast(FP8X4),
+                                  scales=x_scales[:, i * 1024:(i + 1) * 1024],
+                                  in_=xg[:, i * 4096:(i + 1) * 4096])
+
+        def prep_qk(h, part, e):
+            if part == 0:
+                QKT[h] = hd.tile([P, 16 * P], BF16, name="qkT", tag="qkT")
+            tq = ps_t.tile([P, 8, P], BF16, name="tq", tag="t")
+            for j in range(8):
+                if part == 0:
+                    src = Q_SB[h][:, j, :] if j < 4 else KN_SB[h][:, j - 4, :]
+                else:
+                    src = PK_SB[h][:, j, :]
+                nc.tensor.transpose(tq[:, j, :], src, ident_bf[:])
+            evac(e, QKT[h][:, part * 1024:(part + 1) * 1024], tq[:].rearrange("p j i -> p (j i)"))
+
+        def prep_w(h, gp, e):
+            if gp == 0:
+                WG[h] = hd.tile([P, 4 * HD * 4], BF16, name="wg", tag="wg", align_bytes=64)
+            ww = W_SB[h][:].bitcast(F32)
+            tw = ps_t.tile([P, 4, P], F32, name="tw", tag="t")
+            for j in range(4):
+                wb = gp * 4 + j
+                nc.tensor.transpose(tw[:, j, :], ww[:, wb * P:(wb + 1) * P], ident_f[:])
+            wgw = WG[h][:].bitcast(F32).rearrange("p (g o u) -> p g o u", g=4, u=2)
+            evac(e, wgw[:, 2 * gp:2 * gp + 2, :, :], tw[:].rearrange("p (g u) o -> p g o u", u=2))
+
+        def quant_w(h):
+            WC[h] = hd.tile([P, 4 * HD], U32, name="wc", tag="wc", align_bytes=64)
+            WS[h] = hd.tile([P, 4 * HD], U8, name="ws", tag="ws", align_bytes=64)
+            nc.vector.quantize_mx(out=WC[h][:].bitcast(FP8X4), scales=WS[h][:], in_=WG[h][:])
+
+        def regroup_v(h, piece):
+            if piece == 0:
+                VG[h] = hd.tile([P, 3 * HD * 4], BF16, name="vg", tag="vg", align_bytes=64)
+            g, half = divmod(piece, 2)
+            dst = VG[h][:, g * 512 + half * 256:g * 512 + half * 256 + 256].rearrange("p (d t) -> p d t", t=4)
+            src = PV_SB[h][:, 4 * g:4 * g + 4, half * 64:half * 64 + 64].rearrange("p t d -> p d t")
+            if V_REGROUP == "gpsimd":
+                nc.gpsimd.tensor_scalar(out=dst, in0=src, scalar1=1.0, scalar2=0.0, op0=ALU.mult, op1=ALU.add)
+            else:
+                nc.vector.tensor_copy(out=dst, in_=src)
+
+        def proj(h):
+            Y_PS[h] = ps_o.tile([P, NT, HD], F32, name="y_ps", tag="t")
+            for jt in range(NT):
+                for g in range(4):
+                    nc.tensor.matmul_mx(
+                        out=Y_PS[h][:, jt, :],
+                        lhsT=x_codes[:, g * S + jt * P:g * S + (jt + 1) * P].bitcast(FP8X4),
+                        lhsT_scale=x_scales[:, g * S + jt * P:g * S + (jt + 1) * P],
+                        rhs=WC[h][:, g * HD:(g + 1) * HD].bitcast(FP8X4),
+                        rhs_scale=WS[h][:, g * HD:(g + 1) * HD],
+                        start=(g == 0), stop=(g == 3))
+
+        def y_evac(h):
+            dst = VG[h][:, 2 * HD * 4:3 * HD * 4].rearrange("p (d t) -> p d t", t=4)
+            nc.vector.tensor_tensor(out=dst, in0=Y_PS[h][:].rearrange("p t d -> p d t"),
+                                    in1=bvb[:, h * HD:(h + 1) * HD].unsqueeze(2).to_broadcast([P, HD, 4]), op=ALU.add)
+
+        def quant_v(h):
+            VC[h] = hd.tile([P, 3 * HD], U32, name="vc", tag="vc", align_bytes=64)
+            VS[h] = hd.tile([P, 3 * HD], U8, name="vs", tag="vs", align_bytes=64)
+            nc.vector.quantize_mx(out=VC[h][:, 0:256].bitcast(FP8X4), scales=VS[h][:, 0:256], in_=VG[h][:, 0:1024])
+            nc.vector.quantize_mx(out=VC[h][:, 256:384].bitcast(FP8X4), scales=VS[h][:, 256:384], in_=VG[h][:, 1024:1536])
+
+        def widths(it):
+            return [512, 512, P * (it + 1)]
+
+        def st1(n):
+            h, it = divmod(n, NT)
+            kt = QKT[h]
+            lhsT = kt[:, it * P:(it + 1) * P]
+            sA = ps_s.tile([P, 512], F32, name="sA", tag="s")
+            nc.tensor.matmul(out=sA[:], lhsT=lhsT, rhs=kt[:, 1024:1536], start=True, stop=True)
+            sB = ps_s.tile([P, 512], F32, name="sB", tag="s")
+            nc.tensor.matmul(out=sB[:], lhsT=lhsT, rhs=kt[:, 1536:2048], start=True, stop=True)
+            sC = ps_s.tile([P, 512], F32, name="sC", tag="s")
+            if it > 0:
+                nc.tensor.matmul(out=sC[:, 0:it * P], lhsT=lhsT, rhs=kt[:, 512:512 + it * P], start=True, stop=True)
+            nc.tensor.matmul(out=sC[:, it * P:(it + 1) * P], lhsT=lhsT, rhs=kt[:, 512 + it * P:512 + (it + 1) * P],
+                             start=True, stop=False)
+            nc.tensor.matmul(out=sC[:, it * P:(it + 1) * P], lhsT=ident_bf[:], rhs=mask_bf[:], start=False, stop=True)
+            S_PS[n] = [sA, sB, sC]
+
+        def st2(n):
+            h, it = divmod(n, NT)
+            S_SB[n] = tl.tile([P, 1536], F32, name="s_sb", tag="s_sb")
+            off = 0
+            for j, w in enumerate(widths(it)):
+                nc.vector.tensor_scalar(out=S_SB[n][:, off:off + w], in0=S_PS[n][j][:, 0:w], scalar1=-SCALE, scalar2=None,
+                                        op0=ALU.mult, op1=ALU.min, accum_out=mn3[:, 4 * n + j:4 * n + j + 1])
+                off += w
+
+        def st2b(n):
+            nc.vector.tensor_reduce(out=nm[:, n:n + 1], in_=mn3[:, 4 * n:4 * n + 3], axis=AX.X, op=ALU.min)
+
+        def st3(n):
+            h, it = divmod(n, NT)
+            w = sum(widths(it))
+            E_SB[n] = tl.tile([P, 1536], BF16, name="e_sb", tag="e_sb")
+            nc.scalar.activation(out=E_SB[n][:, 0:w], in_=S_SB[n][:, 0:w], func=ACTF.Exp, bias=nm[:, n:n + 1], scale=-1.0,
+                                 accum_out=sums[:, n:n + 1])
+
+        def st4(n):
+            h, it = divmod(n, NT)
+            tP = ps_t.tile([P, 8, P], BF16, name="tP", tag="t")
+            for r in range(8):
+                nc.tensor.transpose(tP[:, r, :], E_SB[n][:, r * P:(r + 1) * P], ident_bf[:])
+            tN = ps_t.tile([P, 8, P], BF16, name="tN", tag="t")
+            for t in range(it + 1):
+                nc.tensor.transpose(tN[:, t, :], E_SB[n][:, 1024 + t * P:1024 + (t + 1) * P], ident_bf[:])
+            T_PS[n] = [tP, tN]
+
+        ETC = {}
+
+        def st5a(n, e):
+            if R2:
+                ETC[n] = tl.tile([P, 1024], BF16, name="etc", tag="etc")
+                evac(e, ETC[n][:], T_PS[n][0][:].rearrange("p r i -> p (r i)"))
+            else:
+                ETG[n] = tl.tile([P, 1024], BF16, name="etg", tag="etg", align_bytes=64)
+                evac(e, ETG[n][:].rearrange("p (g i t) -> p g i t", g=2, t=4), T_PS[n][0][:].rearrange("p (g t) i -> p g i t", t=4))
+
+        def st5g(n):
+            ETG[n] = one.tile([P, 1024], BF16, name="etg", tag="etg", align_bytes=64)
+            nc.gpsimd.tensor_scalar(out=ETG[n][:].rearrange("p (g i t) -> p g i t", g=2, t=4),
+                                    in0=ETC[n][:].rearrange("p (g t i) -> p g i t", g=2, t=4),
+                                    scalar1=1.0, scalar2=0.0, op0=ALU.mult, op1=ALU.add)
+
+        def st5b(n, e):
+            h, it = divmod(n, NT)
+            dst = ENG[h % 2][:].rearrange("p (a i t) -> p a i t", a=NT, t=4)
+            evac(e, dst[:, it, :, 0:it + 1], T_PS[n][1][:, 0:it + 1, :].rearrange("p t i -> p i t"))
+
+        def st6n(n):
+            h, it = divmod(n, NT)
+            if it == 0:
+                EC[h] = hd.tile([P, NT * 384], U32, name="ec", tag="ec", align_bytes=64)
+                ES[h] = hd.tile([P, NT * 384], U8, name="es", tag="es", align_bytes=64)
+            o = it * 384
+            nc.vector.quantize_mx(out=EC[h][:, o + 256:o + 384].bitcast(FP8X4), scales=ES[h][:, o + 256:o + 384],
+                                  in_=ENG[h % 2][:, it * 512:(it + 1) * 512])
+
+        def st6p(n):
+            h, it = divmod(n, NT)
+            o = it * 384
+            nc.vector.quantize_mx(out=EC[h][:, o:o + 256].bitcast(FP8X4), scales=ES[h][:, o:o + 256], in_=ETG[n][:])
+
+        def unused(n, h, it, o):
+            nc.vector.quantize_mx(out=EC[h][:, o + 256:o + 384].bitcast(FP8X4), scales=ES[h][:, o + 256:o + 384],
+                                  in_=ENG[h % 2][:, it * 512:(it + 1) * 512])
+
+        O_PS = {}
+
+        def pv(h):
+            O_PS[h] = ps_o.tile([P, NT, HD], F32, name="o_ps", tag="t")
+            for it in range(NT):
+                for g in range(3):
+                    o = it * 384 + g * P
+                    nc.tensor.matmul_mx(out=O_PS[h][:, it, :],
+                                        lhsT=EC[h][:, o:o + P].bitcast(FP8X4), lhsT_scale=ES[h][:, o:o + P],
+                                        rhs=VC[h][:, g * HD:(g + 1) * HD].bitcast(FP8X4), rhs_scale=VS[h][:, g * HD:(g + 1) * HD],
+                                        start=(g == 0), stop=(g == 2))
+
+        def finish(h):
+            nc.vector.reciprocal(out=rinv[:, h * NT:(h + 1) * NT], in_=sums[:, h * NT:(h + 1) * NT])
+            o_sb = hd.tile([P, NT, HD], F32, name="o_sb", tag="o_sb")
+            nc.vector.tensor_tensor(out=o_sb[:], in0=O_PS[h][:],
+                                    in1=rinv[:, h * NT:(h + 1) * NT].unsqueeze(2).to_broadcast([P, NT, HD]), op=ALU.mult)
+            nc.sync.dma_start(out=out[0].rearrange("(a p) c -> p a c", p=P)[:, :, h * HD:(h + 1) * HD], in_=o_sb[:])
+
+        def ok(n):
+            return 0 <= n < NTILES
+
+        prep_qk(0, 0, "v")
+        prep_qk(0, 1, "s")
+        st1(0)
+        for k in range(NTILES + 6):
+            h, it = divmod(k, NT)
+            if k == 3:
+                x_quant(0)
+                x_quant(1)
+            if it == 3 and h < H:
+                quant_w(h)
+            if it == 1 and 1 <= h <= H:
+                quant_v(h - 1)
+            if ok(k - 3):
+                st6n(k - 3)
+            if ok(k - 4):
+                st6p(k - 4)
+            if R2 and ok(k - 3):
+                st5g(k - 3)
+            if h < H:
+                regroup_v(h, it)
+            if ok(k):
+                st2(k)
+            if ok(k - 2):
+                st4(k - 2)
+                if (k - 2) % NT < SPLIT:
+                    st5b(k - 2, "v")
+            if ok(k):
+                st2b(k)
+            if ok(k - 1):
+                st3(k - 1)
+            if ok(k - 2):
+                st5a(k - 2, "s")
+                if (k - 2) % NT >= SPLIT:
+                    st5b(k - 2, "s")
+            if k < 3:
+                for i in range(3):
+                    j = k * 3 + i
+                    if j < 8:
+                        x_part(j // 2, j % 2, "s" if i % 2 else "v")
+            if it == 0:
+                if h + 2 < H:
+                    load_qk(h + 2)
+                if h + 1 < H:
+                    load_wv(h + 1)
+                if 1 <= h <= H:
+                    proj(h - 1)
+                if 2 <= h <= H + 1:
+                    pv(h - 2)
+                if 1 <= h <= H:
+                    y_evac(h - 1)
+                if 2 <= h <= H + 1:
+                    finish(h - 2)
+            if it == 1 and h < H:
+                prep_w(h, 0, "s")
+                prep_w(h, 1, "s")
+            if it == 2 and h + 1 < H:
+                prep_qk(h + 1, 0, "s")
+                prep_qk(h + 1, 1, "s")
+            if ok(k + 1):
+                st1(k + 1)

@@ -21,8 +21,12 @@ MASKED = -1.0e30
 FLOPS = 2 * S * D * D + 2 * 2 * H * S * (PAST + S) * HD
 
 MANUAL = True
-R2 = False
-SPLIT = 4
+R2 = True
+SPLIT = 2
+LAG = 4
+VP = [0,0,0,3]
+WE = "ss"
+QE = "ss"
 V_REGROUP = "gpsimd"
 
 
@@ -295,12 +299,14 @@ def tile_flashattentionmodule_pa_kernel(tc, x, q, k_new, past_k, past_v, Wv, bv,
                 quant_v(h - 1)
             if ok(k - 3):
                 st6n(k - 3)
-            if ok(k - 4):
-                st6p(k - 4)
+            if ok(k - LAG):
+                st6p(k - LAG)
             if R2 and ok(k - 3):
                 st5g(k - 3)
             if h < H:
-                regroup_v(h, it)
+                for piece in range(4):
+                    if VP[piece] == it:
+                        regroup_v(h, piece)
             if ok(k):
                 st2(k)
             if ok(k - 2):
@@ -315,6 +321,8 @@ def tile_flashattentionmodule_pa_kernel(tc, x, q, k_new, past_k, past_v, Wv, bv,
                 st5a(k - 2, "s")
                 if (k - 2) % NT >= SPLIT:
                     st5b(k - 2, "s")
+            if k < 3 and ok(k + 1):
+                st1(k + 1)
             if k < 3:
                 for i in range(3):
                     j = k * 3 + i
@@ -334,10 +342,10 @@ def tile_flashattentionmodule_pa_kernel(tc, x, q, k_new, past_k, past_v, Wv, bv,
                 if 2 <= h <= H + 1:
                     finish(h - 2)
             if it == 1 and h < H:
-                prep_w(h, 0, "s")
-                prep_w(h, 1, "s")
+                prep_w(h, 0, WE[0])
+                prep_w(h, 1, WE[1])
             if it == 2 and h + 1 < H:
-                prep_qk(h + 1, 0, "s")
-                prep_qk(h + 1, 1, "s")
-            if ok(k + 1):
+                prep_qk(h + 1, 0, QE[0])
+                prep_qk(h + 1, 1, QE[1])
+            if k >= 3 and ok(k + 1):
                 st1(k + 1)

@@ -21,12 +21,15 @@ MASKED = -1.0e30
 FLOPS = 2 * S * D * D + 2 * 2 * H * S * (PAST + S) * HD
 
 MANUAL = True
-R2 = True
-SPLIT = 2
+TBUFS = {"sd": 1, "tP": 2, "tN": 1, "yo": 1}
+R2 = False
 LAG = 4
-VP = [0,0,0,3]
+NV = 1000
 WE = "ss"
 QE = "ss"
+XQ = 2
+A = {"qk0": -4, "qk1": -3, "w0": -2, "w1": -1, "quant_w": 2, "proj0": 4, "proj1": 5, "y_evac": 6, "quant_v": 7, "pv0": 10, "pv1": 11, "finish": 12, "v0": 0, "v1": 1, "v2": 2, "v3": 3}
+F = {("w0", 0): 0, ("w1", 0): 0, ("quant_w", 0): 3, ("proj0", 15): 62, ("proj1", 15): 63, ("y_evac", 15): 64, ("quant_v", 15): 65, ("pv0", 14): 64, ("pv1", 14): 65, ("finish", 14): 66, ("pv0", 15): 66, ("pv1", 15): 67, ("finish", 15): 68}
 V_REGROUP = "gpsimd"
 
 
@@ -38,8 +41,8 @@ def tile_flashattentionmodule_pa_kernel(tc, x, q, k_new, past_k, past_v, Wv, bv,
         hd = ctx.enter_context(tc.tile_pool(name="hd", bufs=2))
         tl = ctx.enter_context(tc.tile_pool(name="tl", bufs=3))
         ps_s = ctx.enter_context(tc.psum_pool(name="ps_s", bufs=3))
-        ps_t = ctx.enter_context(tc.psum_pool(name="ps_t", bufs=5))
-        ps_o = ps_t
+        ps_t = ctx.enter_context(tc.psum_pool(name="ps_t", bufs=1))
+        ps_o = ctx.enter_context(tc.psum_pool(name="ps_o", bufs=1))
         one = ctx.enter_context(tc.tile_pool(name="one", bufs=1))
         if MANUAL:
             ctx.enter_context(tc.manual_schedule())
@@ -58,16 +61,29 @@ def tile_flashattentionmodule_pa_kernel(tc, x, q, k_new, past_k, past_v, Wv, bv,
             nc.sync.dma_start(out=PK_SB[h][:], in_=past_k[0, h].rearrange("(p r) d -> p r d", r=8))
 
         def load_wv(h):
-            W_SB[h] = ld.tile([P, D], BF16, name="w_sb", tag="w_sb")
+            W_SB[h] = ld.tile([P, D], BF16, name="w_sb", tag="w_sb", bufs=4)
             nc.sync.dma_start(out=W_SB[h][:], in_=Wv[h * HD:(h + 1) * HD, :])
+
+        def load_pv(h):
             PV_SB[h] = ld.tile([P, 8, HD], BF16, name="pv_sb", tag="pv_sb")
             nc.sync.dma_start(out=PV_SB[h][:], in_=past_v[0, h].rearrange("(p r) d -> p r d", r=8))
 
         load_qk(0)
         x_sb = const.tile([P, NT, D], BF16, name="x_sb")
-        nc.sync.dma_start(out=x_sb[:], in_=x[0].rearrange("(a p) k -> p a k", p=P))
-        load_wv(0)
+
+        def load_x(a):
+            nc.sync.dma_start(out=x_sb[:, a, :], in_=x[0, a * P:(a + 1) * P, :])
+
+        load_x(0)
         load_qk(1)
+        load_wv(0)
+        load_x(1)
+        load_x(2)
+        load_x(3)
+        load_pv(0)
+        load_wv(1)
+        load_pv(1)
+        load_wv(2)
         bvb = const.tile([P, D], BF16, name="bvb")
         nc.sync.dma_start(out=bvb[:], in_=bv.partition_broadcast(P))
 
@@ -100,24 +116,29 @@ def tile_flashattentionmodule_pa_kernel(tc, x, q, k_new, past_k, past_v, Wv, bv,
             else:
                 nc.scalar.copy(out=out_ap, in_=in_ap)
 
-        def x_part(a, gp, e):
+        TX = {}
+
+        def x_tr(a, gp, tg):
             xw = x_sb[:, a, :].bitcast(F32)
-            tx = ps_t.tile([P, 4, P], F32, name="tx", tag="t")
+            tx = (ps_o if tg == "yo" else ps_t).tile([P, 4, P], F32, name="tx", tag=tg, bufs=TBUFS[tg])
             for j in range(4):
                 wb = gp * 4 + j
                 nc.tensor.transpose(tx[:, j, :], xw[:, wb * P:(wb + 1) * P], ident_f[:])
-            xgw = xg[:].bitcast(F32).rearrange("p (g k u) -> p g k u", g=4, u=2)
-            evac(e, xgw[:, 2 * gp:2 * gp + 2, a * P:(a + 1) * P, :], tx[:].rearrange("p (g u) k -> p g k u", u=2))
+            TX[(a, gp)] = tx
 
-        def x_quant(i):
-            nc.vector.quantize_mx(out=x_codes[:, i * 1024:(i + 1) * 1024].bitcast(FP8X4),
-                                  scales=x_scales[:, i * 1024:(i + 1) * 1024],
-                                  in_=xg[:, i * 4096:(i + 1) * 4096])
+        def x_ev(a, gp, e):
+            xgw = xg[:].bitcast(F32).rearrange("p (a g k u) -> p a g k u", a=NT, g=4, u=2)
+            evac(e, xgw[:, a, 2 * gp:2 * gp + 2, :, :], TX[(a, gp)][:].rearrange("p (g u) k -> p g k u", u=2))
 
-        def prep_qk(h, part, e):
+        def x_quant(a):
+            nc.vector.quantize_mx(out=x_codes[:, a * 512:(a + 1) * 512].bitcast(FP8X4),
+                                  scales=x_scales[:, a * 512:(a + 1) * 512],
+                                  in_=xg[:, a * 2048:(a + 1) * 2048])
+
+        def prep_qk(h, part, e, tg="sd"):
             if part == 0:
-                QKT[h] = hd.tile([P, 16 * P], BF16, name="qkT", tag="qkT")
-            tq = ps_t.tile([P, 8, P], BF16, name="tq", tag="t")
+                QKT[h] = hd.tile([P, 16 * P], BF16, name="qkT", tag="qkT", bufs=3)
+            tq = ps_t.tile([P, 8, P], BF16, name="tq", tag=tg, bufs=TBUFS[tg])
             for j in range(8):
                 if part == 0:
                     src = Q_SB[h][:, j, :] if j < 4 else KN_SB[h][:, j - 4, :]
@@ -126,11 +147,11 @@ def tile_flashattentionmodule_pa_kernel(tc, x, q, k_new, past_k, past_v, Wv, bv,
                 nc.tensor.transpose(tq[:, j, :], src, ident_bf[:])
             evac(e, QKT[h][:, part * 1024:(part + 1) * 1024], tq[:].rearrange("p j i -> p (j i)"))
 
-        def prep_w(h, gp, e):
+        def prep_w(h, gp, e, tg="sd"):
             if gp == 0:
-                WG[h] = hd.tile([P, 4 * HD * 4], BF16, name="wg", tag="wg", align_bytes=64)
+                WG[h] = hd.tile([P, 4 * HD * 4], BF16, name="wg", tag="wg", align_bytes=64, bufs=4)
             ww = W_SB[h][:].bitcast(F32)
-            tw = ps_t.tile([P, 4, P], F32, name="tw", tag="t")
+            tw = (ps_o if tg == "yo" else ps_t).tile([P, 4, P], F32, name="tw", tag=tg, bufs=TBUFS[tg])
             for j in range(4):
                 wb = gp * 4 + j
                 nc.tensor.transpose(tw[:, j, :], ww[:, wb * P:(wb + 1) * P], ident_f[:])
@@ -138,13 +159,13 @@ def tile_flashattentionmodule_pa_kernel(tc, x, q, k_new, past_k, past_v, Wv, bv,
             evac(e, wgw[:, 2 * gp:2 * gp + 2, :, :], tw[:].rearrange("p (g u) o -> p g o u", u=2))
 
         def quant_w(h):
-            WC[h] = hd.tile([P, 4 * HD], U32, name="wc", tag="wc", align_bytes=64)
-            WS[h] = hd.tile([P, 4 * HD], U8, name="ws", tag="ws", align_bytes=64)
+            WC[h] = hd.tile([P, 4 * HD], U32, name="wc", tag="wc", align_bytes=64, bufs=3)
+            WS[h] = hd.tile([P, 4 * HD], U8, name="ws", tag="ws", align_bytes=64, bufs=3)
             nc.vector.quantize_mx(out=WC[h][:].bitcast(FP8X4), scales=WS[h][:], in_=WG[h][:])
 
         def regroup_v(h, piece):
             if piece == 0:
-                VG[h] = hd.tile([P, 3 * HD * 4], BF16, name="vg", tag="vg", align_bytes=64)
+                VG[h] = hd.tile([P, 3 * HD * 4], BF16, name="vg", tag="vg", align_bytes=64, bufs=3)
             g, half = divmod(piece, 2)
             dst = VG[h][:, g * 512 + half * 256:g * 512 + half * 256 + 256].rearrange("p (d t) -> p d t", t=4)
             src = PV_SB[h][:, 4 * g:4 * g + 4, half * 64:half * 64 + 64].rearrange("p t d -> p d t")
@@ -153,14 +174,15 @@ def tile_flashattentionmodule_pa_kernel(tc, x, q, k_new, past_k, past_v, Wv, bv,
             else:
                 nc.vector.tensor_copy(out=dst, in_=src)
 
-        def proj(h):
-            Y_PS[h] = ps_o.tile([P, NT, HD], F32, name="y_ps", tag="t")
-            for jt in range(NT):
+        def proj(h, half):
+            if half == 0:
+                Y_PS[h] = (ps_t if h == H - 1 else ps_o).tile([P, NT, HD], F32, name="y_ps", tag="sd" if h == H - 1 else "yo", bufs=1)
+            for jt in range(2 * half, 2 * half + 2):
                 for g in range(4):
                     nc.tensor.matmul_mx(
                         out=Y_PS[h][:, jt, :],
-                        lhsT=x_codes[:, g * S + jt * P:g * S + (jt + 1) * P].bitcast(FP8X4),
-                        lhsT_scale=x_scales[:, g * S + jt * P:g * S + (jt + 1) * P],
+                        lhsT=x_codes[:, (jt * 4 + g) * P:(jt * 4 + g + 1) * P].bitcast(FP8X4),
+                        lhsT_scale=x_scales[:, (jt * 4 + g) * P:(jt * 4 + g + 1) * P],
                         rhs=WC[h][:, g * HD:(g + 1) * HD].bitcast(FP8X4),
                         rhs_scale=WS[h][:, g * HD:(g + 1) * HD],
                         start=(g == 0), stop=(g == 3))
@@ -171,8 +193,8 @@ def tile_flashattentionmodule_pa_kernel(tc, x, q, k_new, past_k, past_v, Wv, bv,
                                     in1=bvb[:, h * HD:(h + 1) * HD].unsqueeze(2).to_broadcast([P, HD, 4]), op=ALU.add)
 
         def quant_v(h):
-            VC[h] = hd.tile([P, 3 * HD], U32, name="vc", tag="vc", align_bytes=64)
-            VS[h] = hd.tile([P, 3 * HD], U8, name="vs", tag="vs", align_bytes=64)
+            VC[h] = hd.tile([P, 3 * HD], U32, name="vc", tag="vc", align_bytes=64, bufs=3)
+            VS[h] = hd.tile([P, 3 * HD], U8, name="vs", tag="vs", align_bytes=64, bufs=3)
             nc.vector.quantize_mx(out=VC[h][:, 0:256].bitcast(FP8X4), scales=VS[h][:, 0:256], in_=VG[h][:, 0:1024])
             nc.vector.quantize_mx(out=VC[h][:, 256:384].bitcast(FP8X4), scales=VS[h][:, 256:384], in_=VG[h][:, 1024:1536])
 
@@ -216,10 +238,10 @@ def tile_flashattentionmodule_pa_kernel(tc, x, q, k_new, past_k, past_v, Wv, bv,
 
         def st4(n):
             h, it = divmod(n, NT)
-            tP = ps_t.tile([P, 8, P], BF16, name="tP", tag="t")
+            tP = ps_t.tile([P, 8, P], BF16, name="tP", tag="tP", bufs=2)
             for r in range(8):
                 nc.tensor.transpose(tP[:, r, :], E_SB[n][:, r * P:(r + 1) * P], ident_bf[:])
-            tN = ps_t.tile([P, 8, P], BF16, name="tN", tag="t")
+            tN = ps_t.tile([P, 8, P], BF16, name="tN", tag="tN", bufs=1)
             for t in range(it + 1):
                 nc.tensor.transpose(tN[:, t, :], E_SB[n][:, 1024 + t * P:1024 + (t + 1) * P], ident_bf[:])
             T_PS[n] = [tP, tN]
@@ -248,8 +270,8 @@ def tile_flashattentionmodule_pa_kernel(tc, x, q, k_new, past_k, past_v, Wv, bv,
         def st6n(n):
             h, it = divmod(n, NT)
             if it == 0:
-                EC[h] = hd.tile([P, NT * 384], U32, name="ec", tag="ec", align_bytes=64)
-                ES[h] = hd.tile([P, NT * 384], U8, name="es", tag="es", align_bytes=64)
+                EC[h] = hd.tile([P, NT * 384], U32, name="ec", tag="ec", align_bytes=64, bufs=3)
+                ES[h] = hd.tile([P, NT * 384], U8, name="es", tag="es", align_bytes=64, bufs=3)
             o = it * 384
             nc.vector.quantize_mx(out=EC[h][:, o + 256:o + 384].bitcast(FP8X4), scales=ES[h][:, o + 256:o + 384],
                                   in_=ENG[h % 2][:, it * 512:(it + 1) * 512])
@@ -265,9 +287,10 @@ def tile_flashattentionmodule_pa_kernel(tc, x, q, k_new, past_k, past_v, Wv, bv,
 
         O_PS = {}
 
-        def pv(h):
-            O_PS[h] = ps_o.tile([P, NT, HD], F32, name="o_ps", tag="t")
-            for it in range(NT):
+        def pv(h, half):
+            if half == 0:
+                O_PS[h] = (ps_t if h == H - 1 else ps_o).tile([P, NT, HD], F32, name="o_ps", tag="sd" if h == H - 1 else "yo", bufs=1)
+            for it in range(2 * half, 2 * half + 2):
                 for g in range(3):
                     o = it * 384 + g * P
                     nc.tensor.matmul_mx(out=O_PS[h][:, it, :],
@@ -285,67 +308,72 @@ def tile_flashattentionmodule_pa_kernel(tc, x, q, k_new, past_k, past_v, Wv, bv,
         def ok(n):
             return 0 <= n < NTILES
 
-        prep_qk(0, 0, "v")
-        prep_qk(0, 1, "s")
+        def heads_at(k, task):
+            return [hh for hh in range(H) if F.get((task, hh), NT * hh + A[task]) == k]
+
+        prep_qk(0, 0, "v", "tP")
+        prep_qk(0, 1, "s", "tP")
+        x_tr(0, 0, "sd")
+        x_tr(0, 1, "yo")
         st1(0)
-        for k in range(NTILES + 6):
+        x_ev(0, 0, "s")
+        x_ev(0, 1, "s")
+        for k in range(NTILES + 12):
             h, it = divmod(k, NT)
-            if k == 3:
-                x_quant(0)
-                x_quant(1)
-            if it == 3 and h < H:
-                quant_w(h)
-            if it == 1 and 1 <= h <= H:
-                quant_v(h - 1)
+            if it == 0:
+                if h + 2 < H:
+                    load_qk(h + 2)
+                if h + 3 < H:
+                    load_wv(h + 3)
+                if h + 2 < H:
+                    load_pv(h + 2)
+            if 0 <= k - XQ < NT:
+                x_quant(k - XQ)
+            for hh in heads_at(k, "quant_w"):
+                quant_w(hh)
+            for hh in heads_at(k, "quant_v"):
+                quant_v(hh)
             if ok(k - 3):
                 st6n(k - 3)
             if ok(k - LAG):
                 st6p(k - LAG)
-            if R2 and ok(k - 3):
-                st5g(k - 3)
-            if h < H:
-                for piece in range(4):
-                    if VP[piece] == it:
-                        regroup_v(h, piece)
+            for piece in range(4):
+                for hh in heads_at(k, "v%d" % piece):
+                    regroup_v(hh, piece)
             if ok(k):
                 st2(k)
             if ok(k - 2):
-                st4(k - 2)
-                if (k - 2) % NT < SPLIT:
-                    st5b(k - 2, "v")
+                st5b(k - 2, "v")
+                if (k - 2) % NV == NV // 2:
+                    st5a(k - 2, "v")
+            if 1 <= k - 1 < NT:
+                x_ev(k - 1, 1, "v")
+            for hh in heads_at(k, "finish"):
+                finish(hh)
+            for hh in heads_at(k, "y_evac"):
+                y_evac(hh)
             if ok(k):
                 st2b(k)
+            if ok(k + 1):
+                st1(k + 1)
+            if ok(k):
+                st3(k)
             if ok(k - 1):
-                st3(k - 1)
-            if ok(k - 2):
-                st5a(k - 2, "s")
-                if (k - 2) % NT >= SPLIT:
-                    st5b(k - 2, "s")
-            if k < 3 and ok(k + 1):
-                st1(k + 1)
-            if k < 3:
-                for i in range(3):
-                    j = k * 3 + i
-                    if j < 8:
-                        x_part(j // 2, j % 2, "s" if i % 2 else "v")
-            if it == 0:
-                if h + 2 < H:
-                    load_qk(h + 2)
-                if h + 1 < H:
-                    load_wv(h + 1)
-                if 1 <= h <= H:
-                    proj(h - 1)
-                if 2 <= h <= H + 1:
-                    pv(h - 2)
-                if 1 <= h <= H:
-                    y_evac(h - 1)
-                if 2 <= h <= H + 1:
-                    finish(h - 2)
-            if it == 1 and h < H:
-                prep_w(h, 0, WE[0])
-                prep_w(h, 1, WE[1])
-            if it == 2 and h + 1 < H:
-                prep_qk(h + 1, 0, QE[0])
-                prep_qk(h + 1, 1, QE[1])
-            if k >= 3 and ok(k + 1):
-                st1(k + 1)
+                st4(k - 1)
+                if (k - 1) % NV != NV // 2:
+                    st5a(k - 1, "s")
+            if 1 <= k < NT:
+                x_tr(k, 0, "tP")
+                x_ev(k, 0, "s")
+                x_tr(k, 1, "yo")
+            for part in range(2):
+                for hh in heads_at(k, "w%d" % part):
+                    prep_w(hh, part, WE[part], ("tN", "tP")[part] if hh == 0 else "sd")
+                for hh in heads_at(k, "qk%d" % part):
+                    if hh > 0:
+                        prep_qk(hh, part, QE[part])
+            for half in range(2):
+                for hh in heads_at(k, "pv%d" % half):
+                    pv(hh, half)
+                for hh in heads_at(k, "proj%d" % half):
+                    proj(hh, half)

@@ -25,11 +25,14 @@ TBUFS = {"sd": 1, "tP": 2, "tN": 1, "yo": 1}
 R2 = False
 LAG = 4
 NV = 1000
+WV = 2
+TL = 1
+LASTPV = 65
 WE = "ss"
 QE = "ss"
 XQ = 2
 A = {"qk0": -4, "qk1": -3, "w0": -2, "w1": -1, "quant_w": 2, "proj0": 4, "proj1": 5, "y_evac": 6, "quant_v": 7, "pv0": 10, "pv1": 11, "finish": 12, "v0": 0, "v1": 1, "v2": 2, "v3": 3}
-F = {("w0", 0): 0, ("w1", 0): 0, ("quant_w", 0): 3, ("proj0", 15): 62, ("proj1", 15): 63, ("y_evac", 15): 64, ("quant_v", 15): 65, ("pv0", 14): 64, ("pv1", 14): 65, ("finish", 14): 66, ("pv0", 15): 66, ("pv1", 15): 67, ("finish", 15): 68}
+F = {("w0", 0): 0, ("w1", 0): 0, ("quant_w", 0): 3, ("proj0", 15): 62, ("proj1", 15): 63, ("y_evac", 15): 64, ("quant_v", 15): 65, ("pv0", 14): 64, ("pv1", 14): 65, ("finish", 14): 66}
 V_REGROUP = "gpsimd"
 
 
@@ -87,6 +90,14 @@ def tile_flashattentionmodule_pa_kernel(tc, x, q, k_new, past_k, past_v, Wv, bv,
         bvb = const.tile([P, D], BF16, name="bvb")
         nc.sync.dma_start(out=bvb[:], in_=bv.partition_broadcast(P))
 
+        warm = const.tile([P, 2], F32, name="warm")
+        nc.vector.memset(warm[:, 0:1], 0.0)
+        nc.scalar.activation(out=warm[:, 1:2], in_=warm[:, 0:1], func=ACTF.Exp)
+        ENG = []
+        for i in range(2):
+            eng = const.tile([P, NT * P * 4], BF16, name="eng%d" % i, align_bytes=64)
+            nc.vector.memset(eng[:], 0.0)
+            ENG.append(eng)
         ident_bf = const.tile([P, P], BF16, name="ident_bf")
         make_identity(nc, ident_bf[:])
         ident_f = const.tile([P, P], F32, name="ident_f")
@@ -97,11 +108,6 @@ def tile_flashattentionmodule_pa_kernel(tc, x, q, k_new, past_k, past_v, Wv, bv,
                                 pattern=[[-1, P]], channel_multiplier=1)
         mask_bf = const.tile([P, P], BF16, name="mask_bf")
         nc.vector.tensor_copy(out=mask_bf[:], in_=mask_f[:])
-        ENG = []
-        for i in range(2):
-            eng = const.tile([P, NT * P * 4], BF16, name="eng%d" % i, align_bytes=64)
-            nc.gpsimd.memset(eng[:], 0.0)
-            ENG.append(eng)
         mn3 = const.tile([P, NTILES * 4], F32, name="mn3")
         nm = const.tile([P, NTILES], F32, name="nm")
         sums = const.tile([P, NTILES], F32, name="sums")
@@ -147,7 +153,13 @@ def tile_flashattentionmodule_pa_kernel(tc, x, q, k_new, past_k, past_v, Wv, bv,
                 nc.tensor.transpose(tq[:, j, :], src, ident_bf[:])
             evac(e, QKT[h][:, part * 1024:(part + 1) * 1024], tq[:].rearrange("p j i -> p (j i)"))
 
+        TW = {}
+
         def prep_w(h, gp, e, tg="sd"):
+            w_tr(h, gp, tg)
+            w_ev(h, gp, e)
+
+        def w_tr(h, gp, tg):
             if gp == 0:
                 WG[h] = hd.tile([P, 4 * HD * 4], BF16, name="wg", tag="wg", align_bytes=64, bufs=4)
             ww = W_SB[h][:].bitcast(F32)
@@ -155,6 +167,10 @@ def tile_flashattentionmodule_pa_kernel(tc, x, q, k_new, past_k, past_v, Wv, bv,
             for j in range(4):
                 wb = gp * 4 + j
                 nc.tensor.transpose(tw[:, j, :], ww[:, wb * P:(wb + 1) * P], ident_f[:])
+            TW[(h, gp)] = tw
+
+        def w_ev(h, gp, e):
+            tw = TW[(h, gp)]
             wgw = WG[h][:].bitcast(F32).rearrange("p (g o u) -> p g o u", g=4, u=2)
             evac(e, wgw[:, 2 * gp:2 * gp + 2, :, :], tw[:].rearrange("p (g u) o -> p g o u", u=2))
 
@@ -198,11 +214,15 @@ def tile_flashattentionmodule_pa_kernel(tc, x, q, k_new, past_k, past_v, Wv, bv,
             nc.vector.quantize_mx(out=VC[h][:, 0:256].bitcast(FP8X4), scales=VS[h][:, 0:256], in_=VG[h][:, 0:1024])
             nc.vector.quantize_mx(out=VC[h][:, 256:384].bitcast(FP8X4), scales=VS[h][:, 256:384], in_=VG[h][:, 1024:1536])
 
+        def where(n):
+            h, j = divmod(n, NT)
+            return h, (NT - 1 - j if h == H - 1 else j)
+
         def widths(it):
             return [512, 512, P * (it + 1)]
 
         def st1(n):
-            h, it = divmod(n, NT)
+            h, it = where(n)
             kt = QKT[h]
             lhsT = kt[:, it * P:(it + 1) * P]
             sA = ps_s.tile([P, 512], F32, name="sA", tag="s")
@@ -218,26 +238,30 @@ def tile_flashattentionmodule_pa_kernel(tc, x, q, k_new, past_k, past_v, Wv, bv,
             S_PS[n] = [sA, sB, sC]
 
         def st2(n):
-            h, it = divmod(n, NT)
+            h, it = where(n)
+            c = h * NT + it
             S_SB[n] = tl.tile([P, 1536], F32, name="s_sb", tag="s_sb")
             off = 0
             for j, w in enumerate(widths(it)):
                 nc.vector.tensor_scalar(out=S_SB[n][:, off:off + w], in0=S_PS[n][j][:, 0:w], scalar1=-SCALE, scalar2=None,
-                                        op0=ALU.mult, op1=ALU.min, accum_out=mn3[:, 4 * n + j:4 * n + j + 1])
+                                        op0=ALU.mult, op1=ALU.min, accum_out=mn3[:, 4 * c + j:4 * c + j + 1])
                 off += w
 
         def st2b(n):
-            nc.vector.tensor_reduce(out=nm[:, n:n + 1], in_=mn3[:, 4 * n:4 * n + 3], axis=AX.X, op=ALU.min)
+            h, it = where(n)
+            c = h * NT + it
+            nc.vector.tensor_reduce(out=nm[:, c:c + 1], in_=mn3[:, 4 * c:4 * c + 3], axis=AX.X, op=ALU.min)
 
         def st3(n):
-            h, it = divmod(n, NT)
+            h, it = where(n)
             w = sum(widths(it))
             E_SB[n] = tl.tile([P, 1536], BF16, name="e_sb", tag="e_sb")
-            nc.scalar.activation(out=E_SB[n][:, 0:w], in_=S_SB[n][:, 0:w], func=ACTF.Exp, bias=nm[:, n:n + 1], scale=-1.0,
-                                 accum_out=sums[:, n:n + 1])
+            c = h * NT + it
+            nc.scalar.activation(out=E_SB[n][:, 0:w], in_=S_SB[n][:, 0:w], func=ACTF.Exp, bias=nm[:, c:c + 1], scale=-1.0,
+                                 accum_out=sums[:, c:c + 1])
 
         def st4(n):
-            h, it = divmod(n, NT)
+            h, it = where(n)
             tP = ps_t.tile([P, 8, P], BF16, name="tP", tag="tP", bufs=2)
             for r in range(8):
                 nc.tensor.transpose(tP[:, r, :], E_SB[n][:, r * P:(r + 1) * P], ident_bf[:])
@@ -263,13 +287,13 @@ def tile_flashattentionmodule_pa_kernel(tc, x, q, k_new, past_k, past_v, Wv, bv,
                                     scalar1=1.0, scalar2=0.0, op0=ALU.mult, op1=ALU.add)
 
         def st5b(n, e):
-            h, it = divmod(n, NT)
+            h, it = where(n)
             dst = ENG[h % 2][:].rearrange("p (a i t) -> p a i t", a=NT, t=4)
             evac(e, dst[:, it, :, 0:it + 1], T_PS[n][1][:, 0:it + 1, :].rearrange("p t i -> p i t"))
 
         def st6n(n):
-            h, it = divmod(n, NT)
-            if it == 0:
+            h, it = where(n)
+            if n % NT == 0:
                 EC[h] = hd.tile([P, NT * 384], U32, name="ec", tag="ec", align_bytes=64, bufs=3)
                 ES[h] = hd.tile([P, NT * 384], U8, name="es", tag="es", align_bytes=64, bufs=3)
             o = it * 384
@@ -277,7 +301,7 @@ def tile_flashattentionmodule_pa_kernel(tc, x, q, k_new, past_k, past_v, Wv, bv,
                                   in_=ENG[h % 2][:, it * 512:(it + 1) * 512])
 
         def st6p(n):
-            h, it = divmod(n, NT)
+            h, it = where(n)
             o = it * 384
             nc.vector.quantize_mx(out=EC[h][:, o:o + 256].bitcast(FP8X4), scales=ES[h][:, o:o + 256], in_=ETG[n][:])
 
@@ -287,10 +311,12 @@ def tile_flashattentionmodule_pa_kernel(tc, x, q, k_new, past_k, past_v, Wv, bv,
 
         O_PS = {}
 
-        def pv(h, half):
-            if half == 0:
-                O_PS[h] = (ps_t if h == H - 1 else ps_o).tile([P, NT, HD], F32, name="o_ps", tag="sd" if h == H - 1 else "yo", bufs=1)
-            for it in range(2 * half, 2 * half + 2):
+        def pv(h, its, first):
+            if h == H - 1:
+                O_PS[h] = ps_s.tile([P, NT, HD], F32, name="o_ps", tag="s")
+            elif first:
+                O_PS[h] = ps_o.tile([P, NT, HD], F32, name="o_ps", tag="yo", bufs=1)
+            for it in its:
                 for g in range(3):
                     o = it * 384 + g * P
                     nc.tensor.matmul_mx(out=O_PS[h][:, it, :],
@@ -298,12 +324,13 @@ def tile_flashattentionmodule_pa_kernel(tc, x, q, k_new, past_k, past_v, Wv, bv,
                                         rhs=VC[h][:, g * HD:(g + 1) * HD].bitcast(FP8X4), rhs_scale=VS[h][:, g * HD:(g + 1) * HD],
                                         start=(g == 0), stop=(g == 2))
 
-        def finish(h):
-            nc.vector.reciprocal(out=rinv[:, h * NT:(h + 1) * NT], in_=sums[:, h * NT:(h + 1) * NT])
-            o_sb = hd.tile([P, NT, HD], F32, name="o_sb", tag="o_sb")
-            nc.vector.tensor_tensor(out=o_sb[:], in0=O_PS[h][:],
-                                    in1=rinv[:, h * NT:(h + 1) * NT].unsqueeze(2).to_broadcast([P, NT, HD]), op=ALU.mult)
-            nc.sync.dma_start(out=out[0].rearrange("(a p) c -> p a c", p=P)[:, :, h * HD:(h + 1) * HD], in_=o_sb[:])
+        def finish(h, lo, hi):
+            c = h * NT
+            nc.vector.reciprocal(out=rinv[:, c + lo:c + hi], in_=sums[:, c + lo:c + hi])
+            o_sb = hd.tile([P, NT, HD], F32, name="o_sb", tag="o_sb", bufs=4)
+            nc.vector.tensor_tensor(out=o_sb[:, lo:hi, :], in0=O_PS[h][:, lo:hi, :],
+                                    in1=rinv[:, c + lo:c + hi].unsqueeze(2).to_broadcast([P, hi - lo, HD]), op=ALU.mult)
+            nc.sync.dma_start(out=out[0].rearrange("(a p) c -> p a c", p=P)[:, lo:hi, h * HD:(h + 1) * HD], in_=o_sb[:, lo:hi, :])
 
         def ok(n):
             return 0 <= n < NTILES
@@ -335,8 +362,10 @@ def tile_flashattentionmodule_pa_kernel(tc, x, q, k_new, past_k, past_v, Wv, bv,
                 quant_v(hh)
             if ok(k - 3):
                 st6n(k - 3)
-            if ok(k - LAG):
+            if ok(k - LAG) and k - LAG < NTILES - TL:
                 st6p(k - LAG)
+            if ok(k - LAG + 1) and k - LAG + 1 >= NTILES - TL:
+                st6p(k - LAG + 1)
             for piece in range(4):
                 for hh in heads_at(k, "v%d" % piece):
                     regroup_v(hh, piece)
@@ -346,14 +375,24 @@ def tile_flashattentionmodule_pa_kernel(tc, x, q, k_new, past_k, past_v, Wv, bv,
                 st5b(k - 2, "v")
                 if (k - 2) % NV == NV // 2:
                     st5a(k - 2, "v")
-            if 1 <= k - 1 < NT:
-                x_ev(k - 1, 1, "v")
-            for hh in heads_at(k, "finish"):
-                finish(hh)
-            for hh in heads_at(k, "y_evac"):
-                y_evac(hh)
             if ok(k):
                 st2b(k)
+            if 1 <= k - 1 < NT:
+                x_ev(k - 1, 1, "v")
+            for hh in heads_at(k - 1, "w1"):
+                if hh > 0 and hh % WV == 0:
+                    w_ev(hh, 1, "v")
+            for hh in heads_at(k, "finish"):
+                if hh < H - 1:
+                    finish(hh, 0, NT)
+            if k == LASTPV + 1:
+                finish(H - 1, 2, 4)
+            if k == LASTPV + 2:
+                finish(H - 1, 1, 2)
+            if k == LASTPV + 3:
+                finish(H - 1, 0, 1)
+            for hh in heads_at(k, "y_evac"):
+                y_evac(hh)
             if ok(k + 1):
                 st1(k + 1)
             if ok(k):
@@ -362,18 +401,28 @@ def tile_flashattentionmodule_pa_kernel(tc, x, q, k_new, past_k, past_v, Wv, bv,
                 st4(k - 1)
                 if (k - 1) % NV != NV // 2:
                     st5a(k - 1, "s")
+            if k == LASTPV:
+                pv(H - 1, [3, 2], True)
+            if k == LASTPV + 1:
+                pv(H - 1, [1], False)
+            if k == LASTPV + 2:
+                pv(H - 1, [0], False)
+            for half in range(2):
+                for hh in heads_at(k, "pv%d" % half):
+                    if hh < H - 1:
+                        pv(hh, [2 * half, 2 * half + 1], half == 0)
+                for hh in heads_at(k, "proj%d" % half):
+                    proj(hh, half)
             if 1 <= k < NT:
                 x_tr(k, 0, "tP")
                 x_ev(k, 0, "s")
                 x_tr(k, 1, "yo")
             for part in range(2):
                 for hh in heads_at(k, "w%d" % part):
-                    prep_w(hh, part, WE[part], ("tN", "tP")[part] if hh == 0 else "sd")
+                    if hh > 0 and part == 1 and hh % WV == 0:
+                        w_tr(hh, part, "sd")
+                    else:
+                        prep_w(hh, part, WE[part], ("tN", "tP")[part] if hh == 0 else "sd")
                 for hh in heads_at(k, "qk%d" % part):
                     if hh > 0:
                         prep_qk(hh, part, QE[part])
-            for half in range(2):
-                for hh in heads_at(k, "pv%d" % half):
-                    pv(hh, half)
-                for hh in heads_at(k, "proj%d" % half):
-                    proj(hh, half)

@@ -25,7 +25,7 @@ TBUFS = {"sd": 1, "tP": 2, "tN": 1, "yo": 1}
 R2 = False
 LAG = 4
 NV = 1000
-WV = 2
+WV = 1000
 TL = 1
 LASTPV = 65
 WE = "ss"

@@ -20,20 +20,14 @@ SCALE = 1.0 / math.sqrt(HD)
 MASKED = -1.0e30
 FLOPS = 2 * S * D * D + 2 * 2 * H * S * (PAST + S) * HD
 
-MANUAL = True
 TBUFS = {"sd": 1, "tP": 2, "tN": 1, "yo": 1}
-R2 = False
 LAG = 4
-NV = 1000
-WV = 1000
-TL = 1
 LASTPV = 65
 WE = "ss"
 QE = "ss"
 XQ = 2
 A = {"qk0": -4, "qk1": -3, "w0": -2, "w1": -1, "quant_w": 2, "proj0": 4, "proj1": 5, "y_evac": 6, "quant_v": 7, "pv0": 10, "pv1": 11, "finish": 12, "v0": 0, "v1": 1, "v2": 2, "v3": 3}
 F = {("w0", 0): 0, ("w1", 0): 0, ("quant_w", 0): 3, ("proj0", 15): 62, ("proj1", 15): 63, ("y_evac", 15): 64, ("quant_v", 15): 65, ("pv0", 14): 64, ("pv1", 14): 65, ("finish", 14): 66}
-V_REGROUP = "gpsimd"
 
 
 def tile_flashattentionmodule_pa_kernel(tc, x, q, k_new, past_k, past_v, Wv, bv, out):
@@ -46,20 +40,18 @@ def tile_flashattentionmodule_pa_kernel(tc, x, q, k_new, past_k, past_v, Wv, bv,
         ps_s = ctx.enter_context(tc.psum_pool(name="ps_s", bufs=3))
         ps_t = ctx.enter_context(tc.psum_pool(name="ps_t", bufs=1))
         ps_o = ctx.enter_context(tc.psum_pool(name="ps_o", bufs=1))
-        one = ctx.enter_context(tc.tile_pool(name="one", bufs=1))
-        if MANUAL:
-            ctx.enter_context(tc.manual_schedule())
+        ctx.enter_context(tc.manual_schedule())
 
         NTILES = H * NT
         Q_SB, KN_SB, PK_SB, PV_SB, W_SB = {}, {}, {}, {}, {}
         QKT, WG, WC, WS, VG, VC, VS, EC, ES, Y_PS = {}, {}, {}, {}, {}, {}, {}, {}, {}, {}
-        S_PS, S_SB, E_SB, T_PS, ETG = {}, {}, {}, {}, {}
+        S_PS, S_SB, TP_PS, TN_PS, ETG, ETN = {}, {}, {}, {}, {}, {}
 
         def load_qk(h):
             Q_SB[h] = ld.tile([P, NT, HD], BF16, name="q_sb", tag="q_sb")
             nc.sync.dma_start(out=Q_SB[h][:], in_=q[0, h].rearrange("(a p) d -> p a d", p=P))
             KN_SB[h] = ld.tile([P, NT, HD], BF16, name="kn_sb", tag="kn_sb")
-            nc.sync.dma_start(out=KN_SB[h][:], in_=k_new[0, h].rearrange("(a p) d -> p a d", p=P))
+            nc.sync.dma_start(out=KN_SB[h][:], in_=k_new[0, h].rearrange("(p r) d -> p r d", r=NT))
             PK_SB[h] = ld.tile([P, 8, HD], BF16, name="pk_sb", tag="pk_sb")
             nc.sync.dma_start(out=PK_SB[h][:], in_=past_k[0, h].rearrange("(p r) d -> p r d", r=8))
 
@@ -75,7 +67,7 @@ def tile_flashattentionmodule_pa_kernel(tc, x, q, k_new, past_k, past_v, Wv, bv,
         x_sb = const.tile([P, NT, D], BF16, name="x_sb")
 
         def load_x(a):
-            nc.sync.dma_start(out=x_sb[:, a, :], in_=x[0, a * P:(a + 1) * P, :])
+            nc.sync.dma_start(out=x_sb[:, a, :], in_=x[0].rearrange("(p a) k -> a p k", a=NT)[a])
 
         load_x(0)
         load_qk(1)
@@ -93,11 +85,12 @@ def tile_flashattentionmodule_pa_kernel(tc, x, q, k_new, past_k, past_v, Wv, bv,
         warm = const.tile([P, 2], F32, name="warm")
         nc.vector.memset(warm[:, 0:1], 0.0)
         nc.scalar.activation(out=warm[:, 1:2], in_=warm[:, 0:1], func=ACTF.Exp)
-        ENG = []
-        for i in range(2):
-            eng = const.tile([P, NT * P * 4], BF16, name="eng%d" % i, align_bytes=64)
-            nc.vector.memset(eng[:], 0.0)
-            ENG.append(eng)
+        E_SB = []
+        for i in range(NT + 1):
+            e_sb = const.tile([P, 1536], BF16, name="e_sb%d" % i, align_bytes=64)
+            if i < NT - 1:
+                nc.vector.memset(e_sb[:, 1024:1536], 0.0)
+            E_SB.append(e_sb)
         ident_bf = const.tile([P, P], BF16, name="ident_bf")
         make_identity(nc, ident_bf[:])
         ident_f = const.tile([P, P], F32, name="ident_f")
@@ -107,10 +100,12 @@ def tile_flashattentionmodule_pa_kernel(tc, x, q, k_new, past_k, past_v, Wv, bv,
         nc.gpsimd.affine_select(out=mask_f[:], in_=mask_f[:], compare_op=ALU.is_ge, fill=MASKED, base=0,
                                 pattern=[[-1, P]], channel_multiplier=1)
         mask_bf = const.tile([P, P], BF16, name="mask_bf")
-        nc.vector.tensor_copy(out=mask_bf[:], in_=mask_f[:])
+        nc.vector.tensor_copy(out=mask_bf[:].rearrange("i (r w) -> i r w", r=4), in_=mask_f[:].rearrange("i (w r) -> i r w", r=4))
         mn3 = const.tile([P, NTILES * 4], F32, name="mn3")
         nm = const.tile([P, NTILES], F32, name="nm")
         sums = const.tile([P, NTILES], F32, name="sums")
+        sums_n = const.tile([P, NTILES], F32, name="sums_n")
+        sums_t = const.tile([P, NTILES], F32, name="sums_t")
         rinv = const.tile([P, NTILES], F32, name="rinv")
         xg = const.tile([P, 4 * S * 4], BF16, name="xg", align_bytes=64)
         x_codes = const.tile([P, 4 * S], U32, name="x_codes", align_bytes=64)
@@ -185,10 +180,7 @@ def tile_flashattentionmodule_pa_kernel(tc, x, q, k_new, past_k, past_v, Wv, bv,
             g, half = divmod(piece, 2)
             dst = VG[h][:, g * 512 + half * 256:g * 512 + half * 256 + 256].rearrange("p (d t) -> p d t", t=4)
             src = PV_SB[h][:, 4 * g:4 * g + 4, half * 64:half * 64 + 64].rearrange("p t d -> p d t")
-            if V_REGROUP == "gpsimd":
-                nc.gpsimd.tensor_scalar(out=dst, in0=src, scalar1=1.0, scalar2=0.0, op0=ALU.mult, op1=ALU.add)
-            else:
-                nc.vector.tensor_copy(out=dst, in_=src)
+            nc.gpsimd.tensor_scalar(out=dst, in0=src, scalar1=1.0, scalar2=0.0, op0=ALU.mult, op1=ALU.add)
 
         def proj(h, half):
             if half == 0:
@@ -218,6 +210,9 @@ def tile_flashattentionmodule_pa_kernel(tc, x, q, k_new, past_k, past_v, Wv, bv,
             h, j = divmod(n, NT)
             return h, (NT - 1 - j if h == H - 1 else j)
 
+        def e_tile(n):
+            return NT if n == NTILES - NT else where(n)[1]
+
         def widths(it):
             return [512, 512, P * (it + 1)]
 
@@ -230,11 +225,10 @@ def tile_flashattentionmodule_pa_kernel(tc, x, q, k_new, past_k, past_v, Wv, bv,
             sB = ps_s.tile([P, 512], F32, name="sB", tag="s")
             nc.tensor.matmul(out=sB[:], lhsT=lhsT, rhs=kt[:, 1536:2048], start=True, stop=True)
             sC = ps_s.tile([P, 512], F32, name="sC", tag="s")
-            if it > 0:
-                nc.tensor.matmul(out=sC[:, 0:it * P], lhsT=lhsT, rhs=kt[:, 512:512 + it * P], start=True, stop=True)
-            nc.tensor.matmul(out=sC[:, it * P:(it + 1) * P], lhsT=lhsT, rhs=kt[:, 512 + it * P:512 + (it + 1) * P],
-                             start=True, stop=False)
-            nc.tensor.matmul(out=sC[:, it * P:(it + 1) * P], lhsT=ident_bf[:], rhs=mask_bf[:], start=False, stop=True)
+            w = 32 * (it + 1)
+            sv = sC[:, 0:4 * w].rearrange("q (r p) -> q r p", r=4)
+            nc.tensor.matmul(out=sv, lhsT=lhsT, rhs=kt[:, 512:1024].rearrange("d (r p) -> d r p", r=4)[:, :, 0:w], start=True, stop=False)
+            nc.tensor.matmul(out=sv[:, :, w - 32:w], lhsT=ident_bf[:], rhs=mask_bf[:].rearrange("i (r p) -> i r p", r=4), start=False, stop=True)
             S_PS[n] = [sA, sB, sC]
 
         def st2(n):
@@ -254,60 +248,47 @@ def tile_flashattentionmodule_pa_kernel(tc, x, q, k_new, past_k, past_v, Wv, bv,
 
         def st3(n):
             h, it = where(n)
-            w = sum(widths(it))
-            E_SB[n] = tl.tile([P, 1536], BF16, name="e_sb", tag="e_sb")
             c = h * NT + it
-            nc.scalar.activation(out=E_SB[n][:, 0:w], in_=S_SB[n][:, 0:w], func=ACTF.Exp, bias=nm[:, c:c + 1], scale=-1.0,
-                                 accum_out=sums[:, c:c + 1])
+            w = 32 * (it + 1)
+            nc.scalar.activation(out=E_SB[e_tile(n)][:, 0:1024].rearrange("q (c p e) -> q c p e", c=4, e=2),
+                                 in_=S_SB[n][:, 0:1024].rearrange("q (c e p) -> q c p e", c=4, e=2),
+                                 func=ACTF.Exp, bias=nm[:, c:c + 1], scale=-1.0, accum_out=sums[:, c:c + 1])
+            nc.scalar.activation(out=E_SB[e_tile(n)][:, 1024:1536].rearrange("q (u p e) -> q u p e", u=2, e=2)[:, :, 0:w, :],
+                                 in_=S_SB[n][:, 1024:1024 + 4 * w].rearrange("q (u e p) -> q u p e", u=2, e=2),
+                                 func=ACTF.Exp, bias=nm[:, c:c + 1], scale=-1.0, accum_out=sums_n[:, c:c + 1])
 
         def st4(n):
-            h, it = where(n)
-            tP = ps_t.tile([P, 8, P], BF16, name="tP", tag="tP", bufs=2)
-            for r in range(8):
-                nc.tensor.transpose(tP[:, r, :], E_SB[n][:, r * P:(r + 1) * P], ident_bf[:])
-            tN = ps_t.tile([P, 8, P], BF16, name="tN", tag="tN", bufs=1)
-            for t in range(it + 1):
-                nc.tensor.transpose(tN[:, t, :], E_SB[n][:, 1024 + t * P:1024 + (t + 1) * P], ident_bf[:])
-            T_PS[n] = [tP, tN]
-
-        ETC = {}
+            words = E_SB[e_tile(n)][:].bitcast(F32)
+            TP_PS[n] = ps_t.tile([P, 4, P], F32, name="tP", tag="tP", bufs=2)
+            for c in range(4):
+                nc.tensor.transpose(TP_PS[n][:, c, :], words[:, c * P:(c + 1) * P], ident_f[:])
+            if n % 2 == 0:
+                TN_PS[n // 2] = ps_t.tile([P, 2, 2, P], F32, name="tN", tag="tN", bufs=1)
+            for u in range(2):
+                nc.tensor.transpose(TN_PS[n // 2][:, n % 2, u, :], words[:, 512 + u * P:512 + (u + 1) * P], ident_f[:])
 
         def st5a(n, e):
-            if R2:
-                ETC[n] = tl.tile([P, 1024], BF16, name="etc", tag="etc")
-                evac(e, ETC[n][:], T_PS[n][0][:].rearrange("p r i -> p (r i)"))
-            else:
-                ETG[n] = tl.tile([P, 1024], BF16, name="etg", tag="etg", align_bytes=64)
-                evac(e, ETG[n][:].rearrange("p (g i t) -> p g i t", g=2, t=4), T_PS[n][0][:].rearrange("p (g t) i -> p g i t", t=4))
+            ETG[n] = tl.tile([P, 1024], BF16, name="etg", tag="etg", align_bytes=64)
+            evac(e, ETG[n][:].bitcast(F32).rearrange("p (g i u) -> p g i u", g=2, u=2),
+                 TP_PS[n][:].rearrange("p (g u) i -> p g i u", u=2))
 
-        def st5g(n):
-            ETG[n] = one.tile([P, 1024], BF16, name="etg", tag="etg", align_bytes=64)
-            nc.gpsimd.tensor_scalar(out=ETG[n][:].rearrange("p (g i t) -> p g i t", g=2, t=4),
-                                    in0=ETC[n][:].rearrange("p (g t i) -> p g i t", g=2, t=4),
-                                    scalar1=1.0, scalar2=0.0, op0=ALU.mult, op1=ALU.add)
+        def st5b(m, e):
+            ETN[m] = tl.tile([P, 1024], BF16, name="etn", tag="etn", align_bytes=64)
+            evac(e, ETN[m][:].bitcast(F32).rearrange("p (j i u) -> p j i u", j=2, u=2),
+                 TN_PS[m][:].rearrange("p j u i -> p j i u"))
 
-        def st5b(n, e):
-            h, it = where(n)
-            dst = ENG[h % 2][:].rearrange("p (a i t) -> p a i t", a=NT, t=4)
-            evac(e, dst[:, it, :, 0:it + 1], T_PS[n][1][:, 0:it + 1, :].rearrange("p t i -> p i t"))
-
-        def st6n(n):
-            h, it = where(n)
-            if n % NT == 0:
-                EC[h] = hd.tile([P, NT * 384], U32, name="ec", tag="ec", align_bytes=64, bufs=3)
-                ES[h] = hd.tile([P, NT * 384], U8, name="es", tag="es", align_bytes=64, bufs=3)
-            o = it * 384
-            nc.vector.quantize_mx(out=EC[h][:, o + 256:o + 384].bitcast(FP8X4), scales=ES[h][:, o + 256:o + 384],
-                                  in_=ENG[h % 2][:, it * 512:(it + 1) * 512])
+        def st6n(m):
+            h, j = divmod(2 * m, NT)
+            o = 1024 + j * P
+            nc.vector.quantize_mx(out=EC[h][:, o:o + 256].bitcast(FP8X4), scales=ES[h][:, o:o + 256], in_=ETN[m][:])
 
         def st6p(n):
-            h, it = where(n)
-            o = it * 384
+            h, j = divmod(n, NT)
+            if j == 0:
+                EC[h] = hd.tile([P, NT * 384], U32, name="ec", tag="ec", align_bytes=64, bufs=3)
+                ES[h] = hd.tile([P, NT * 384], U8, name="es", tag="es", align_bytes=64, bufs=3)
+            o = j * 256
             nc.vector.quantize_mx(out=EC[h][:, o:o + 256].bitcast(FP8X4), scales=ES[h][:, o:o + 256], in_=ETG[n][:])
-
-        def unused(n, h, it, o):
-            nc.vector.quantize_mx(out=EC[h][:, o + 256:o + 384].bitcast(FP8X4), scales=ES[h][:, o + 256:o + 384],
-                                  in_=ENG[h % 2][:, it * 512:(it + 1) * 512])
 
         O_PS = {}
 
@@ -317,8 +298,9 @@ def tile_flashattentionmodule_pa_kernel(tc, x, q, k_new, past_k, past_v, Wv, bv,
             elif first:
                 O_PS[h] = ps_o.tile([P, NT, HD], F32, name="o_ps", tag="yo", bufs=1)
             for it in its:
+                j = NT - 1 - it if h == H - 1 else it
                 for g in range(3):
-                    o = it * 384 + g * P
+                    o = j * 256 + g * P if g < 2 else 1024 + j * P
                     nc.tensor.matmul_mx(out=O_PS[h][:, it, :],
                                         lhsT=EC[h][:, o:o + P].bitcast(FP8X4), lhsT_scale=ES[h][:, o:o + P],
                                         rhs=VC[h][:, g * HD:(g + 1) * HD].bitcast(FP8X4), rhs_scale=VS[h][:, g * HD:(g + 1) * HD],
@@ -326,7 +308,8 @@ def tile_flashattentionmodule_pa_kernel(tc, x, q, k_new, past_k, past_v, Wv, bv,
 
         def finish(h, lo, hi):
             c = h * NT
-            nc.vector.reciprocal(out=rinv[:, c + lo:c + hi], in_=sums[:, c + lo:c + hi])
+            nc.vector.tensor_tensor(out=sums_t[:, c + lo:c + hi], in0=sums[:, c + lo:c + hi], in1=sums_n[:, c + lo:c + hi], op=ALU.add)
+            nc.vector.reciprocal(out=rinv[:, c + lo:c + hi], in_=sums_t[:, c + lo:c + hi])
             o_sb = hd.tile([P, NT, HD], F32, name="o_sb", tag="o_sb", bufs=4)
             nc.vector.tensor_tensor(out=o_sb[:, lo:hi, :], in0=O_PS[h][:, lo:hi, :],
                                     in1=rinv[:, c + lo:c + hi].unsqueeze(2).to_broadcast([P, hi - lo, HD]), op=ALU.mult)
@@ -360,28 +343,20 @@ def tile_flashattentionmodule_pa_kernel(tc, x, q, k_new, past_k, past_v, Wv, bv,
                 quant_w(hh)
             for hh in heads_at(k, "quant_v"):
                 quant_v(hh)
-            if ok(k - 3):
-                st6n(k - 3)
-            if ok(k - LAG) and k - LAG < NTILES - TL:
-                st6p(k - LAG)
-            if ok(k - LAG + 1) and k - LAG + 1 >= NTILES - TL:
-                st6p(k - LAG + 1)
+            for n in (k - LAG, k - LAG + 1):
+                if ok(n) and (n == NTILES - 1) == (n > k - LAG):
+                    st6p(n)
+                    if n % 2 == 1:
+                        st6n(n // 2)
             for piece in range(4):
                 for hh in heads_at(k, "v%d" % piece):
                     regroup_v(hh, piece)
             if ok(k):
                 st2(k)
-            if ok(k - 2):
-                st5b(k - 2, "v")
-                if (k - 2) % NV == NV // 2:
-                    st5a(k - 2, "v")
             if ok(k):
                 st2b(k)
             if 1 <= k - 1 < NT:
                 x_ev(k - 1, 1, "v")
-            for hh in heads_at(k - 1, "w1"):
-                if hh > 0 and hh % WV == 0:
-                    w_ev(hh, 1, "v")
             for hh in heads_at(k, "finish"):
                 if hh < H - 1:
                     finish(hh, 0, NT)
@@ -399,8 +374,9 @@ def tile_flashattentionmodule_pa_kernel(tc, x, q, k_new, past_k, past_v, Wv, bv,
                 st3(k)
             if ok(k - 1):
                 st4(k - 1)
-                if (k - 1) % NV != NV // 2:
-                    st5a(k - 1, "s")
+                st5a(k - 1, "s")
+                if (k - 1) % 2 == 1:
+                    st5b((k - 1) // 2, "s")
             if k == LASTPV:
                 pv(H - 1, [3, 2], True)
             if k == LASTPV + 1:
@@ -419,10 +395,7 @@ def tile_flashattentionmodule_pa_kernel(tc, x, q, k_new, past_k, past_v, Wv, bv,
                 x_tr(k, 1, "yo")
             for part in range(2):
                 for hh in heads_at(k, "w%d" % part):
-                    if hh > 0 and part == 1 and hh % WV == 0:
-                        w_tr(hh, part, "sd")
-                    else:
-                        prep_w(hh, part, WE[part], ("tN", "tP")[part] if hh == 0 else "sd")
+                    prep_w(hh, part, WE[part], ("tN", "tP")[part] if hh == 0 else "sd")
                 for hh in heads_at(k, "qk%d" % part):
                     if hh > 0:
                         prep_qk(hh, part, QE[part])

@@ -231,20 +231,16 @@ def tile_flashattentionmodule_pa_kernel(tc, x, q, k_new, past_k, past_v, Wv, bv,
             nc.tensor.matmul(out=sv[:, :, w - 32:w], lhsT=ident_bf[:], rhs=mask_bf[:].rearrange("i (r p) -> i r p", r=4), start=False, stop=True)
             S_PS[n] = [sA, sB, sC]
 
-        def st2(n):
+        def st2(n, part):
             h, it = where(n)
             c = h * NT + it
-            S_SB[n] = tl.tile([P, 1536], F32, name="s_sb", tag="s_sb")
-            off = 0
-            for j, w in enumerate(widths(it)):
-                nc.vector.tensor_scalar(out=S_SB[n][:, off:off + w], in0=S_PS[n][j][:, 0:w], scalar1=-SCALE, scalar2=None,
-                                        op0=ALU.mult, op1=ALU.min, accum_out=mn3[:, 4 * c + j:4 * c + j + 1])
-                off += w
-
-        def st2b(n):
-            h, it = where(n)
-            c = h * NT + it
-            nc.vector.tensor_reduce(out=nm[:, c:c + 1], in_=mn3[:, 4 * c:4 * c + 3], axis=AX.X, op=ALU.min)
+            if part == 0:
+                S_SB[n] = tl.tile([P, 1536], F32, name="s_sb", tag="s_sb")
+            w = widths(it)[part]
+            nc.vector.tensor_scalar(out=S_SB[n][:, 512 * part:512 * part + w], in0=S_PS[n][part][:, 0:w], scalar1=-SCALE,
+                                    scalar2=None if part == 0 else mn3[:, 4 * c + part - 1:4 * c + part],
+                                    op0=ALU.mult, op1=ALU.min,
+                                    accum_out=nm[:, c:c + 1] if part == 2 else mn3[:, 4 * c + part:4 * c + part + 1])
 
         def st3(n):
             h, it = where(n)
@@ -306,10 +302,16 @@ def tile_flashattentionmodule_pa_kernel(tc, x, q, k_new, past_k, past_v, Wv, bv,
                                         rhs=VC[h][:, g * HD:(g + 1) * HD].bitcast(FP8X4), rhs_scale=VS[h][:, g * HD:(g + 1) * HD],
                                         start=(g == 0), stop=(g == 2))
 
-        def finish(h, lo, hi):
+        def finish_a(h, lo, hi):
             c = h * NT
             nc.vector.tensor_tensor(out=sums_t[:, c + lo:c + hi], in0=sums[:, c + lo:c + hi], in1=sums_n[:, c + lo:c + hi], op=ALU.add)
+
+        def finish_b(h, lo, hi):
+            c = h * NT
             nc.vector.reciprocal(out=rinv[:, c + lo:c + hi], in_=sums_t[:, c + lo:c + hi])
+
+        def finish_c(h, lo, hi):
+            c = h * NT
             o_sb = hd.tile([P, NT, HD], F32, name="o_sb", tag="o_sb", bufs=4)
             nc.vector.tensor_tensor(out=o_sb[:, lo:hi, :], in0=O_PS[h][:, lo:hi, :],
                                     in1=rinv[:, c + lo:c + hi].unsqueeze(2).to_broadcast([P, hi - lo, HD]), op=ALU.mult)
@@ -337,37 +339,47 @@ def tile_flashattentionmodule_pa_kernel(tc, x, q, k_new, past_k, past_v, Wv, bv,
                     load_wv(h + 3)
                 if h + 2 < H:
                     load_pv(h + 2)
+            def quants(news):
+                for n in (k - LAG, k - LAG + 1):
+                    if ok(n) and (n == NTILES - 1) == (n > k - LAG):
+                        if not news:
+                            st6p(n)
+                        elif n % 2 == 1:
+                            st6n(n // 2)
+
+            done = [hh for hh in heads_at(k, "finish") if hh < H - 1]
             if 0 <= k - XQ < NT:
                 x_quant(k - XQ)
-            for hh in heads_at(k, "quant_w"):
-                quant_w(hh)
-            for hh in heads_at(k, "quant_v"):
-                quant_v(hh)
-            for n in (k - LAG, k - LAG + 1):
-                if ok(n) and (n == NTILES - 1) == (n > k - LAG):
-                    st6p(n)
-                    if n % 2 == 1:
-                        st6n(n // 2)
+            for hh in done:
+                finish_a(hh, 0, NT)
+            if ok(k):
+                st2(k, 0)
+            quants(False)
             for piece in range(4):
                 for hh in heads_at(k, "v%d" % piece):
                     regroup_v(hh, piece)
             if ok(k):
-                st2(k)
+                st2(k, 1)
+            for hh in done:
+                finish_b(hh, 0, NT)
+            for hh in heads_at(k, "quant_w"):
+                quant_w(hh)
+            quants(True)
             if ok(k):
-                st2b(k)
+                st2(k, 2)
             if 1 <= k - 1 < NT:
                 x_ev(k - 1, 1, "v")
-            for hh in heads_at(k, "finish"):
-                if hh < H - 1:
-                    finish(hh, 0, NT)
-            if k == LASTPV + 1:
-                finish(H - 1, 2, 4)
-            if k == LASTPV + 2:
-                finish(H - 1, 1, 2)
-            if k == LASTPV + 3:
-                finish(H - 1, 0, 1)
+            for hh in done:
+                finish_c(hh, 0, NT)
+            for i, (lo, hi) in enumerate(((2, 4), (1, 2), (0, 1))):
+                if k == LASTPV + 1 + i:
+                    finish_a(H - 1, lo, hi)
+                    finish_b(H - 1, lo, hi)
+                    finish_c(H - 1, lo, hi)
             for hh in heads_at(k, "y_evac"):
                 y_evac(hh)
+            for hh in heads_at(k, "quant_v"):
+                quant_v(hh)
             if ok(k + 1):
                 st1(k + 1)
             if ok(k):

@@ -51,7 +51,7 @@ def tile_flashattentionmodule_pa_kernel(tc, x, q, k_new, past_k, past_v, Wv, bv,
             Q_SB[h] = ld.tile([P, NT, HD], BF16, name="q_sb", tag="q_sb")
             nc.sync.dma_start(out=Q_SB[h][:], in_=q[0, h].rearrange("(a p) d -> p a d", p=P))
             KN_SB[h] = ld.tile([P, NT, HD], BF16, name="kn_sb", tag="kn_sb")
-            nc.sync.dma_start(out=KN_SB[h][:], in_=k_new[0, h].rearrange("(p r) d -> p r d", r=NT))
+            nc.sync.dma_start(out=KN_SB[h][:].rearrange("p (u e) d -> p u e d", u=2), in_=k_new[0, h].rearrange("(u p e) d -> p u e d", u=2, e=2))
             PK_SB[h] = ld.tile([P, 8, HD], BF16, name="pk_sb", tag="pk_sb")
             nc.sync.dma_start(out=PK_SB[h][:], in_=past_k[0, h].rearrange("(p r) d -> p r d", r=8))
 
@@ -67,7 +67,7 @@ def tile_flashattentionmodule_pa_kernel(tc, x, q, k_new, past_k, past_v, Wv, bv,
         x_sb = const.tile([P, NT, D], BF16, name="x_sb")
 
         def load_x(a):
-            nc.sync.dma_start(out=x_sb[:, a, :], in_=x[0].rearrange("(p a) k -> a p k", a=NT)[a])
+            nc.sync.dma_start(out=x_sb[:, a, :], in_=x[0].rearrange("(u p e) k -> u e p k", u=2, e=2)[a // 2, a % 2])
 
         load_x(0)
         load_qk(1)
@@ -100,11 +100,12 @@ def tile_flashattentionmodule_pa_kernel(tc, x, q, k_new, past_k, past_v, Wv, bv,
         nc.gpsimd.affine_select(out=mask_f[:], in_=mask_f[:], compare_op=ALU.is_ge, fill=MASKED, base=0,
                                 pattern=[[-1, P]], channel_multiplier=1)
         mask_bf = const.tile([P, P], BF16, name="mask_bf")
-        nc.vector.tensor_copy(out=mask_bf[:].rearrange("i (r w) -> i r w", r=4), in_=mask_f[:].rearrange("i (w r) -> i r w", r=4))
+        nc.vector.tensor_copy(out=mask_bf[:].rearrange("i (e w) -> i e w", e=2), in_=mask_f[:].rearrange("i (w e) -> i e w", e=2))
         mn3 = const.tile([P, NTILES * 4], F32, name="mn3")
         nm = const.tile([P, NTILES], F32, name="nm")
         sums = const.tile([P, NTILES], F32, name="sums")
         sums_n = const.tile([P, NTILES], F32, name="sums_n")
+        nc.vector.memset(sums_n[:], 0.0)
         sums_t = const.tile([P, NTILES], F32, name="sums_t")
         rinv = const.tile([P, NTILES], F32, name="rinv")
         xg = const.tile([P, 4 * S * 4], BF16, name="xg", align_bytes=64)
@@ -216,20 +217,28 @@ def tile_flashattentionmodule_pa_kernel(tc, x, q, k_new, past_k, past_v, Wv, bv,
         def widths(it):
             return [512, 512, P * (it + 1)]
 
-        def st1(n):
+        def st1(n, part):
             h, it = where(n)
             kt = QKT[h]
             lhsT = kt[:, it * P:(it + 1) * P]
-            sA = ps_s.tile([P, 512], F32, name="sA", tag="s")
-            nc.tensor.matmul(out=sA[:], lhsT=lhsT, rhs=kt[:, 1024:1536], start=True, stop=True)
-            sB = ps_s.tile([P, 512], F32, name="sB", tag="s")
-            nc.tensor.matmul(out=sB[:], lhsT=lhsT, rhs=kt[:, 1536:2048], start=True, stop=True)
-            sC = ps_s.tile([P, 512], F32, name="sC", tag="s")
-            w = 32 * (it + 1)
-            sv = sC[:, 0:4 * w].rearrange("q (r p) -> q r p", r=4)
-            nc.tensor.matmul(out=sv, lhsT=lhsT, rhs=kt[:, 512:1024].rearrange("d (r p) -> d r p", r=4)[:, :, 0:w], start=True, stop=False)
-            nc.tensor.matmul(out=sv[:, :, w - 32:w], lhsT=ident_bf[:], rhs=mask_bf[:].rearrange("i (r p) -> i r p", r=4), start=False, stop=True)
-            S_PS[n] = [sA, sB, sC]
+            if part == 0:
+                S_PS[n] = []
+            ps = ps_s.tile([P, 512], F32, name="ps", tag="s")
+            S_PS[n].append(ps)
+            if part < 2:
+                nc.tensor.matmul(out=ps[:], lhsT=lhsT, rhs=kt[:, 1024 + 512 * part:1536 + 512 * part], start=True, stop=True)
+            else:
+                half = it % 2 == 0
+                f = 256 * ((it + 1) // 2)
+                mask = mask_bf[:].rearrange("i (e p) -> i e p", e=2)
+                if f > 0:
+                    nc.tensor.matmul(out=ps[:, 0:f], lhsT=lhsT, rhs=kt[:, 512:512 + f], start=True, stop=half)
+                if half:
+                    dv = ps[:, f:f + P].rearrange("q (e p) -> q e p", e=2)
+                    nc.tensor.matmul(out=dv, lhsT=lhsT, rhs=kt[:, 512 + f:768 + f].rearrange("d (e p) -> d e p", e=2)[:, :, 0:64], start=True, stop=False)
+                else:
+                    dv = ps[:, f - 256:f].rearrange("q (e p) -> q e p", e=2)[:, :, 64:P]
+                nc.tensor.matmul(out=dv, lhsT=ident_bf[:], rhs=mask, start=False, stop=True)
 
         def st2(n, part):
             h, it = where(n)
@@ -245,19 +254,25 @@ def tile_flashattentionmodule_pa_kernel(tc, x, q, k_new, past_k, past_v, Wv, bv,
         def st3(n):
             h, it = where(n)
             c = h * NT + it
-            w = 32 * (it + 1)
-            nc.scalar.activation(out=E_SB[e_tile(n)][:, 0:1024].rearrange("q (c p e) -> q c p e", c=4, e=2),
-                                 in_=S_SB[n][:, 0:1024].rearrange("q (c e p) -> q c p e", c=4, e=2),
+            nb = 4 + (it + 1) // 2
+            f = 256 * nb
+            e_sb = E_SB[e_tile(n)]
+            nc.scalar.activation(out=e_sb[:, 0:f].rearrange("q (c p e) -> q c p e", c=nb, e=2),
+                                 in_=S_SB[n][:, 0:f].rearrange("q (c e p) -> q c p e", c=nb, e=2),
                                  func=ACTF.Exp, bias=nm[:, c:c + 1], scale=-1.0, accum_out=sums[:, c:c + 1])
-            nc.scalar.activation(out=E_SB[e_tile(n)][:, 1024:1536].rearrange("q (u p e) -> q u p e", u=2, e=2)[:, :, 0:w, :],
-                                 in_=S_SB[n][:, 1024:1024 + 4 * w].rearrange("q (u e p) -> q u p e", u=2, e=2),
-                                 func=ACTF.Exp, bias=nm[:, c:c + 1], scale=-1.0, accum_out=sums_n[:, c:c + 1])
+            if it % 2 == 0:
+                nc.scalar.activation(out=e_sb[:, f:f + P].rearrange("q (p e) -> q p e", e=2),
+                                     in_=S_SB[n][:, f:f + P].rearrange("q (e p) -> q p e", e=2),
+                                     func=ACTF.Exp, bias=nm[:, c:c + 1], scale=-1.0, accum_out=sums_n[:, c:c + 1])
 
-        def st4(n):
+        def st4p(n):
             words = E_SB[e_tile(n)][:].bitcast(F32)
             TP_PS[n] = ps_t.tile([P, 4, P], F32, name="tP", tag="tP", bufs=2)
             for c in range(4):
                 nc.tensor.transpose(TP_PS[n][:, c, :], words[:, c * P:(c + 1) * P], ident_f[:])
+
+        def st4n(n):
+            words = E_SB[e_tile(n)][:].bitcast(F32)
             if n % 2 == 0:
                 TN_PS[n // 2] = ps_t.tile([P, 2, 2, P], F32, name="tN", tag="tN", bufs=1)
             for u in range(2):
@@ -327,7 +342,8 @@ def tile_flashattentionmodule_pa_kernel(tc, x, q, k_new, past_k, past_v, Wv, bv,
         prep_qk(0, 1, "s", "tP")
         x_tr(0, 0, "sd")
         x_tr(0, 1, "yo")
-        st1(0)
+        for part in range(3):
+            st1(0, part)
         x_ev(0, 0, "s")
         x_ev(0, 1, "s")
         for k in range(NTILES + 12):
@@ -381,14 +397,14 @@ def tile_flashattentionmodule_pa_kernel(tc, x, q, k_new, past_k, past_v, Wv, bv,
             for hh in heads_at(k, "quant_v"):
                 quant_v(hh)
             if ok(k + 1):
-                st1(k + 1)
+                st1(k + 1, 0)
             if ok(k):
                 st3(k)
             if ok(k - 1):
-                st4(k - 1)
+                st4p(k - 1)
                 st5a(k - 1, "s")
-                if (k - 1) % 2 == 1:
-                    st5b((k - 1) // 2, "s")
+            if ok(k + 1):
+                st1(k + 1, 1)
             if k == LASTPV:
                 pv(H - 1, [3, 2], True)
             if k == LASTPV + 1:
@@ -401,6 +417,12 @@ def tile_flashattentionmodule_pa_kernel(tc, x, q, k_new, past_k, past_v, Wv, bv,
                         pv(hh, [2 * half, 2 * half + 1], half == 0)
                 for hh in heads_at(k, "proj%d" % half):
                     proj(hh, half)
+            if ok(k - 1):
+                st4n(k - 1)
+                if (k - 1) % 2 == 1:
+                    st5b((k - 1) // 2, "s")
+            if ok(k + 1):
+                st1(k + 1, 2)
             if 1 <= k < NT:
                 x_tr(k, 0, "tP")
                 x_ev(k, 0, "s")

@@ -23,11 +23,10 @@ FLOPS = 2 * S * D * D + 2 * 2 * H * S * (PAST + S) * HD
 TBUFS = {"sd": 1, "tP": 2, "tN": 1, "yo": 1}
 LAG = 4
 LASTPV = 65
-WE = "ss"
 QE = "ss"
 XQ = 2
-A = {"qk0": -4, "qk1": -3, "w0": -2, "w1": -1, "quant_w": 2, "proj0": 4, "proj1": 5, "y_evac": 6, "quant_v": 7, "pv0": 10, "pv1": 11, "finish": 12, "v0": 0, "v1": 1, "v2": 2, "v3": 3}
-F = {("w0", 0): 0, ("w1", 0): 0, ("quant_w", 0): 3, ("proj0", 15): 62, ("proj1", 15): 63, ("y_evac", 15): 64, ("quant_v", 15): 65, ("pv0", 14): 64, ("pv1", 14): 65, ("finish", 14): 66}
+A = {"qk0": -4, "qk1": -3, "w0": -2, "w1": -1, "quant_w": 2, "proj0": 4, "proj1": 5, "y_evac": 6, "quant_v": 7, "pv0": 10, "pv1": 11, "quant_n": 8, "finish": 12, "v0": 0, "v1": 1, "v2": 2, "v3": 3}
+F = {("w0", 0): -1, ("w1", 0): -1, ("quant_w", 0): 3, ("proj0", 15): 62, ("proj1", 15): 63, ("y_evac", 15): 64, ("quant_v", 15): 65, ("pv0", 14): 64, ("pv1", 14): 65, ("finish", 14): 66}
 
 
 def tile_flashattentionmodule_pa_kernel(tc, x, q, k_new, past_k, past_v, Wv, bv, out):
@@ -70,8 +69,8 @@ def tile_flashattentionmodule_pa_kernel(tc, x, q, k_new, past_k, past_v, Wv, bv,
             nc.sync.dma_start(out=x_sb[:, a, :], in_=x[0].rearrange("(u p e) k -> u e p k", u=2, e=2)[a // 2, a % 2])
 
         load_x(0)
-        load_qk(1)
         load_wv(0)
+        load_qk(1)
         load_x(1)
         load_x(2)
         load_x(3)
@@ -104,9 +103,6 @@ def tile_flashattentionmodule_pa_kernel(tc, x, q, k_new, past_k, past_v, Wv, bv,
         mn3 = const.tile([P, NTILES * 4], F32, name="mn3")
         nm = const.tile([P, NTILES], F32, name="nm")
         sums = const.tile([P, NTILES], F32, name="sums")
-        sums_n = const.tile([P, NTILES], F32, name="sums_n")
-        nc.vector.memset(sums_n[:], 0.0)
-        sums_t = const.tile([P, NTILES], F32, name="sums_t")
         rinv = const.tile([P, NTILES], F32, name="rinv")
         xg = const.tile([P, 4 * S * 4], BF16, name="xg", align_bytes=64)
         x_codes = const.tile([P, 4 * S], U32, name="x_codes", align_bytes=64)
@@ -146,7 +142,11 @@ def tile_flashattentionmodule_pa_kernel(tc, x, q, k_new, past_k, past_v, Wv, bv,
                     src = Q_SB[h][:, j, :] if j < 4 else KN_SB[h][:, j - 4, :]
                 else:
                     src = PK_SB[h][:, j, :]
-                nc.tensor.transpose(tq[:, j, :], src, ident_bf[:])
+                dst = tq[:, j, :]
+                if part == 1 or j >= 4:
+                    b, par = divmod(j, 2)
+                    dst = tq[:].rearrange("d j i -> d (j i)").rearrange("d (b h e l) -> d b h e l", b=4, h=2, e=2)[:, b, :, par, :]
+                nc.tensor.transpose(dst, src, ident_bf[:])
             evac(e, QKT[h][:, part * 1024:(part + 1) * 1024], tq[:].rearrange("p j i -> p (j i)"))
 
         TW = {}
@@ -228,17 +228,9 @@ def tile_flashattentionmodule_pa_kernel(tc, x, q, k_new, past_k, past_v, Wv, bv,
             if part < 2:
                 nc.tensor.matmul(out=ps[:], lhsT=lhsT, rhs=kt[:, 1024 + 512 * part:1536 + 512 * part], start=True, stop=True)
             else:
-                half = it % 2 == 0
-                f = 256 * ((it + 1) // 2)
-                mask = mask_bf[:].rearrange("i (e p) -> i e p", e=2)
-                if f > 0:
-                    nc.tensor.matmul(out=ps[:, 0:f], lhsT=lhsT, rhs=kt[:, 512:512 + f], start=True, stop=half)
-                if half:
-                    dv = ps[:, f:f + P].rearrange("q (e p) -> q e p", e=2)
-                    nc.tensor.matmul(out=dv, lhsT=lhsT, rhs=kt[:, 512 + f:768 + f].rearrange("d (e p) -> d e p", e=2)[:, :, 0:64], start=True, stop=False)
-                else:
-                    dv = ps[:, f - 256:f].rearrange("q (e p) -> q e p", e=2)[:, :, 64:P]
-                nc.tensor.matmul(out=dv, lhsT=ident_bf[:], rhs=mask, start=False, stop=True)
+                w = P * (it + 1)
+                nc.tensor.matmul(out=ps[:, 0:w], lhsT=lhsT, rhs=kt[:, 512:512 + w], start=True, stop=False)
+                nc.tensor.matmul(out=ps[:, w - P:w], lhsT=ident_bf[:], rhs=mask_bf[:], start=False, stop=True)
 
         def st2(n, part):
             h, it = where(n)
@@ -254,16 +246,10 @@ def tile_flashattentionmodule_pa_kernel(tc, x, q, k_new, past_k, past_v, Wv, bv,
         def st3(n):
             h, it = where(n)
             c = h * NT + it
-            nb = 4 + (it + 1) // 2
-            f = 256 * nb
-            e_sb = E_SB[e_tile(n)]
-            nc.scalar.activation(out=e_sb[:, 0:f].rearrange("q (c p e) -> q c p e", c=nb, e=2),
-                                 in_=S_SB[n][:, 0:f].rearrange("q (c e p) -> q c p e", c=nb, e=2),
+            b = 9 + it
+            nc.scalar.activation(out=E_SB[e_tile(n)][:, 0:b * P].rearrange("q (b l e) -> q b l e", b=b, e=2),
+                                 in_=S_SB[n][:, 0:b * P].rearrange("q (b e l) -> q b l e", b=b, e=2),
                                  func=ACTF.Exp, bias=nm[:, c:c + 1], scale=-1.0, accum_out=sums[:, c:c + 1])
-            if it % 2 == 0:
-                nc.scalar.activation(out=e_sb[:, f:f + P].rearrange("q (p e) -> q p e", e=2),
-                                     in_=S_SB[n][:, f:f + P].rearrange("q (e p) -> q p e", e=2),
-                                     func=ACTF.Exp, bias=nm[:, c:c + 1], scale=-1.0, accum_out=sums_n[:, c:c + 1])
 
         def st4p(n):
             words = E_SB[e_tile(n)][:].bitcast(F32)
@@ -279,27 +265,30 @@ def tile_flashattentionmodule_pa_kernel(tc, x, q, k_new, past_k, past_v, Wv, bv,
                 nc.tensor.transpose(TN_PS[n // 2][:, n % 2, u, :], words[:, 512 + u * P:512 + (u + 1) * P], ident_f[:])
 
         def st5a(n, e):
-            ETG[n] = tl.tile([P, 1024], BF16, name="etg", tag="etg", align_bytes=64)
-            evac(e, ETG[n][:].bitcast(F32).rearrange("p (g i u) -> p g i u", g=2, u=2),
-                 TP_PS[n][:].rearrange("p (g u) i -> p g i u", u=2))
+            if n % 2 == 0:
+                ETG[n // 2] = tl.tile([P, 2048], BF16, name="etg", tag="etg", align_bytes=64)
+            words = ETG[n // 2][:].bitcast(F32).rearrange("p (j g i u) -> p j g i u", j=2, g=2, u=2)
+            evac(e, words[:, n % 2, :, :, :], TP_PS[n][:].rearrange("p (g u) i -> p g i u", u=2))
 
         def st5b(m, e):
-            ETN[m] = tl.tile([P, 1024], BF16, name="etn", tag="etn", align_bytes=64)
-            evac(e, ETN[m][:].bitcast(F32).rearrange("p (j i u) -> p j i u", j=2, u=2),
+            h, j = divmod(2 * m, NT)
+            if j == 0:
+                ETN[h] = hd.tile([P, 2048], BF16, name="etn", tag="etn", align_bytes=64)
+            evac(e, ETN[h][:].bitcast(F32).rearrange("p (j i u) -> p j i u", j=NT, u=2)[:, j:j + 2, :, :],
                  TN_PS[m][:].rearrange("p j u i -> p j i u"))
 
-        def st6n(m):
-            h, j = divmod(2 * m, NT)
-            o = 1024 + j * P
-            nc.vector.quantize_mx(out=EC[h][:, o:o + 256].bitcast(FP8X4), scales=ES[h][:, o:o + 256], in_=ETN[m][:])
+        def st6n(h, lo, hi):
+            o = 1024 + lo * P
+            e = 1024 + hi * P
+            nc.vector.quantize_mx(out=EC[h][:, o:e].bitcast(FP8X4), scales=ES[h][:, o:e], in_=ETN[h][:, lo * 512:hi * 512])
 
-        def st6p(n):
-            h, j = divmod(n, NT)
+        def st6p(m):
+            h, j = divmod(2 * m, NT)
             if j == 0:
                 EC[h] = hd.tile([P, NT * 384], U32, name="ec", tag="ec", align_bytes=64, bufs=3)
                 ES[h] = hd.tile([P, NT * 384], U8, name="es", tag="es", align_bytes=64, bufs=3)
             o = j * 256
-            nc.vector.quantize_mx(out=EC[h][:, o:o + 256].bitcast(FP8X4), scales=ES[h][:, o:o + 256], in_=ETG[n][:])
+            nc.vector.quantize_mx(out=EC[h][:, o:o + 512].bitcast(FP8X4), scales=ES[h][:, o:o + 512], in_=ETG[m][:])
 
         O_PS = {}
 
@@ -317,13 +306,9 @@ def tile_flashattentionmodule_pa_kernel(tc, x, q, k_new, past_k, past_v, Wv, bv,
                                         rhs=VC[h][:, g * HD:(g + 1) * HD].bitcast(FP8X4), rhs_scale=VS[h][:, g * HD:(g + 1) * HD],
                                         start=(g == 0), stop=(g == 2))
 
-        def finish_a(h, lo, hi):
-            c = h * NT
-            nc.vector.tensor_tensor(out=sums_t[:, c + lo:c + hi], in0=sums[:, c + lo:c + hi], in1=sums_n[:, c + lo:c + hi], op=ALU.add)
-
         def finish_b(h, lo, hi):
             c = h * NT
-            nc.vector.reciprocal(out=rinv[:, c + lo:c + hi], in_=sums_t[:, c + lo:c + hi])
+            nc.vector.reciprocal(out=rinv[:, c + lo:c + hi], in_=sums[:, c + lo:c + hi])
 
         def finish_c(h, lo, hi):
             c = h * NT
@@ -346,6 +331,8 @@ def tile_flashattentionmodule_pa_kernel(tc, x, q, k_new, past_k, past_v, Wv, bv,
             st1(0, part)
         x_ev(0, 0, "s")
         x_ev(0, 1, "s")
+        prep_w(0, 0, "s", "tN")
+        prep_w(0, 1, "s", "tP")
         for k in range(NTILES + 12):
             h, it = divmod(k, NT)
             if it == 0:
@@ -355,81 +342,84 @@ def tile_flashattentionmodule_pa_kernel(tc, x, q, k_new, past_k, past_v, Wv, bv,
                     load_wv(h + 3)
                 if h + 2 < H:
                     load_pv(h + 2)
-            def quants(news):
+            def quant_past():
                 for n in (k - LAG, k - LAG + 1):
-                    if ok(n) and (n == NTILES - 1) == (n > k - LAG):
-                        if not news:
-                            st6p(n)
-                        elif n % 2 == 1:
-                            st6n(n // 2)
+                    if ok(n) and n % 2 == 1 and (n == NTILES - 1) == (n > k - LAG):
+                        st6p(n // 2)
+
+            def quant_new():
+                for hh in heads_at(k, "quant_n"):
+                    if hh < H - 1:
+                        st6n(hh, 0, NT)
+                if k == LASTPV:
+                    st6n(H - 1, 0, 2)
+                if k == LASTPV + 1:
+                    st6n(H - 1, 2, NT)
 
             done = [hh for hh in heads_at(k, "finish") if hh < H - 1]
             if 0 <= k - XQ < NT:
                 x_quant(k - XQ)
-            for hh in done:
-                finish_a(hh, 0, NT)
             if ok(k):
                 st2(k, 0)
-            quants(False)
+            for hh in done:
+                finish_b(hh, 0, NT)
+            for hh in heads_at(k, "quant_w"):
+                quant_w(hh)
+            quant_past()
+            quant_new()
             for piece in range(4):
                 for hh in heads_at(k, "v%d" % piece):
                     regroup_v(hh, piece)
             if ok(k):
                 st2(k, 1)
             for hh in done:
-                finish_b(hh, 0, NT)
-            for hh in heads_at(k, "quant_w"):
-                quant_w(hh)
-            quants(True)
+                finish_c(hh, 0, NT)
+            for hh in heads_at(k, "y_evac"):
+                y_evac(hh)
             if ok(k):
                 st2(k, 2)
             if 1 <= k - 1 < NT:
                 x_ev(k - 1, 1, "v")
-            for hh in done:
-                finish_c(hh, 0, NT)
-            for i, (lo, hi) in enumerate(((2, 4), (1, 2), (0, 1))):
-                if k == LASTPV + 1 + i:
-                    finish_a(H - 1, lo, hi)
-                    finish_b(H - 1, lo, hi)
-                    finish_c(H - 1, lo, hi)
-            for hh in heads_at(k, "y_evac"):
-                y_evac(hh)
+            if k == LASTPV:
+                finish_b(H - 1, 0, NT)
+            if k == LASTPV + 1:
+                finish_c(H - 1, 2, 4)
+            if k == LASTPV + 2:
+                finish_c(H - 1, 0, 2)
             for hh in heads_at(k, "quant_v"):
                 quant_v(hh)
             if ok(k + 1):
                 st1(k + 1, 0)
+            if ok(k + 1):
+                st1(k + 1, 1)
+            if ok(k + 1):
+                st1(k + 1, 2)
             if ok(k):
                 st3(k)
             if ok(k - 1):
                 st4p(k - 1)
                 st5a(k - 1, "s")
-            if ok(k + 1):
-                st1(k + 1, 1)
+            if ok(k - 1):
+                st4n(k - 1)
+                if (k - 1) % 2 == 1:
+                    st5b((k - 1) // 2, "s")
             if k == LASTPV:
                 pv(H - 1, [3, 2], True)
             if k == LASTPV + 1:
-                pv(H - 1, [1], False)
-            if k == LASTPV + 2:
-                pv(H - 1, [0], False)
+                pv(H - 1, [1, 0], False)
             for half in range(2):
                 for hh in heads_at(k, "pv%d" % half):
                     if hh < H - 1:
                         pv(hh, [2 * half, 2 * half + 1], half == 0)
                 for hh in heads_at(k, "proj%d" % half):
                     proj(hh, half)
-            if ok(k - 1):
-                st4n(k - 1)
-                if (k - 1) % 2 == 1:
-                    st5b((k - 1) // 2, "s")
-            if ok(k + 1):
-                st1(k + 1, 2)
             if 1 <= k < NT:
                 x_tr(k, 0, "tP")
                 x_ev(k, 0, "s")
                 x_tr(k, 1, "yo")
             for part in range(2):
                 for hh in heads_at(k, "w%d" % part):
-                    prep_w(hh, part, WE[part], ("tN", "tP")[part] if hh == 0 else "sd")
+                    prep_w(hh, part, "s", "sd")
                 for hh in heads_at(k, "qk%d" % part):
                     if hh > 0:
                         prep_qk(hh, part, QE[part])

@@ -392,17 +392,8 @@ def tile_flashattentionmodule_pa_kernel(tc, x, q, k_new, past_k, past_v, Wv, bv,
                 st1(k + 1, 0)
             if ok(k + 1):
                 st1(k + 1, 1)
-            if ok(k + 1):
-                st1(k + 1, 2)
             if ok(k):
                 st3(k)
-            if ok(k - 1):
-                st4p(k - 1)
-                st5a(k - 1, "s")
-            if ok(k - 1):
-                st4n(k - 1)
-                if (k - 1) % 2 == 1:
-                    st5b((k - 1) // 2, "s")
             if k == LASTPV:
                 pv(H - 1, [3, 2], True)
             if k == LASTPV + 1:
@@ -413,6 +404,15 @@ def tile_flashattentionmodule_pa_kernel(tc, x, q, k_new, past_k, past_v, Wv, bv,
                         pv(hh, [2 * half, 2 * half + 1], half == 0)
                 for hh in heads_at(k, "proj%d" % half):
                     proj(hh, half)
+            if ok(k + 1):
+                st1(k + 1, 2)
+            if ok(k - 1):
+                st4p(k - 1)
+                st5a(k - 1, "s")
+            if ok(k - 1):
+                st4n(k - 1)
+                if (k - 1) % 2 == 1:
+                    st5b((k - 1) // 2, "s")
             if 1 <= k < NT:
                 x_tr(k, 0, "tP")
                 x_ev(k, 0, "s")

@@ -25,8 +25,8 @@ LAG = 4
 LASTPV = 65
 QE = "ss"
 XQ = 2
-A = {"qk0": -4, "qk1": -3, "w0": -2, "w1": -1, "quant_w": 2, "proj0": 4, "proj1": 5, "y_evac": 6, "quant_v": 7, "pv0": 10, "pv1": 11, "quant_n": 8, "finish": 12, "v0": 0, "v1": 1, "v2": 2, "v3": 3}
-F = {("w0", 0): -1, ("w1", 0): -1, ("quant_w", 0): 3, ("proj0", 15): 62, ("proj1", 15): 63, ("y_evac", 15): 64, ("quant_v", 15): 65, ("pv0", 14): 64, ("pv1", 14): 65, ("finish", 14): 66}
+A = {"qk0": -4, "qk1": -3, "w0": -2, "w1": -1, "quant_w": 1, "proj0": 4, "proj1": 5, "y_evac": 6, "quant_va": 6, "quant_vb": 7, "pv0": 10, "pv1": 11, "quant_n": 8, "recip": 11, "finish": 12, "v0": 0, "v1": 1, "v2": 2, "v3": 3}
+F = {("w0", 0): -1, ("w1", 0): -1, ("quant_w", 0): 3, ("proj0", 15): 62, ("proj1", 15): 63, ("y_evac", 15): 64, ("quant_va", 15): 64, ("quant_vb", 15): 65, ("pv0", 14): 64, ("pv1", 14): 65, ("recip", 14): 65, ("finish", 14): 66}
 
 
 def tile_flashattentionmodule_pa_kernel(tc, x, q, k_new, past_k, past_v, Wv, bv, out):
@@ -68,7 +68,9 @@ def tile_flashattentionmodule_pa_kernel(tc, x, q, k_new, past_k, past_v, Wv, bv,
         def load_x(a):
             nc.sync.dma_start(out=x_sb[:, a, :], in_=x[0].rearrange("(u p e) k -> u e p k", u=2, e=2)[a // 2, a % 2])
 
-        load_x(0)
+        for i in range(2):
+            nc.sync.dma_start(out=x_sb[:, 0, i * 1024:(i + 1) * 1024],
+                              in_=x[0].rearrange("(u p e) k -> u e p k", u=2, e=2)[0, 0][:, i * 1024:(i + 1) * 1024])
         load_wv(0)
         load_qk(1)
         load_x(1)
@@ -201,11 +203,12 @@ def tile_flashattentionmodule_pa_kernel(tc, x, q, k_new, past_k, past_v, Wv, bv,
             nc.vector.tensor_tensor(out=dst, in0=Y_PS[h][:].rearrange("p t d -> p d t"),
                                     in1=bvb[:, h * HD:(h + 1) * HD].unsqueeze(2).to_broadcast([P, HD, 4]), op=ALU.add)
 
-        def quant_v(h):
-            VC[h] = hd.tile([P, 3 * HD], U32, name="vc", tag="vc", align_bytes=64, bufs=3)
-            VS[h] = hd.tile([P, 3 * HD], U8, name="vs", tag="vs", align_bytes=64, bufs=3)
-            nc.vector.quantize_mx(out=VC[h][:, 0:256].bitcast(FP8X4), scales=VS[h][:, 0:256], in_=VG[h][:, 0:1024])
-            nc.vector.quantize_mx(out=VC[h][:, 256:384].bitcast(FP8X4), scales=VS[h][:, 256:384], in_=VG[h][:, 1024:1536])
+        def quant_v(h, part):
+            if part == 0:
+                VC[h] = hd.tile([P, 3 * HD], U32, name="vc", tag="vc", align_bytes=64, bufs=3)
+                VS[h] = hd.tile([P, 3 * HD], U8, name="vs", tag="vs", align_bytes=64, bufs=3)
+            lo, hi = ((0, 256), (256, 384))[part]
+            nc.vector.quantize_mx(out=VC[h][:, lo:hi].bitcast(FP8X4), scales=VS[h][:, lo:hi], in_=VG[h][:, 4 * lo:4 * hi])
 
         def where(n):
             h, j = divmod(n, NT)
@@ -310,11 +313,15 @@ def tile_flashattentionmodule_pa_kernel(tc, x, q, k_new, past_k, past_v, Wv, bv,
             c = h * NT
             nc.vector.reciprocal(out=rinv[:, c + lo:c + hi], in_=sums[:, c + lo:c + hi])
 
-        def finish_c(h, lo, hi):
+        def finish_c(h, lo, hi, e="v"):
             c = h * NT
             o_sb = hd.tile([P, NT, HD], F32, name="o_sb", tag="o_sb", bufs=4)
-            nc.vector.tensor_tensor(out=o_sb[:, lo:hi, :], in0=O_PS[h][:, lo:hi, :],
-                                    in1=rinv[:, c + lo:c + hi].unsqueeze(2).to_broadcast([P, hi - lo, HD]), op=ALU.mult)
+            if e == "v":
+                nc.vector.tensor_tensor(out=o_sb[:, lo:hi, :], in0=O_PS[h][:, lo:hi, :],
+                                        in1=rinv[:, c + lo:c + hi].unsqueeze(2).to_broadcast([P, hi - lo, HD]), op=ALU.mult)
+            else:
+                for it in range(lo, hi):
+                    nc.scalar.activation(out=o_sb[:, it, :], in_=O_PS[h][:, it, :], func=ACTF.Copy, scale=rinv[:, c + it:c + it + 1])
             nc.sync.dma_start(out=out[0].rearrange("(a p) c -> p a c", p=P)[:, lo:hi, h * HD:(h + 1) * HD], in_=o_sb[:, lo:hi, :])
 
         def ok(n):
@@ -326,9 +333,9 @@ def tile_flashattentionmodule_pa_kernel(tc, x, q, k_new, past_k, past_v, Wv, bv,
         prep_qk(0, 0, "v", "tP")
         prep_qk(0, 1, "s", "tP")
         x_tr(0, 0, "sd")
-        x_tr(0, 1, "yo")
         for part in range(3):
             st1(0, part)
+        x_tr(0, 1, "yo")
         x_ev(0, 0, "s")
         x_ev(0, 1, "s")
         prep_w(0, 0, "s", "tN")
@@ -357,53 +364,63 @@ def tile_flashattentionmodule_pa_kernel(tc, x, q, k_new, past_k, past_v, Wv, bv,
                     st6n(H - 1, 2, NT)
 
             done = [hh for hh in heads_at(k, "finish") if hh < H - 1]
-            if 0 <= k - XQ < NT:
-                x_quant(k - XQ)
+            if k == LASTPV:
+                finish_b(H - 1, 0, NT)
             if ok(k):
                 st2(k, 0)
+            if 0 <= k - XQ < NT:
+                x_quant(k - XQ)
             for hh in done:
-                finish_b(hh, 0, NT)
+                if hh < H - 2:
+                    finish_c(hh, 0, NT)
+            quant_past()
+            for hh in heads_at(k, "quant_va"):
+                quant_v(hh, 0)
+            if ok(k):
+                st2(k, 1)
+            if 1 <= k - 1 < NT:
+                x_ev(k - 1, 1, "v")
             for hh in heads_at(k, "quant_w"):
                 quant_w(hh)
-            quant_past()
+            for hh in heads_at(k, "y_evac"):
+                y_evac(hh)
+            for hh in heads_at(k, "quant_vb"):
+                quant_v(hh, 1)
+            for hh in heads_at(k, "recip"):
+                if hh < H - 1:
+                    finish_b(hh, 0, NT)
             quant_new()
             for piece in range(4):
                 for hh in heads_at(k, "v%d" % piece):
                     regroup_v(hh, piece)
             if ok(k):
-                st2(k, 1)
-            for hh in done:
-                finish_c(hh, 0, NT)
-            for hh in heads_at(k, "y_evac"):
-                y_evac(hh)
-            if ok(k):
                 st2(k, 2)
-            if 1 <= k - 1 < NT:
-                x_ev(k - 1, 1, "v")
-            if k == LASTPV:
-                finish_b(H - 1, 0, NT)
             if k == LASTPV + 1:
                 finish_c(H - 1, 2, 4)
             if k == LASTPV + 2:
                 finish_c(H - 1, 0, 2)
-            for hh in heads_at(k, "quant_v"):
-                quant_v(hh)
             if ok(k + 1):
                 st1(k + 1, 0)
             if ok(k + 1):
                 st1(k + 1, 1)
             if ok(k):
                 st3(k)
-            if k == LASTPV:
-                pv(H - 1, [3, 2], True)
-            if k == LASTPV + 1:
-                pv(H - 1, [1, 0], False)
-            for half in range(2):
-                for hh in heads_at(k, "pv%d" % half):
-                    if hh < H - 1:
-                        pv(hh, [2 * half, 2 * half + 1], half == 0)
-                for hh in heads_at(k, "proj%d" % half):
-                    proj(hh, half)
+            def mx_passes():
+                if k == LASTPV + 1:
+                    finish_c(H - 2, 0, NT, "s")
+                if k == LASTPV:
+                    pv(H - 1, [3, 2], True)
+                if k == LASTPV + 1:
+                    pv(H - 1, [1, 0], False)
+                for half in range(2):
+                    for hh in heads_at(k, "pv%d" % half):
+                        if hh < H - 1:
+                            pv(hh, [2 * half, 2 * half + 1], half == 0)
+                    for hh in heads_at(k, "proj%d" % half):
+                        proj(hh, half)
+
+            if k < NTILES:
+                mx_passes()
             if ok(k + 1):
                 st1(k + 1, 2)
             if ok(k - 1):
@@ -413,6 +430,8 @@ def tile_flashattentionmodule_pa_kernel(tc, x, q, k_new, past_k, past_v, Wv, bv,
                 st4n(k - 1)
                 if (k - 1) % 2 == 1:
                     st5b((k - 1) // 2, "s")
+            if k >= NTILES:
+                mx_passes()
             if 1 <= k < NT:
                 x_tr(k, 0, "tP")
                 x_ev(k, 0, "s")

@@ -20,12 +20,12 @@ SCALE = 1.0 / math.sqrt(HD)
 MASKED = -1.0e30
 FLOPS = 2 * S * D * D + 2 * 2 * H * S * (PAST + S) * HD
 
-TBUFS = {"sd": 1, "tP": 2, "tN": 1, "yo": 1}
+TBUFS = {"tr": 3, "tN": 1, "yo": 1}
 LAG = 4
 LASTPV = 65
 QE = "ss"
 XQ = 2
-A = {"qk0": -4, "qk1": -3, "w0": -2, "w1": -1, "quant_w": 1, "proj0": 4, "proj1": 5, "y_evac": 6, "quant_va": 6, "quant_vb": 7, "pv0": 10, "pv1": 11, "quant_n": 8, "recip": 11, "finish": 12, "v0": 0, "v1": 1, "v2": 2, "v3": 3}
+A = {"qk0": -4, "qk1": -3, "w0": -2, "w1": -1, "quant_w": 2, "proj0": 4, "proj1": 5, "y_evac": 6, "quant_va": 5, "quant_vb": 7, "pv0": 10, "pv1": 11, "quant_n": 8, "recip": 11, "finish": 12, "v0": 0, "v1": 1, "v2": 2, "v3": 3}
 F = {("w0", 0): -1, ("w1", 0): -1, ("quant_w", 0): 3, ("proj0", 15): 62, ("proj1", 15): 63, ("y_evac", 15): 64, ("quant_va", 15): 64, ("quant_vb", 15): 65, ("pv0", 14): 64, ("pv1", 14): 65, ("recip", 14): 65, ("finish", 14): 66}
 
 
@@ -135,7 +135,7 @@ def tile_flashattentionmodule_pa_kernel(tc, x, q, k_new, past_k, past_v, Wv, bv,
                                   scales=x_scales[:, a * 512:(a + 1) * 512],
                                   in_=xg[:, a * 2048:(a + 1) * 2048])
 
-        def prep_qk(h, part, e, tg="sd"):
+        def prep_qk(h, part, e, tg="tr"):
             if part == 0:
                 QKT[h] = hd.tile([P, 16 * P], BF16, name="qkT", tag="qkT", bufs=3)
             tq = ps_t.tile([P, 8, P], BF16, name="tq", tag=tg, bufs=TBUFS[tg])
@@ -153,7 +153,7 @@ def tile_flashattentionmodule_pa_kernel(tc, x, q, k_new, past_k, past_v, Wv, bv,
 
         TW = {}
 
-        def prep_w(h, gp, e, tg="sd"):
+        def prep_w(h, gp, e, tg="tr"):
             w_tr(h, gp, tg)
             w_ev(h, gp, e)
 
@@ -187,7 +187,7 @@ def tile_flashattentionmodule_pa_kernel(tc, x, q, k_new, past_k, past_v, Wv, bv,
 
         def proj(h, half):
             if half == 0:
-                Y_PS[h] = (ps_t if h == H - 1 else ps_o).tile([P, NT, HD], F32, name="y_ps", tag="sd" if h == H - 1 else "yo", bufs=1)
+                Y_PS[h] = (ps_t if h == H - 1 else ps_o).tile([P, NT, HD], F32, name="y_ps", tag="tr" if h == H - 1 else "yo", bufs=3 if h == H - 1 else 1)
             for jt in range(2 * half, 2 * half + 2):
                 for g in range(4):
                     nc.tensor.matmul_mx(
@@ -241,10 +241,13 @@ def tile_flashattentionmodule_pa_kernel(tc, x, q, k_new, past_k, past_v, Wv, bv,
             if part == 0:
                 S_SB[n] = tl.tile([P, 1536], F32, name="s_sb", tag="s_sb")
             w = widths(it)[part]
+            chained = n >= 2
             nc.vector.tensor_scalar(out=S_SB[n][:, 512 * part:512 * part + w], in0=S_PS[n][part][:, 0:w], scalar1=-SCALE,
-                                    scalar2=None if part == 0 else mn3[:, 4 * c + part - 1:4 * c + part],
+                                    scalar2=mn3[:, 4 * c + part - 1:4 * c + part] if chained and part > 0 else None,
                                     op0=ALU.mult, op1=ALU.min,
-                                    accum_out=nm[:, c:c + 1] if part == 2 else mn3[:, 4 * c + part:4 * c + part + 1])
+                                    accum_out=nm[:, c:c + 1] if chained and part == 2 else mn3[:, 4 * c + part:4 * c + part + 1])
+            if part == 2 and not chained:
+                nc.vector.tensor_reduce(out=nm[:, c:c + 1], in_=mn3[:, 4 * c:4 * c + 3], axis=AX.X, op=ALU.min)
 
         def st3(n):
             h, it = where(n)
@@ -256,7 +259,7 @@ def tile_flashattentionmodule_pa_kernel(tc, x, q, k_new, past_k, past_v, Wv, bv,
 
         def st4p(n):
             words = E_SB[e_tile(n)][:].bitcast(F32)
-            TP_PS[n] = ps_t.tile([P, 4, P], F32, name="tP", tag="tP", bufs=2)
+            TP_PS[n] = ps_t.tile([P, 4, P], F32, name="tP", tag="tr", bufs=3)
             for c in range(4):
                 nc.tensor.transpose(TP_PS[n][:, c, :], words[:, c * P:(c + 1) * P], ident_f[:])
 
@@ -330,16 +333,16 @@ def tile_flashattentionmodule_pa_kernel(tc, x, q, k_new, past_k, past_v, Wv, bv,
         def heads_at(k, task):
             return [hh for hh in range(H) if F.get((task, hh), NT * hh + A[task]) == k]
 
-        prep_qk(0, 0, "v", "tP")
-        prep_qk(0, 1, "s", "tP")
-        x_tr(0, 0, "sd")
+        prep_qk(0, 0, "v", "tr")
+        prep_qk(0, 1, "s", "tr")
+        x_tr(0, 0, "tr")
         for part in range(3):
             st1(0, part)
         x_tr(0, 1, "yo")
         x_ev(0, 0, "s")
         x_ev(0, 1, "s")
         prep_w(0, 0, "s", "tN")
-        prep_w(0, 1, "s", "tP")
+        prep_w(0, 1, "s", "tr")
         for k in range(NTILES + 12):
             h, it = divmod(k, NT)
             if it == 0:
@@ -374,14 +377,14 @@ def tile_flashattentionmodule_pa_kernel(tc, x, q, k_new, past_k, past_v, Wv, bv,
                 if hh < H - 2:
                     finish_c(hh, 0, NT)
             quant_past()
-            for hh in heads_at(k, "quant_va"):
-                quant_v(hh, 0)
+            for hh in heads_at(k, "quant_w"):
+                quant_w(hh)
             if ok(k):
                 st2(k, 1)
             if 1 <= k - 1 < NT:
                 x_ev(k - 1, 1, "v")
-            for hh in heads_at(k, "quant_w"):
-                quant_w(hh)
+            for hh in heads_at(k, "quant_va"):
+                quant_v(hh, 0)
             for hh in heads_at(k, "y_evac"):
                 y_evac(hh)
             for hh in heads_at(k, "quant_vb"):
@@ -433,12 +436,12 @@ def tile_flashattentionmodule_pa_kernel(tc, x, q, k_new, past_k, past_v, Wv, bv,
             if k >= NTILES:
                 mx_passes()
             if 1 <= k < NT:
-                x_tr(k, 0, "tP")
+                x_tr(k, 0, "tr")
                 x_ev(k, 0, "s")
                 x_tr(k, 1, "yo")
             for part in range(2):
                 for hh in heads_at(k, "w%d" % part):
-                    prep_w(hh, part, "s", "sd")
+                    prep_w(hh, part, "s", "tr")
                 for hh in heads_at(k, "qk%d" % part):
                     if hh > 0:
                         prep_qk(hh, part, QE[part])

@@ -377,16 +377,16 @@ def tile_flashattentionmodule_pa_kernel(tc, x, q, k_new, past_k, past_v, Wv, bv,
                 if hh < H - 2:
                     finish_c(hh, 0, NT)
             quant_past()
-            for hh in heads_at(k, "quant_w"):
-                quant_w(hh)
+            for hh in heads_at(k, "y_evac"):
+                y_evac(hh)
             if ok(k):
                 st2(k, 1)
             if 1 <= k - 1 < NT:
                 x_ev(k - 1, 1, "v")
             for hh in heads_at(k, "quant_va"):
                 quant_v(hh, 0)
-            for hh in heads_at(k, "y_evac"):
-                y_evac(hh)
+            for hh in heads_at(k, "quant_w"):
+                quant_w(hh)
             for hh in heads_at(k, "quant_vb"):
                 quant_v(hh, 1)
             for hh in heads_at(k, "recip"):

@@ -8,6 +8,7 @@ F32 = mybir.dt.float32
 BF16 = mybir.dt.bfloat16
 U32 = mybir.dt.uint32
 U8 = mybir.dt.uint8
+I32 = mybir.dt.int32
 FP8X4 = mybir.dt.float8_e4m3fn_x4
 ALU = mybir.AluOpType
 ACTF = mybir.ActivationFunctionType
@@ -26,7 +27,7 @@ LASTPV = 65
 QE = "ss"
 XQ = 2
 A = {"qk0": -4, "qk1": -3, "w0": -2, "w1": -1, "quant_w": 2, "proj0": 4, "proj1": 5, "y_evac": 6, "quant_va": 5, "quant_vb": 7, "pv0": 10, "pv1": 11, "quant_n": 8, "recip": 11, "finish": 12, "v0": 0, "v1": 1, "v2": 2, "v3": 3}
-F = {("w0", 0): -1, ("w1", 0): -1, ("quant_w", 0): 3, ("proj0", 15): 62, ("proj1", 15): 63, ("y_evac", 15): 64, ("quant_va", 15): 64, ("quant_vb", 15): 65, ("pv0", 14): 64, ("pv1", 14): 65, ("recip", 14): 65, ("finish", 14): 66}
+F = {("w0", 0): -1, ("w1", 0): -1, ("quant_w", 0): 3, ("quant_w", 15): 61, ("proj0", 15): 61, ("proj1", 15): 62, ("y_evac", 15): 63, ("quant_va", 15): 64, ("quant_vb", 15): 64, ("pv0", 14): 64, ("pv1", 14): 65, ("recip", 14): 65, ("finish", 14): 66}
 
 
 def tile_flashattentionmodule_pa_kernel(tc, x, q, k_new, past_k, past_v, Wv, bv, out):
@@ -66,11 +67,11 @@ def tile_flashattentionmodule_pa_kernel(tc, x, q, k_new, past_k, past_v, Wv, bv,
         x_sb = const.tile([P, NT, D], BF16, name="x_sb")
 
         def load_x(a):
-            nc.sync.dma_start(out=x_sb[:, a, :], in_=x[0].rearrange("(u p e) k -> u e p k", u=2, e=2)[a // 2, a % 2])
+            nc.sync.dma_start(out=x_sb[:, a, :], in_=x[0].rearrange("(p t) k -> t p k", t=4)[a])
 
         for i in range(2):
             nc.sync.dma_start(out=x_sb[:, 0, i * 1024:(i + 1) * 1024],
-                              in_=x[0].rearrange("(u p e) k -> u e p k", u=2, e=2)[0, 0][:, i * 1024:(i + 1) * 1024])
+                              in_=x[0].rearrange("(p t) k -> t p k", t=4)[0][:, i * 1024:(i + 1) * 1024])
         load_wv(0)
         load_qk(1)
         load_x(1)
@@ -86,12 +87,23 @@ def tile_flashattentionmodule_pa_kernel(tc, x, q, k_new, past_k, past_v, Wv, bv,
         warm = const.tile([P, 2], F32, name="warm")
         nc.vector.memset(warm[:, 0:1], 0.0)
         nc.scalar.activation(out=warm[:, 1:2], in_=warm[:, 0:1], func=ACTF.Exp)
-        E_SB = []
-        for i in range(NT + 1):
-            e_sb = const.tile([P, 1536], BF16, name="e_sb%d" % i, align_bytes=64)
-            if i < NT - 1:
-                nc.vector.memset(e_sb[:, 1024:1536], 0.0)
-            E_SB.append(e_sb)
+        e01 = const.tile([P, 2432], BF16, name="e01", align_bytes=64)
+        e2 = const.tile([P, 1536], BF16, name="e2", align_bytes=64)
+        nc.vector.memset(e2[:, 1408:1536], 0.0)
+        e3 = const.tile([P, 1536], BF16, name="e3", align_bytes=64)
+        e3x = const.tile([P, 1536], BF16, name="e3x", align_bytes=64)
+        VN, V1C, V0C = [], [], []
+        for i in range(3):
+            vn = const.tile([P, 5 * HD], U8, name="vn%d" % i, align_bytes=64)
+            nc.vector.memset(vn[:].bitcast(U32), 0)
+            VN.append(vn)
+        for i in range(2):
+            v1c = const.tile([P, 5 * HD], U8, name="v1c%d" % i, align_bytes=64)
+            nc.vector.memset(v1c[:].bitcast(U32), 0)
+            V1C.append(v1c)
+            v0c = const.tile([P, 5 * HD], U8, name="v0c%d" % i, align_bytes=64)
+            nc.vector.memset(v0c[:].bitcast(U32), 0)
+            V0C.append(v0c)
         ident_bf = const.tile([P, P], BF16, name="ident_bf")
         make_identity(nc, ident_bf[:])
         ident_f = const.tile([P, P], F32, name="ident_f")
@@ -205,17 +217,31 @@ def tile_flashattentionmodule_pa_kernel(tc, x, q, k_new, past_k, past_v, Wv, bv,
 
         def quant_v(h, part):
             if part == 0:
-                VC[h] = hd.tile([P, 3 * HD], U32, name="vc", tag="vc", align_bytes=64, bufs=3)
-                VS[h] = hd.tile([P, 3 * HD], U8, name="vs", tag="vs", align_bytes=64, bufs=3)
-            lo, hi = ((0, 256), (256, 384))[part]
-            nc.vector.quantize_mx(out=VC[h][:, lo:hi].bitcast(FP8X4), scales=VS[h][:, lo:hi], in_=VG[h][:, 4 * lo:4 * hi])
+                VC[h] = hd.tile([P, 2 * HD], U32, name="vc", tag="vc", align_bytes=64, bufs=3)
+                VS[h] = hd.tile([P, 2 * HD], U8, name="vs", tag="vs", align_bytes=64, bufs=3)
+                nc.vector.quantize_mx(out=VC[h][:].bitcast(FP8X4), scales=VS[h][:], in_=VG[h][:, 0:1024])
+            else:
+                vn = VN[h % 3]
+                nc.vector.quantize_mx(out=vn[:, 0:512].bitcast(FP8X4), scales=vn[:, 512:640], in_=VG[h][:, 1024:1536])
+
+        def spread_v(h):
+            nc.sync.dma_start(out=V1C[h % 2][0:64, :].bitcast(I32), in_=VN[h % 3][0:64, :].bitcast(I32))
+            nc.sync.dma_start(out=V0C[h % 2][64:96, :].bitcast(I32), in_=VN[h % 3][0:32, :].bitcast(I32))
 
         def where(n):
             h, j = divmod(n, NT)
             return h, (NT - 1 - j if h == H - 1 else j)
 
-        def e_tile(n):
-            return NT if n == NTILES - NT else where(n)[1]
+        def e_row(n):
+            it = where(n)[1]
+            return e01 if it < 2 else e2 if it == 2 else e3x if n == NTILES - NT else e3
+
+        def e_past(n):
+            it = where(n)[1]
+            return 1408 if it == 0 else 0
+
+        def e_first(n):
+            return 1280 if where(n)[1] == 0 else 0
 
         def widths(it):
             return [512, 512, P * (it + 1)]
@@ -241,8 +267,9 @@ def tile_flashattentionmodule_pa_kernel(tc, x, q, k_new, past_k, past_v, Wv, bv,
             if part == 0:
                 S_SB[n] = tl.tile([P, 1536], F32, name="s_sb", tag="s_sb")
             w = widths(it)[part]
+            o = (P, P + 512, 0)[part] if it == 0 else 512 * part
             chained = n >= 2
-            nc.vector.tensor_scalar(out=S_SB[n][:, 512 * part:512 * part + w], in0=S_PS[n][part][:, 0:w], scalar1=-SCALE,
+            nc.vector.tensor_scalar(out=S_SB[n][:, o:o + w], in0=S_PS[n][part][:, 0:w], scalar1=-SCALE,
                                     scalar2=mn3[:, 4 * c + part - 1:4 * c + part] if chained and part > 0 else None,
                                     op0=ALU.mult, op1=ALU.min,
                                     accum_out=nm[:, c:c + 1] if chained and part == 2 else mn3[:, 4 * c + part:4 * c + part + 1])
@@ -253,22 +280,26 @@ def tile_flashattentionmodule_pa_kernel(tc, x, q, k_new, past_k, past_v, Wv, bv,
             h, it = where(n)
             c = h * NT + it
             b = 9 + it
-            nc.scalar.activation(out=E_SB[e_tile(n)][:, 0:b * P].rearrange("q (b l e) -> q b l e", b=b, e=2),
+            nc.scalar.activation(out=e_row(n)[:, e_first(n):e_first(n) + b * P].rearrange("q (b l e) -> q b l e", b=b, e=2),
                                  in_=S_SB[n][:, 0:b * P].rearrange("q (b e l) -> q b l e", b=b, e=2),
                                  func=ACTF.Exp, bias=nm[:, c:c + 1], scale=-1.0, accum_out=sums[:, c:c + 1])
 
         def st4p(n):
-            words = E_SB[e_tile(n)][:].bitcast(F32)
+            words = e_row(n)[:, e_past(n):e_past(n) + 1024].bitcast(F32)
             TP_PS[n] = ps_t.tile([P, 4, P], F32, name="tP", tag="tr", bufs=3)
             for c in range(4):
                 nc.tensor.transpose(TP_PS[n][:, c, :], words[:, c * P:(c + 1) * P], ident_f[:])
 
         def st4n(n):
-            words = E_SB[e_tile(n)][:].bitcast(F32)
-            if n % 2 == 0:
-                TN_PS[n // 2] = ps_t.tile([P, 2, 2, P], F32, name="tN", tag="tN", bufs=1)
+            h, it = where(n)
+            if it < 2 and n % NT in (0, 2):
+                return
+            j = max(it - 1, 0)
+            if (h, j > 0) not in TN_PS:
+                TN_PS[(h, j > 0)] = ps_t.tile([P, 2, 2, P], F32, name="tN", tag="tN", bufs=1)
+            words = e_row(n)[:, 1024:1536].bitcast(F32)
             for u in range(2):
-                nc.tensor.transpose(TN_PS[n // 2][:, n % 2, u, :], words[:, 512 + u * P:512 + (u + 1) * P], ident_f[:])
+                nc.tensor.transpose(TN_PS[(h, j > 0)][:, max(j - 1, 0), u, :], words[:, u:256:2], ident_f[:])
 
         def st5a(n, e):
             if n % 2 == 0:
@@ -277,11 +308,13 @@ def tile_flashattentionmodule_pa_kernel(tc, x, q, k_new, past_k, past_v, Wv, bv,
             evac(e, words[:, n % 2, :, :, :], TP_PS[n][:].rearrange("p (g u) i -> p g i u", u=2))
 
         def st5b(m, e):
-            h, j = divmod(2 * m, NT)
-            if j == 0:
-                ETN[h] = hd.tile([P, 2048], BF16, name="etn", tag="etn", align_bytes=64)
-            evac(e, ETN[h][:].bitcast(F32).rearrange("p (j i u) -> p j i u", j=NT, u=2)[:, j:j + 2, :, :],
-                 TN_PS[m][:].rearrange("p j u i -> p j i u"))
+            h = m // 2
+            wide = (m % 2 == 1) != (h == H - 1)
+            if m % 2 == 0:
+                ETN[h] = hd.tile([P, 1536], BF16, name="etn", tag="etn", align_bytes=64)
+            lo, hi = (1, 3) if wide else (0, 1)
+            evac(e, ETN[h][:].bitcast(F32).rearrange("p (j i u) -> p j i u", j=3, u=2)[:, lo:hi, :, :],
+                 TN_PS[(h, wide)][:, 0:hi - lo, :, :].rearrange("p j u i -> p j i u"))
 
         def st6n(h, lo, hi):
             o = 1024 + lo * P
@@ -291,8 +324,8 @@ def tile_flashattentionmodule_pa_kernel(tc, x, q, k_new, past_k, past_v, Wv, bv,
         def st6p(m):
             h, j = divmod(2 * m, NT)
             if j == 0:
-                EC[h] = hd.tile([P, NT * 384], U32, name="ec", tag="ec", align_bytes=64, bufs=3)
-                ES[h] = hd.tile([P, NT * 384], U8, name="es", tag="es", align_bytes=64, bufs=3)
+                EC[h] = hd.tile([P, NT * 256 + 384], U32, name="ec", tag="ec", align_bytes=64, bufs=3)
+                ES[h] = hd.tile([P, NT * 256 + 384], U8, name="es", tag="es", align_bytes=64, bufs=3)
             o = j * 256
             nc.vector.quantize_mx(out=EC[h][:, o:o + 512].bitcast(FP8X4), scales=ES[h][:, o:o + 512], in_=ETG[m][:])
 
@@ -305,11 +338,13 @@ def tile_flashattentionmodule_pa_kernel(tc, x, q, k_new, past_k, past_v, Wv, bv,
                 O_PS[h] = ps_o.tile([P, NT, HD], F32, name="o_ps", tag="yo", bufs=1)
             for it in its:
                 j = NT - 1 - it if h == H - 1 else it
+                vn = (V0C[h % 2], V1C[h % 2], VN[h % 3], VN[h % 3])[it]
                 for g in range(3):
-                    o = j * 256 + g * P if g < 2 else 1024 + j * P
+                    o = j * 256 + g * P if g < 2 else 1024 + max(it - 1, 0) * P
                     nc.tensor.matmul_mx(out=O_PS[h][:, it, :],
                                         lhsT=EC[h][:, o:o + P].bitcast(FP8X4), lhsT_scale=ES[h][:, o:o + P],
-                                        rhs=VC[h][:, g * HD:(g + 1) * HD].bitcast(FP8X4), rhs_scale=VS[h][:, g * HD:(g + 1) * HD],
+                                        rhs=(VC[h][:, g * HD:(g + 1) * HD] if g < 2 else vn[:, 0:512]).bitcast(FP8X4),
+                                        rhs_scale=VS[h][:, g * HD:(g + 1) * HD] if g < 2 else vn[:, 512:640],
                                         start=(g == 0), stop=(g == 2))
 
         def finish_b(h, lo, hi):
@@ -345,6 +380,8 @@ def tile_flashattentionmodule_pa_kernel(tc, x, q, k_new, past_k, past_v, Wv, bv,
         prep_w(0, 1, "s", "tr")
         for k in range(NTILES + 12):
             h, it = divmod(k, NT)
+            for hh in heads_at(k - 1, "quant_vb"):
+                spread_v(hh)
             if it == 0:
                 if h + 2 < H:
                     load_qk(h + 2)
@@ -360,11 +397,12 @@ def tile_flashattentionmodule_pa_kernel(tc, x, q, k_new, past_k, past_v, Wv, bv,
             def quant_new():
                 for hh in heads_at(k, "quant_n"):
                     if hh < H - 1:
-                        st6n(hh, 0, NT)
+                        st6n(hh, 0, 1)
+                        st6n(hh, 1, 3)
                 if k == LASTPV:
-                    st6n(H - 1, 0, 2)
+                    st6n(H - 1, 1, 3)
                 if k == LASTPV + 1:
-                    st6n(H - 1, 2, NT)
+                    st6n(H - 1, 0, 1)
 
             done = [hh for hh in heads_at(k, "finish") if hh < H - 1]
             if k == LASTPV:

@@ -462,8 +462,6 @@ def tile_flashattentionmodule_pa_kernel(tc, x, q, k_new, past_k, past_v, Wv, bv,
 
             if k < NTILES:
                 mx_passes()
-            if ok(k + 1):
-                st1(k + 1, 2)
             if ok(k - 1):
                 st4p(k - 1)
                 st5a(k - 1, "s")
@@ -483,3 +481,5 @@ def tile_flashattentionmodule_pa_kernel(tc, x, q, k_new, past_k, past_v, Wv, bv,
                 for hh in heads_at(k, "qk%d" % part):
                     if hh > 0:
                         prep_qk(hh, part, QE[part])
+            if ok(k + 1):
+                st1(k + 1, 2)

@@ -26,8 +26,8 @@ LAG = 4
 LASTPV = 65
 QE = "ss"
 XQ = 2
-A = {"qk0": -4, "qk1": -3, "w0": -2, "w1": -1, "quant_w": 2, "proj0": 4, "proj1": 5, "y_evac": 6, "quant_va": 5, "quant_vb": 7, "pv0": 10, "pv1": 11, "quant_n": 8, "recip": 11, "finish": 12, "v0": 0, "v1": 1, "v2": 2, "v3": 3}
-F = {("w0", 0): -1, ("w1", 0): -1, ("quant_w", 0): 3, ("quant_w", 15): 61, ("proj0", 15): 61, ("proj1", 15): 62, ("y_evac", 15): 63, ("quant_va", 15): 64, ("quant_vb", 15): 64, ("pv0", 14): 64, ("pv1", 14): 65, ("recip", 14): 65, ("finish", 14): 66}
+A = {"qk0": -4, "qk1": -3, "w0": -2, "w1": -1, "quant_w": 2, "proj0": 4, "proj1": 5, "y_evac": 6, "quant_va": 5, "quant_vb": 7, "pv0": 10, "pv1": 11, "quant_n": 8, "quant_t1": 4, "recip": 11, "finish": 12, "v0": 0, "v1": 1, "v2": 2, "v3": 3}
+F = {("w0", 0): -1, ("w1", 0): -1, ("quant_w", 0): 3, ("quant_w", 15): 61, ("proj0", 15): 61, ("proj1", 15): 62, ("y_evac", 15): 63, ("quant_va", 15): 64, ("quant_vb", 15): 64, ("pv0", 14): 64, ("pv1", 14): 65, ("recip", 14): 65, ("finish", 14): 66, ("quant_n", 15): 65, ("quant_t1", 15): 65}
 
 
 def tile_flashattentionmodule_pa_kernel(tc, x, q, k_new, past_k, past_v, Wv, bv, out):
@@ -46,6 +46,7 @@ def tile_flashattentionmodule_pa_kernel(tc, x, q, k_new, past_k, past_v, Wv, bv,
         Q_SB, KN_SB, PK_SB, PV_SB, W_SB = {}, {}, {}, {}, {}
         QKT, WG, WC, WS, VG, VC, VS, EC, ES, Y_PS = {}, {}, {}, {}, {}, {}, {}, {}, {}, {}
         S_PS, S_SB, TP_PS, TN_PS, ETG, ETN = {}, {}, {}, {}, {}, {}
+        ET1, C1, S1 = {}, {}, {}
 
         def load_qk(h):
             Q_SB[h] = ld.tile([P, NT, HD], BF16, name="q_sb", tag="q_sb")
@@ -87,23 +88,16 @@ def tile_flashattentionmodule_pa_kernel(tc, x, q, k_new, past_k, past_v, Wv, bv,
         warm = const.tile([P, 2], F32, name="warm")
         nc.vector.memset(warm[:, 0:1], 0.0)
         nc.scalar.activation(out=warm[:, 1:2], in_=warm[:, 0:1], func=ACTF.Exp)
-        e01 = const.tile([P, 2432], BF16, name="e01", align_bytes=64)
-        e2 = const.tile([P, 1536], BF16, name="e2", align_bytes=64)
-        nc.vector.memset(e2[:, 1408:1536], 0.0)
+        EB = [const.tile([P, 2560], BF16, name="eb%d" % i, align_bytes=64) for i in range(2)]
+        ec1 = const.tile([P, 2560], BF16, name="ec1", align_bytes=64)
         e3 = const.tile([P, 1536], BF16, name="e3", align_bytes=64)
         e3x = const.tile([P, 1536], BF16, name="e3x", align_bytes=64)
-        VN, V1C, V0C = [], [], []
-        for i in range(3):
-            vn = const.tile([P, 5 * HD], U8, name="vn%d" % i, align_bytes=64)
-            nc.vector.memset(vn[:].bitcast(U32), 0)
-            VN.append(vn)
-        for i in range(2):
-            v1c = const.tile([P, 5 * HD], U8, name="v1c%d" % i, align_bytes=64)
-            nc.vector.memset(v1c[:].bitcast(U32), 0)
-            V1C.append(v1c)
-            v0c = const.tile([P, 5 * HD], U8, name="v0c%d" % i, align_bytes=64)
-            nc.vector.memset(v0c[:].bitcast(U32), 0)
-            V0C.append(v0c)
+        VN, V2, V0, V1 = [], [], [], []
+        for name, lst, cnt in (("vn", VN, 3), ("v2_", V2, 2), ("v0_", V0, 2), ("v1_", V1, 2)):
+            for i in range(cnt):
+                vt = const.tile([P, 5 * HD], U8, name=name + str(i), align_bytes=64)
+                nc.vector.memset(vt[:].bitcast(U32), 0)
+                lst.append(vt)
         ident_bf = const.tile([P, P], BF16, name="ident_bf")
         make_identity(nc, ident_bf[:])
         ident_f = const.tile([P, P], F32, name="ident_f")
@@ -225,23 +219,29 @@ def tile_flashattentionmodule_pa_kernel(tc, x, q, k_new, past_k, past_v, Wv, bv,
                 nc.vector.quantize_mx(out=vn[:, 0:512].bitcast(FP8X4), scales=vn[:, 512:640], in_=VG[h][:, 1024:1536])
 
         def spread_v(h):
-            nc.sync.dma_start(out=V1C[h % 2][0:64, :].bitcast(I32), in_=VN[h % 3][0:64, :].bitcast(I32))
-            nc.sync.dma_start(out=V0C[h % 2][64:96, :].bitcast(I32), in_=VN[h % 3][0:32, :].bitcast(I32))
+            r = 64 * (h % 2)
+            vn = VN[h % 3]
+            nc.sync.dma_start(out=V1[h % 2][r:r + 64, :].bitcast(I32), in_=vn[0:64, :].bitcast(I32))
+            nc.sync.dma_start(out=V0[h % 2][96:128, :].bitcast(I32), in_=vn[0:32, :].bitcast(I32))
+            nc.sync.dma_start(out=V2[h % 2][0:96, :].bitcast(I32), in_=vn[0:96, :].bitcast(I32))
 
         def where(n):
             h, j = divmod(n, NT)
-            return h, (NT - 1 - j if h == H - 1 else j)
+            return h, ((3, 2, 0, 1)[j] if h == H - 1 else j)
+
+        def flipped(n):
+            h, it = where(n)
+            return it == 0 or it == 1 and h % 2 == 1
 
         def e_row(n):
-            it = where(n)[1]
-            return e01 if it < 2 else e2 if it == 2 else e3x if n == NTILES - NT else e3
-
-        def e_past(n):
-            it = where(n)[1]
-            return 1408 if it == 0 else 0
+            h, it = where(n)
+            return ec1 if it == 1 else EB[h % 2] if it % 2 == 0 else e3x if n == NTILES - NT else e3
 
         def e_first(n):
-            return 1280 if where(n)[1] == 0 else 0
+            return 0 if not flipped(n) else 1408 if where(n)[1] == 0 else 1280
+
+        def e_past(n):
+            return 1536 if flipped(n) else 0
 
         def widths(it):
             return [512, 512, P * (it + 1)]
@@ -267,7 +267,8 @@ def tile_flashattentionmodule_pa_kernel(tc, x, q, k_new, past_k, past_v, Wv, bv,
             if part == 0:
                 S_SB[n] = tl.tile([P, 1536], F32, name="s_sb", tag="s_sb")
             w = widths(it)[part]
-            o = (P, P + 512, 0)[part] if it == 0 else 512 * part
+            nw = P * (it + 1)
+            o = (nw, nw + 512, 0)[part] if flipped(n) else 512 * part
             chained = n >= 2
             nc.vector.tensor_scalar(out=S_SB[n][:, o:o + w], in0=S_PS[n][part][:, 0:w], scalar1=-SCALE,
                                     scalar2=mn3[:, 4 * c + part - 1:4 * c + part] if chained and part > 0 else None,
@@ -290,11 +291,19 @@ def tile_flashattentionmodule_pa_kernel(tc, x, q, k_new, past_k, past_v, Wv, bv,
             for c in range(4):
                 nc.tensor.transpose(TP_PS[n][:, c, :], words[:, c * P:(c + 1) * P], ident_f[:])
 
+        def new_op(n):
+            h, it = where(n)
+            if it == 3:
+                return 2
+            if it == 1:
+                return 0 if h % 2 == 1 else None
+            return 1 if it == (0 if h == H - 1 else 2) else None
+
         def st4n(n):
             h, it = where(n)
-            if it < 2 and n % NT in (0, 2):
+            j = new_op(n)
+            if j is None:
                 return
-            j = max(it - 1, 0)
             if (h, j > 0) not in TN_PS:
                 TN_PS[(h, j > 0)] = ps_t.tile([P, 2, 2, P], F32, name="tN", tag="tN", bufs=1)
             words = e_row(n)[:, 1024:1536].bitcast(F32)
@@ -307,29 +316,32 @@ def tile_flashattentionmodule_pa_kernel(tc, x, q, k_new, past_k, past_v, Wv, bv,
             words = ETG[n // 2][:].bitcast(F32).rearrange("p (j g i u) -> p j g i u", j=2, g=2, u=2)
             evac(e, words[:, n % 2, :, :, :], TP_PS[n][:].rearrange("p (g u) i -> p g i u", u=2))
 
-        def st5b(m, e):
-            h = m // 2
-            wide = (m % 2 == 1) != (h == H - 1)
-            if m % 2 == 0:
-                ETN[h] = hd.tile([P, 1536], BF16, name="etn", tag="etn", align_bytes=64)
-            lo, hi = (1, 3) if wide else (0, 1)
-            evac(e, ETN[h][:].bitcast(F32).rearrange("p (j i u) -> p j i u", j=3, u=2)[:, lo:hi, :, :],
-                 TN_PS[(h, wide)][:, 0:hi - lo, :, :].rearrange("p j u i -> p j i u"))
+        def st5n(h, wide, e):
+            if wide:
+                ETN[h] = hd.tile([P, 1024], BF16, name="etn", tag="etn", align_bytes=64)
+                evac(e, ETN[h][:].bitcast(F32).rearrange("p (j i u) -> p j i u", j=2, u=2), TN_PS[(h, True)][:].rearrange("p j u i -> p j i u"))
+            else:
+                ET1[h // 2] = hd.tile([P, 512], BF16, name="et1", tag="et1", align_bytes=64)
+                evac(e, ET1[h // 2][:].bitcast(F32).rearrange("p (i u) -> p i u", u=2), TN_PS[(h, False)][:, 0, :, :].rearrange("p u i -> p i u"))
 
-        def st6n(h, lo, hi):
-            o = 1024 + lo * P
-            e = 1024 + hi * P
-            nc.vector.quantize_mx(out=EC[h][:, o:e].bitcast(FP8X4), scales=ES[h][:, o:e], in_=ETN[h][:, lo * 512:hi * 512])
+        def st6n(h):
+            nc.vector.quantize_mx(out=EC[h][:, 1024:1280].bitcast(FP8X4), scales=ES[h][:, 1024:1280], in_=ETN[h][:])
+
+        def st6t1(m):
+            C1[m] = hd.tile([P, P], U32, name="c1", tag="c1", align_bytes=64)
+            S1[m] = hd.tile([P, P], U8, name="s1", tag="s1", align_bytes=64)
+            nc.vector.quantize_mx(out=C1[m][:].bitcast(FP8X4), scales=S1[m][:], in_=ET1[m][:])
 
         def st6p(m):
             h, j = divmod(2 * m, NT)
             if j == 0:
-                EC[h] = hd.tile([P, NT * 256 + 384], U32, name="ec", tag="ec", align_bytes=64, bufs=3)
-                ES[h] = hd.tile([P, NT * 256 + 384], U8, name="es", tag="es", align_bytes=64, bufs=3)
+                EC[h] = hd.tile([P, NT * 256 + 256], U32, name="ec", tag="ec", align_bytes=64, bufs=3)
+                ES[h] = hd.tile([P, NT * 256 + 256], U8, name="es", tag="es", align_bytes=64, bufs=3)
             o = j * 256
             nc.vector.quantize_mx(out=EC[h][:, o:o + 512].bitcast(FP8X4), scales=ES[h][:, o:o + 512], in_=ETG[m][:])
 
         O_PS = {}
+        SLOT = {h: {where(h * NT + j)[1]: j for j in range(NT)} for h in range(H)}
 
         def pv(h, its, first):
             if h == H - 1:
@@ -337,12 +349,15 @@ def tile_flashattentionmodule_pa_kernel(tc, x, q, k_new, past_k, past_v, Wv, bv,
             elif first:
                 O_PS[h] = ps_o.tile([P, NT, HD], F32, name="o_ps", tag="yo", bufs=1)
             for it in its:
-                j = NT - 1 - it if h == H - 1 else it
-                vn = (V0C[h % 2], V1C[h % 2], VN[h % 3], VN[h % 3])[it]
+                j = SLOT[h][it]
+                vn = (V0[h % 2], V1[h % 2], V2[h % 2], VN[h % 3])[it]
                 for g in range(3):
-                    o = j * 256 + g * P if g < 2 else 1024 + max(it - 1, 0) * P
+                    ec, es = EC[h], ES[h]
+                    o = j * 256 + g * P if g < 2 else 1024 + (it == 3) * P
+                    if g == 2 and it == 1:
+                        ec, es, o = C1[h // 2], S1[h // 2], 0
                     nc.tensor.matmul_mx(out=O_PS[h][:, it, :],
-                                        lhsT=EC[h][:, o:o + P].bitcast(FP8X4), lhsT_scale=ES[h][:, o:o + P],
+                                        lhsT=ec[:, o:o + P].bitcast(FP8X4), lhsT_scale=es[:, o:o + P],
                                         rhs=(VC[h][:, g * HD:(g + 1) * HD] if g < 2 else vn[:, 0:512]).bitcast(FP8X4),
                                         rhs_scale=VS[h][:, g * HD:(g + 1) * HD] if g < 2 else vn[:, 512:640],
                                         start=(g == 0), stop=(g == 2))
@@ -396,13 +411,10 @@ def tile_flashattentionmodule_pa_kernel(tc, x, q, k_new, past_k, past_v, Wv, bv,
 
             def quant_new():
                 for hh in heads_at(k, "quant_n"):
-                    if hh < H - 1:
-                        st6n(hh, 0, 1)
-                        st6n(hh, 1, 3)
-                if k == LASTPV:
-                    st6n(H - 1, 1, 3)
-                if k == LASTPV + 1:
-                    st6n(H - 1, 0, 1)
+                    st6n(hh)
+                for hh in heads_at(k, "quant_t1"):
+                    if hh % 2 == 1:
+                        st6t1(hh // 2)
 
             done = [hh for hh in heads_at(k, "finish") if hh < H - 1]
             if k == LASTPV:
@@ -452,11 +464,12 @@ def tile_flashattentionmodule_pa_kernel(tc, x, q, k_new, past_k, past_v, Wv, bv,
                 if k == LASTPV:
                     pv(H - 1, [3, 2], True)
                 if k == LASTPV + 1:
-                    pv(H - 1, [1, 0], False)
+                    pv(H - 1, [0, 1], False)
                 for half in range(2):
                     for hh in heads_at(k, "pv%d" % half):
                         if hh < H - 1:
-                            pv(hh, [2 * half, 2 * half + 1], half == 0)
+                            lo = 2 * (1 - half if hh == H - 2 else half)
+                            pv(hh, [lo, lo + 1], half == 0)
                     for hh in heads_at(k, "proj%d" % half):
                         proj(hh, half)
 
@@ -467,8 +480,11 @@ def tile_flashattentionmodule_pa_kernel(tc, x, q, k_new, past_k, past_v, Wv, bv,
                 st5a(k - 1, "s")
             if ok(k - 1):
                 st4n(k - 1)
-                if (k - 1) % 2 == 1:
-                    st5b((k - 1) // 2, "s")
+                h1, it1 = where(k - 1)
+                if new_op(k - 1) == 0:
+                    st5n(h1, False, "s")
+                elif it1 == (0 if h1 == H - 1 else 3):
+                    st5n(h1, True, "s")
             if k >= NTILES:
                 mx_passes()
             if 1 <= k < NT:

@@ -27,7 +27,7 @@ LASTPV = 65
 QE = "ss"
 XQ = 2
 A = {"qk0": -4, "qk1": -3, "w0": -2, "w1": -1, "quant_w": 2, "proj0": 4, "proj1": 5, "y_evac": 6, "quant_va": 5, "quant_vb": 7, "pv0": 10, "pv1": 11, "quant_n": 8, "quant_t1": 4, "recip": 11, "finish": 12, "v0": 0, "v1": 1, "v2": 2, "v3": 3}
-F = {("w0", 0): -1, ("w1", 0): -1, ("quant_w", 0): 3, ("quant_w", 15): 61, ("proj0", 15): 61, ("proj1", 15): 62, ("y_evac", 15): 63, ("quant_va", 15): 64, ("quant_vb", 15): 64, ("pv0", 14): 64, ("pv1", 14): 65, ("recip", 14): 65, ("finish", 14): 66, ("quant_n", 15): 65, ("quant_t1", 15): 65}
+F = {("v0", 0): 2, ("v1", 0): 2, ("w0", 0): 0, ("w1", 0): 0, ("quant_w", 0): 3, ("quant_w", 15): 61, ("proj0", 15): 61, ("proj1", 15): 62, ("y_evac", 15): -9, ("quant_va", 15): 64, ("quant_vb", 15): 63, ("pv0", 14): 64, ("pv1", 14): 64, ("recip", 14): 64, ("finish", 14): 66, ("quant_t1", 15): 63}
 
 
 def tile_flashattentionmodule_pa_kernel(tc, x, q, k_new, past_k, past_v, Wv, bv, out):
@@ -91,7 +91,6 @@ def tile_flashattentionmodule_pa_kernel(tc, x, q, k_new, past_k, past_v, Wv, bv,
         EB = [const.tile([P, 2560], BF16, name="eb%d" % i, align_bytes=64) for i in range(2)]
         ec1 = const.tile([P, 2560], BF16, name="ec1", align_bytes=64)
         e3 = const.tile([P, 1536], BF16, name="e3", align_bytes=64)
-        e3x = const.tile([P, 1536], BF16, name="e3x", align_bytes=64)
         VN, V2, V0, V1 = [], [], [], []
         for name, lst, cnt in (("vn", VN, 3), ("v2_", V2, 2), ("v0_", V0, 2), ("v1_", V1, 2)):
             for i in range(cnt):
@@ -110,6 +109,7 @@ def tile_flashattentionmodule_pa_kernel(tc, x, q, k_new, past_k, past_v, Wv, bv,
         nc.vector.tensor_copy(out=mask_bf[:].rearrange("i (e w) -> i e w", e=2), in_=mask_f[:].rearrange("i (w e) -> i e w", e=2))
         mn3 = const.tile([P, NTILES * 4], F32, name="mn3")
         nm = const.tile([P, NTILES], F32, name="nm")
+        nm_g = const.tile([P, 2], F32, name="nm_g")
         sums = const.tile([P, NTILES], F32, name="sums")
         rinv = const.tile([P, NTILES], F32, name="rinv")
         xg = const.tile([P, 4 * S * 4], BF16, name="xg", align_bytes=64)
@@ -141,21 +141,26 @@ def tile_flashattentionmodule_pa_kernel(tc, x, q, k_new, past_k, past_v, Wv, bv,
                                   scales=x_scales[:, a * 512:(a + 1) * 512],
                                   in_=xg[:, a * 2048:(a + 1) * 2048])
 
-        def prep_qk(h, part, e, tg="tr"):
-            if part == 0:
+        TQ = {}
+
+        def qk_tr(h, j0, n, tg):
+            if j0 == 0:
                 QKT[h] = hd.tile([P, 16 * P], BF16, name="qkT", tag="qkT", bufs=3)
-            tq = ps_t.tile([P, 8, P], BF16, name="tq", tag=tg, bufs=TBUFS[tg])
-            for j in range(8):
-                if part == 0:
-                    src = Q_SB[h][:, j, :] if j < 4 else KN_SB[h][:, j - 4, :]
-                else:
-                    src = PK_SB[h][:, j, :]
+            tq = (ps_o if tg == "yo" else ps_t).tile([P, n, P], BF16, name="tq", tag=tg, bufs=TBUFS[tg])
+            for j in range(n):
                 dst = tq[:, j, :]
-                if part == 1 or j >= 4:
+                i = j0 + j
+                if i < 4:
+                    src = Q_SB[h][:, i, :]
+                else:
+                    src = KN_SB[h][:, i - 4, :] if i < 8 else PK_SB[h][:, i - 8, :]
                     b, par = divmod(j, 2)
-                    dst = tq[:].rearrange("d j i -> d (j i)").rearrange("d (b h e l) -> d b h e l", b=4, h=2, e=2)[:, b, :, par, :]
+                    dst = tq[:].rearrange("d j i -> d (j i)").rearrange("d (b h e l) -> d b h e l", b=n // 2, h=2, e=2)[:, b, :, par, :]
                 nc.tensor.transpose(dst, src, ident_bf[:])
-            evac(e, QKT[h][:, part * 1024:(part + 1) * 1024], tq[:].rearrange("p j i -> p (j i)"))
+            TQ[(h, j0)] = tq
+
+        def qk_ev(h, j0, n, e):
+            evac(e, QKT[h][:, j0 * P:(j0 + n) * P], TQ[(h, j0)][:].rearrange("p j i -> p (j i)"))
 
         TW = {}
 
@@ -227,7 +232,7 @@ def tile_flashattentionmodule_pa_kernel(tc, x, q, k_new, past_k, past_v, Wv, bv,
 
         def where(n):
             h, j = divmod(n, NT)
-            return h, ((3, 2, 0, 1)[j] if h == H - 1 else j)
+            return h, ((1, 3, 2, 0)[j] if h == H - 1 else j)
 
         def flipped(n):
             h, it = where(n)
@@ -235,7 +240,7 @@ def tile_flashattentionmodule_pa_kernel(tc, x, q, k_new, past_k, past_v, Wv, bv,
 
         def e_row(n):
             h, it = where(n)
-            return ec1 if it == 1 else EB[h % 2] if it % 2 == 0 else e3x if n == NTILES - NT else e3
+            return ec1 if it == 1 else EB[h % 2] if it % 2 == 0 else e3
 
         def e_first(n):
             return 0 if not flipped(n) else 1408 if where(n)[1] == 0 else 1280
@@ -275,7 +280,8 @@ def tile_flashattentionmodule_pa_kernel(tc, x, q, k_new, past_k, past_v, Wv, bv,
                                     op0=ALU.mult, op1=ALU.min,
                                     accum_out=nm[:, c:c + 1] if chained and part == 2 else mn3[:, 4 * c + part:4 * c + part + 1])
             if part == 2 and not chained:
-                nc.vector.tensor_reduce(out=nm[:, c:c + 1], in_=mn3[:, 4 * c:4 * c + 3], axis=AX.X, op=ALU.min)
+                nc.gpsimd.tensor_scalar(out=nm_g[:, n:n + 1], in0=mn3[:, 4 * c:4 * c + 1], scalar1=mn3[:, 4 * c + 1:4 * c + 2],
+                                        scalar2=mn3[:, 4 * c + 2:4 * c + 3], op0=ALU.min, op1=ALU.min)
 
         def st3(n):
             h, it = where(n)
@@ -283,7 +289,7 @@ def tile_flashattentionmodule_pa_kernel(tc, x, q, k_new, past_k, past_v, Wv, bv,
             b = 9 + it
             nc.scalar.activation(out=e_row(n)[:, e_first(n):e_first(n) + b * P].rearrange("q (b l e) -> q b l e", b=b, e=2),
                                  in_=S_SB[n][:, 0:b * P].rearrange("q (b e l) -> q b l e", b=b, e=2),
-                                 func=ACTF.Exp, bias=nm[:, c:c + 1], scale=-1.0, accum_out=sums[:, c:c + 1])
+                                 func=ACTF.Exp, bias=nm_g[:, n:n + 1] if n < 2 else nm[:, c:c + 1], scale=-1.0, accum_out=sums[:, c:c + 1])
 
         def st4p(n):
             words = e_row(n)[:, e_past(n):e_past(n) + 1024].bitcast(F32)
@@ -316,16 +322,22 @@ def tile_flashattentionmodule_pa_kernel(tc, x, q, k_new, past_k, past_v, Wv, bv,
             words = ETG[n // 2][:].bitcast(F32).rearrange("p (j g i u) -> p j g i u", j=2, g=2, u=2)
             evac(e, words[:, n % 2, :, :, :], TP_PS[n][:].rearrange("p (g u) i -> p g i u", u=2))
 
-        def st5n(h, wide, e):
-            if wide:
-                ETN[h] = hd.tile([P, 1024], BF16, name="etn", tag="etn", align_bytes=64)
-                evac(e, ETN[h][:].bitcast(F32).rearrange("p (j i u) -> p j i u", j=2, u=2), TN_PS[(h, True)][:].rearrange("p j u i -> p j i u"))
-            else:
+        def st5n(n, e):
+            h, it = where(n)
+            j = new_op(n)
+            if j == 0:
                 ET1[h // 2] = hd.tile([P, 512], BF16, name="et1", tag="et1", align_bytes=64)
                 evac(e, ET1[h // 2][:].bitcast(F32).rearrange("p (i u) -> p i u", u=2), TN_PS[(h, False)][:, 0, :, :].rearrange("p u i -> p i u"))
+                return
+            if h not in ETN:
+                ETN[h] = hd.tile([P, 1024], BF16, name="etn", tag="etn", align_bytes=64)
+            for lo, hi in ([(j - 1, j)] if j and h == H - 1 else [(0, 2)] if j == 2 else []):
+                evac(e, ETN[h][:, 512 * lo:512 * hi].bitcast(F32).rearrange("p (j i u) -> p j i u", j=hi - lo, u=2),
+                     TN_PS[(h, True)][:, lo:hi, :, :].rearrange("p j u i -> p j i u"))
 
-        def st6n(h):
-            nc.vector.quantize_mx(out=EC[h][:, 1024:1280].bitcast(FP8X4), scales=ES[h][:, 1024:1280], in_=ETN[h][:])
+        def st6n(h, lo, hi):
+            o, e = 1024 + P * lo, 1024 + P * hi
+            nc.vector.quantize_mx(out=EC[h][:, o:e].bitcast(FP8X4), scales=ES[h][:, o:e], in_=ETN[h][:, 512 * lo:512 * hi])
 
         def st6t1(m):
             C1[m] = hd.tile([P, P], U32, name="c1", tag="c1", align_bytes=64)
@@ -366,16 +378,17 @@ def tile_flashattentionmodule_pa_kernel(tc, x, q, k_new, past_k, past_v, Wv, bv,
             c = h * NT
             nc.vector.reciprocal(out=rinv[:, c + lo:c + hi], in_=sums[:, c + lo:c + hi])
 
-        def finish_c(h, lo, hi, e="v"):
+        def finish_c(h, its, e="v"):
             c = h * NT
             o_sb = hd.tile([P, NT, HD], F32, name="o_sb", tag="o_sb", bufs=4)
+            n = len(range(NT)[its])
             if e == "v":
-                nc.vector.tensor_tensor(out=o_sb[:, lo:hi, :], in0=O_PS[h][:, lo:hi, :],
-                                        in1=rinv[:, c + lo:c + hi].unsqueeze(2).to_broadcast([P, hi - lo, HD]), op=ALU.mult)
+                nc.vector.tensor_tensor(out=o_sb[:, its, :], in0=O_PS[h][:, its, :],
+                                        in1=rinv[:, c:c + NT][:, its].unsqueeze(2).to_broadcast([P, n, HD]), op=ALU.mult)
             else:
-                for it in range(lo, hi):
+                for it in range(NT):
                     nc.scalar.activation(out=o_sb[:, it, :], in_=O_PS[h][:, it, :], func=ACTF.Copy, scale=rinv[:, c + it:c + it + 1])
-            nc.sync.dma_start(out=out[0].rearrange("(a p) c -> p a c", p=P)[:, lo:hi, h * HD:(h + 1) * HD], in_=o_sb[:, lo:hi, :])
+            nc.sync.dma_start(out=out[0].rearrange("(a p) c -> p a c", p=P)[:, its, h * HD:(h + 1) * HD], in_=o_sb[:, its, :])
 
         def ok(n):
             return 0 <= n < NTILES
@@ -383,16 +396,16 @@ def tile_flashattentionmodule_pa_kernel(tc, x, q, k_new, past_k, past_v, Wv, bv,
         def heads_at(k, task):
             return [hh for hh in range(H) if F.get((task, hh), NT * hh + A[task]) == k]
 
-        prep_qk(0, 0, "v", "tr")
-        prep_qk(0, 1, "s", "tr")
-        x_tr(0, 0, "tr")
-        for part in range(3):
-            st1(0, part)
-        x_tr(0, 1, "yo")
+        for j0, tg, e in ((0, "tr", "s"), (4, "tr", "v"), (8, "tr", "v"), (12, "yo", "s")):
+            qk_tr(0, j0, 4, tg)
+            qk_ev(0, j0, 4, e)
+        x_tr(0, 0, "tN")
+        st1(0, 0)
+        st1(0, 1)
         x_ev(0, 0, "s")
+        x_tr(0, 1, "yo")
         x_ev(0, 1, "s")
-        prep_w(0, 0, "s", "tN")
-        prep_w(0, 1, "s", "tr")
+        st1(0, 2)
         for k in range(NTILES + 12):
             h, it = divmod(k, NT)
             for hh in heads_at(k - 1, "quant_vb"):
@@ -411,81 +424,99 @@ def tile_flashattentionmodule_pa_kernel(tc, x, q, k_new, past_k, past_v, Wv, bv,
 
             def quant_new():
                 for hh in heads_at(k, "quant_n"):
-                    st6n(hh)
+                    if hh < H - 1:
+                        st6n(hh, 0, 2)
+                if k == LASTPV:
+                    st6n(H - 1, 1, 2)
+                if k == LASTPV + 1:
+                    st6n(H - 1, 0, 1)
                 for hh in heads_at(k, "quant_t1"):
                     if hh % 2 == 1:
                         st6t1(hh // 2)
 
-            done = [hh for hh in heads_at(k, "finish") if hh < H - 1]
-            if k == LASTPV:
-                finish_b(H - 1, 0, NT)
-            if ok(k):
+            def fill_a():
+                for hh in heads_at(k, "finish"):
+                    if hh < H - 2:
+                        finish_c(hh, slice(0, NT))
+                quant_past()
+                for hh in heads_at(k, "quant_w"):
+                    quant_w(hh)
+
+            def fill_b():
+                for hh in heads_at(k, "quant_va"):
+                    quant_v(hh, 0)
+                for hh in heads_at(k, "y_evac"):
+                    y_evac(hh)
+                for hh in heads_at(k, "quant_vb"):
+                    if hh < H - 2:
+                        quant_v(hh, 1)
+                for hh in heads_at(k, "recip"):
+                    if hh < H - 1:
+                        finish_b(hh, 0, NT)
+                quant_new()
+
+            if k < NTILES - 1:
                 st2(k, 0)
-            if 0 <= k - XQ < NT:
-                x_quant(k - XQ)
-            for hh in done:
-                if hh < H - 2:
-                    finish_c(hh, 0, NT)
-            quant_past()
-            for hh in heads_at(k, "y_evac"):
-                y_evac(hh)
-            if ok(k):
+                if 0 <= k - XQ < NT:
+                    x_quant(k - XQ)
+                fill_a()
                 st2(k, 1)
-            if 1 <= k - 1 < NT:
-                x_ev(k - 1, 1, "v")
-            for hh in heads_at(k, "quant_va"):
-                quant_v(hh, 0)
-            for hh in heads_at(k, "quant_w"):
-                quant_w(hh)
-            for hh in heads_at(k, "quant_vb"):
-                quant_v(hh, 1)
-            for hh in heads_at(k, "recip"):
-                if hh < H - 1:
-                    finish_b(hh, 0, NT)
-            quant_new()
+                if 1 <= k - 1 < NT:
+                    x_ev(k - 1, 1, "v")
+                fill_b()
+                st2(k, 2)
+            elif k == NTILES - 1:
+                st2(k, 0)
+                quant_v(H - 2, 1)
+                y_evac(H - 1)
+                st2(k, 1)
+                quant_v(H - 1, 1)
+                st2(k, 2)
+                fill_a()
+                fill_b()
+            else:
+                if k == LASTPV:
+                    finish_b(H - 1, 0, NT)
+                fill_a()
+                fill_b()
+                if k == LASTPV + 1:
+                    finish_c(H - 1, slice(1, NT, 2))
+                if k == LASTPV + 2:
+                    finish_c(H - 1, slice(0, NT, 2))
             for piece in range(4):
                 for hh in heads_at(k, "v%d" % piece):
                     regroup_v(hh, piece)
-            if ok(k):
-                st2(k, 2)
-            if k == LASTPV + 1:
-                finish_c(H - 1, 2, 4)
-            if k == LASTPV + 2:
-                finish_c(H - 1, 0, 2)
             if ok(k + 1):
                 st1(k + 1, 0)
-            if ok(k + 1):
                 st1(k + 1, 1)
-            if ok(k):
+                if k == 0:
+                    st1(k + 1, 2)
+            if k < NTILES - 1:
                 st3(k)
+
             def mx_passes():
-                if k == LASTPV + 1:
-                    finish_c(H - 2, 0, NT, "s")
                 if k == LASTPV:
-                    pv(H - 1, [3, 2], True)
+                    finish_c(H - 2, slice(0, NT), "s")
+                    pv(H - 1, [1, 3], True)
                 if k == LASTPV + 1:
-                    pv(H - 1, [0, 1], False)
+                    pv(H - 1, [2, 0], False)
                 for half in range(2):
                     for hh in heads_at(k, "pv%d" % half):
                         if hh < H - 1:
-                            lo = 2 * (1 - half if hh == H - 2 else half)
-                            pv(hh, [lo, lo + 1], half == 0)
+                            pv(hh, [2 * half, 2 * half + 1], half == 0)
                     for hh in heads_at(k, "proj%d" % half):
                         proj(hh, half)
 
-            if k < NTILES:
+            if k < NTILES - 1:
                 mx_passes()
             if ok(k - 1):
                 st4p(k - 1)
                 st5a(k - 1, "s")
-            if ok(k - 1):
+                if k == NTILES - 1:
+                    st3(k)
                 st4n(k - 1)
-                h1, it1 = where(k - 1)
-                if new_op(k - 1) == 0:
-                    st5n(h1, False, "s")
-                elif it1 == (0 if h1 == H - 1 else 3):
-                    st5n(h1, True, "s")
-            if k >= NTILES:
+                st5n(k - 1, "s")
+            if k >= NTILES - 1:
                 mx_passes()
             if 1 <= k < NT:
                 x_tr(k, 0, "tr")
@@ -496,6 +527,7 @@ def tile_flashattentionmodule_pa_kernel(tc, x, q, k_new, past_k, past_v, Wv, bv,
                     prep_w(hh, part, "s", "tr")
                 for hh in heads_at(k, "qk%d" % part):
                     if hh > 0:
-                        prep_qk(hh, part, QE[part])
-            if ok(k + 1):
+                        qk_tr(hh, 8 * part, 8, "tr")
+                        qk_ev(hh, 8 * part, 8, "s")
+            if ok(k + 1) and k > 0:
                 st1(k + 1, 2)

@@ -26,7 +26,7 @@ LAG = 4
 LASTPV = 65
 QE = "ss"
 XQ = 2
-A = {"qk0": -4, "qk1": -3, "w0": -2, "w1": -1, "quant_w": 2, "proj0": 4, "proj1": 5, "y_evac": 6, "quant_va": 5, "quant_vb": 7, "pv0": 10, "pv1": 11, "quant_n": 8, "quant_t1": 4, "recip": 11, "finish": 12, "v0": 0, "v1": 1, "v2": 2, "v3": 3}
+A = {"qk0": -4, "qk1": -3, "w0": -2, "w1": -1, "quant_w": 1, "proj0": 4, "proj1": 5, "y_evac": 6, "quant_va": 6, "quant_vb": 7, "pv0": 10, "pv1": 11, "quant_n": 8, "quant_t1": 4, "recip": 11, "finish": 12, "v0": 0, "v1": 1, "v2": 2, "v3": 3}
 F = {("v0", 0): 2, ("v1", 0): 2, ("w0", 0): 0, ("w1", 0): 0, ("quant_w", 0): 3, ("quant_w", 15): 61, ("proj0", 15): 61, ("proj1", 15): 62, ("y_evac", 15): -9, ("quant_va", 15): 64, ("quant_vb", 15): 63, ("pv0", 14): 64, ("pv1", 14): 64, ("recip", 14): 64, ("finish", 14): 66, ("quant_t1", 15): 63}
 
 
@@ -36,7 +36,7 @@ def tile_flashattentionmodule_pa_kernel(tc, x, q, k_new, past_k, past_v, Wv, bv,
         const = ctx.enter_context(tc.tile_pool(name="const", bufs=1))
         ld = ctx.enter_context(tc.tile_pool(name="ld", bufs=3))
         hd = ctx.enter_context(tc.tile_pool(name="hd", bufs=2))
-        tl = ctx.enter_context(tc.tile_pool(name="tl", bufs=3))
+        tl = ctx.enter_context(tc.tile_pool(name="tl", bufs=4))
         ps_s = ctx.enter_context(tc.psum_pool(name="ps_s", bufs=3))
         ps_t = ctx.enter_context(tc.psum_pool(name="ps_t", bufs=1))
         ps_o = ctx.enter_context(tc.psum_pool(name="ps_o", bufs=1))
@@ -439,12 +439,12 @@ def tile_flashattentionmodule_pa_kernel(tc, x, q, k_new, past_k, past_v, Wv, bv,
                     if hh < H - 2:
                         finish_c(hh, slice(0, NT))
                 quant_past()
-                for hh in heads_at(k, "quant_w"):
-                    quant_w(hh)
-
-            def fill_b():
                 for hh in heads_at(k, "quant_va"):
                     quant_v(hh, 0)
+
+            def fill_b():
+                for hh in heads_at(k, "quant_w"):
+                    quant_w(hh)
                 for hh in heads_at(k, "y_evac"):
                     y_evac(hh)
                 for hh in heads_at(k, "quant_vb"):

@@ -48,13 +48,23 @@ def tile_flashattentionmodule_pa_kernel(tc, x, q, k_new, past_k, past_v, Wv, bv,
         S_PS, S_SB, TP_PS, TN_PS, ETG, ETN = {}, {}, {}, {}, {}, {}
         ET1, C1, S1 = {}, {}, {}
 
-        def load_qk(h):
+        def load_q(h):
             Q_SB[h] = ld.tile([P, NT, HD], BF16, name="q_sb", tag="q_sb")
             nc.sync.dma_start(out=Q_SB[h][:], in_=q[0, h].rearrange("(a p) d -> p a d", p=P))
+
+        def load_kn(h):
             KN_SB[h] = ld.tile([P, NT, HD], BF16, name="kn_sb", tag="kn_sb")
             nc.sync.dma_start(out=KN_SB[h][:].rearrange("p (u e) d -> p u e d", u=2), in_=k_new[0, h].rearrange("(u p e) d -> p u e d", u=2, e=2))
-            PK_SB[h] = ld.tile([P, 8, HD], BF16, name="pk_sb", tag="pk_sb")
-            nc.sync.dma_start(out=PK_SB[h][:], in_=past_k[0, h].rearrange("(p r) d -> p r d", r=8))
+
+        def load_qk(h):
+            load_q(h)
+            load_kn(h)
+            load_pk(h, 0, 8)
+
+        def load_pk(h, lo, hi):
+            if lo == 0:
+                PK_SB[h] = ld.tile([P, 8, HD], BF16, name="pk_sb", tag="pk_sb")
+            nc.sync.dma_start(out=PK_SB[h][:, lo:hi, :], in_=past_k[0, h].rearrange("(p r) d -> p r d", r=8)[:, lo:hi, :])
 
         def load_wv(h):
             W_SB[h] = ld.tile([P, D], BF16, name="w_sb", tag="w_sb", bufs=4)
@@ -64,7 +74,10 @@ def tile_flashattentionmodule_pa_kernel(tc, x, q, k_new, past_k, past_v, Wv, bv,
             PV_SB[h] = ld.tile([P, 8, HD], BF16, name="pv_sb", tag="pv_sb")
             nc.sync.dma_start(out=PV_SB[h][:], in_=past_v[0, h].rearrange("(p r) d -> p r d", r=8))
 
-        load_qk(0)
+        load_q(0)
+        load_pk(0, 0, 4)
+        load_pk(0, 4, 8)
+        load_kn(0)
         x_sb = const.tile([P, NT, D], BF16, name="x_sb")
 
         def load_x(a):
@@ -111,6 +124,8 @@ def tile_flashattentionmodule_pa_kernel(tc, x, q, k_new, past_k, past_v, Wv, bv,
         nm = const.tile([P, NTILES], F32, name="nm")
         nm_g = const.tile([P, 2], F32, name="nm_g")
         sums = const.tile([P, NTILES], F32, name="sums")
+        half_s = const.tile([P, 1], F32, name="half_s")
+        half_v = const.tile([P, 1], F32, name="half_v")
         rinv = const.tile([P, NTILES], F32, name="rinv")
         xg = const.tile([P, 4 * S * 4], BF16, name="xg", align_bytes=64)
         x_codes = const.tile([P, 4 * S], U32, name="x_codes", align_bytes=64)
@@ -283,19 +298,22 @@ def tile_flashattentionmodule_pa_kernel(tc, x, q, k_new, past_k, past_v, Wv, bv,
                 nc.gpsimd.tensor_scalar(out=nm_g[:, n:n + 1], in0=mn3[:, 4 * c:4 * c + 1], scalar1=mn3[:, 4 * c + 1:4 * c + 2],
                                         scalar2=mn3[:, 4 * c + 2:4 * c + 3], op0=ALU.min, op1=ALU.min)
 
-        def st3(n):
+        def st3(n, lo=0, hi=None, total=None):
             h, it = where(n)
             c = h * NT + it
-            b = 9 + it
-            nc.scalar.activation(out=e_row(n)[:, e_first(n):e_first(n) + b * P].rearrange("q (b l e) -> q b l e", b=b, e=2),
-                                 in_=S_SB[n][:, 0:b * P].rearrange("q (b e l) -> q b l e", b=b, e=2),
-                                 func=ACTF.Exp, bias=nm_g[:, n:n + 1] if n < 2 else nm[:, c:c + 1], scale=-1.0, accum_out=sums[:, c:c + 1])
+            hi = hi or 9 + it
+            b = hi - lo
+            o = e_first(n) + lo * P
+            nc.scalar.activation(out=e_row(n)[:, o:o + b * P].rearrange("q (b l e) -> q b l e", b=b, e=2),
+                                 in_=S_SB[n][:, lo * P:hi * P].rearrange("q (b e l) -> q b l e", b=b, e=2),
+                                 func=ACTF.Exp, bias=nm_g[:, n:n + 1] if n < 2 else nm[:, c:c + 1], scale=-1.0,
+                                 accum_out=sums[:, c:c + 1] if total is None else total)
 
-        def st4p(n):
+        def st4p(n, lo=0, hi=4):
             words = e_row(n)[:, e_past(n):e_past(n) + 1024].bitcast(F32)
-            TP_PS[n] = ps_t.tile([P, 4, P], F32, name="tP", tag="tr", bufs=3)
-            for c in range(4):
-                nc.tensor.transpose(TP_PS[n][:, c, :], words[:, c * P:(c + 1) * P], ident_f[:])
+            TP_PS[(n, lo)] = ps_t.tile([P, hi - lo, P], F32, name="tP", tag="tr", bufs=3)
+            for c in range(lo, hi):
+                nc.tensor.transpose(TP_PS[(n, lo)][:, c - lo, :], words[:, c * P:(c + 1) * P], ident_f[:])
 
         def new_op(n):
             h, it = where(n)
@@ -316,11 +334,12 @@ def tile_flashattentionmodule_pa_kernel(tc, x, q, k_new, past_k, past_v, Wv, bv,
             for u in range(2):
                 nc.tensor.transpose(TN_PS[(h, j > 0)][:, max(j - 1, 0), u, :], words[:, u:256:2], ident_f[:])
 
-        def st5a(n, e):
+        def st5a(n, e, lo=0, hi=4):
             if n % 2 == 0:
                 ETG[n // 2] = tl.tile([P, 2048], BF16, name="etg", tag="etg", align_bytes=64)
-            words = ETG[n // 2][:].bitcast(F32).rearrange("p (j g i u) -> p j g i u", j=2, g=2, u=2)
-            evac(e, words[:, n % 2, :, :, :], TP_PS[n][:].rearrange("p (g u) i -> p g i u", u=2))
+            o = n % 2 * 1024 + 256 * lo
+            evac(e, ETG[n // 2][:, o:o + 256 * (hi - lo)].bitcast(F32).rearrange("p (g i u) -> p g i u", g=(hi - lo) // 2, u=2),
+                 TP_PS[(n, lo)][:].rearrange("p (g u) i -> p g i u", u=2))
 
         def st5n(n, e):
             h, it = where(n)
@@ -344,13 +363,13 @@ def tile_flashattentionmodule_pa_kernel(tc, x, q, k_new, past_k, past_v, Wv, bv,
             S1[m] = hd.tile([P, P], U8, name="s1", tag="s1", align_bytes=64)
             nc.vector.quantize_mx(out=C1[m][:].bitcast(FP8X4), scales=S1[m][:], in_=ET1[m][:])
 
-        def st6p(m):
+        def st6p(m, lo=0, hi=2048):
             h, j = divmod(2 * m, NT)
             if j == 0:
                 EC[h] = hd.tile([P, NT * 256 + 256], U32, name="ec", tag="ec", align_bytes=64, bufs=3)
                 ES[h] = hd.tile([P, NT * 256 + 256], U8, name="es", tag="es", align_bytes=64, bufs=3)
-            o = j * 256
-            nc.vector.quantize_mx(out=EC[h][:, o:o + 512].bitcast(FP8X4), scales=ES[h][:, o:o + 512], in_=ETG[m][:])
+            o, e = j * 256 + lo // 4, j * 256 + hi // 4
+            nc.vector.quantize_mx(out=EC[h][:, o:e].bitcast(FP8X4), scales=ES[h][:, o:e], in_=ETG[m][:, lo:hi])
 
         O_PS = {}
         SLOT = {h: {where(h * NT + j)[1]: j for j in range(NT)} for h in range(H)}
@@ -386,7 +405,7 @@ def tile_flashattentionmodule_pa_kernel(tc, x, q, k_new, past_k, past_v, Wv, bv,
                 nc.vector.tensor_tensor(out=o_sb[:, its, :], in0=O_PS[h][:, its, :],
                                         in1=rinv[:, c:c + NT][:, its].unsqueeze(2).to_broadcast([P, n, HD]), op=ALU.mult)
             else:
-                for it in range(NT):
+                for it in range(NT)[its]:
                     nc.scalar.activation(out=o_sb[:, it, :], in_=O_PS[h][:, it, :], func=ACTF.Copy, scale=rinv[:, c + it:c + it + 1])
             nc.sync.dma_start(out=out[0].rearrange("(a p) c -> p a c", p=P)[:, its, h * HD:(h + 1) * HD], in_=o_sb[:, its, :])
 
@@ -396,7 +415,7 @@ def tile_flashattentionmodule_pa_kernel(tc, x, q, k_new, past_k, past_v, Wv, bv,
         def heads_at(k, task):
             return [hh for hh in range(H) if F.get((task, hh), NT * hh + A[task]) == k]
 
-        for j0, tg, e in ((0, "tr", "s"), (4, "tr", "v"), (8, "tr", "v"), (12, "yo", "s")):
+        for j0, tg, e in ((0, "tr", "s"), (8, "tr", "v"), (12, "yo", "s"), (4, "tr", "v")):
             qk_tr(0, j0, 4, tg)
             qk_ev(0, j0, 4, e)
         x_tr(0, 0, "tN")
@@ -418,9 +437,12 @@ def tile_flashattentionmodule_pa_kernel(tc, x, q, k_new, past_k, past_v, Wv, bv,
                 if h + 2 < H:
                     load_pv(h + 2)
             def quant_past():
-                for n in (k - LAG, k - LAG + 1):
-                    if ok(n) and n % 2 == 1 and (n == NTILES - 1) == (n > k - LAG):
-                        st6p(n // 2)
+                n = k - LAG
+                if ok(n) and n % 2 == 1 and n < NTILES - 1:
+                    st6p(n // 2)
+                if k == LASTPV + 1:
+                    for lo, hi in ((0, 1024), (1024, 1536)):
+                        st6p(NTILES // 2 - 1, lo, hi)
 
             def quant_new():
                 for hh in heads_at(k, "quant_n"):
@@ -430,6 +452,7 @@ def tile_flashattentionmodule_pa_kernel(tc, x, q, k_new, past_k, past_v, Wv, bv,
                     st6n(H - 1, 1, 2)
                 if k == LASTPV + 1:
                     st6n(H - 1, 0, 1)
+                    st6p(NTILES // 2 - 1, 1536, 2048)
                 for hh in heads_at(k, "quant_t1"):
                     if hh % 2 == 1:
                         st6t1(hh // 2)
@@ -476,11 +499,13 @@ def tile_flashattentionmodule_pa_kernel(tc, x, q, k_new, past_k, past_v, Wv, bv,
                 fill_b()
             else:
                 if k == LASTPV:
-                    finish_b(H - 1, 0, NT)
+                    finish_b(H - 1, 1, NT)
+                if k == LASTPV + 1:
+                    nc.vector.tensor_tensor(out=half_v[:], in0=half_s[:], in1=sums[:, (H - 1) * NT:(H - 1) * NT + 1], op=ALU.add)
                 fill_a()
                 fill_b()
                 if k == LASTPV + 1:
-                    finish_c(H - 1, slice(1, NT, 2))
+                    nc.vector.reciprocal(out=rinv[:, (H - 1) * NT:(H - 1) * NT + 1], in_=half_v[:])
                 if k == LASTPV + 2:
                     finish_c(H - 1, slice(0, NT, 2))
             for piece in range(4):
@@ -499,6 +524,7 @@ def tile_flashattentionmodule_pa_kernel(tc, x, q, k_new, past_k, past_v, Wv, bv,
                     finish_c(H - 2, slice(0, NT), "s")
                     pv(H - 1, [1, 3], True)
                 if k == LASTPV + 1:
+                    finish_c(H - 1, slice(1, NT, 2), "s")
                     pv(H - 1, [2, 0], False)
                 for half in range(2):
                     for hh in heads_at(k, "pv%d" % half):
@@ -509,13 +535,21 @@ def tile_flashattentionmodule_pa_kernel(tc, x, q, k_new, past_k, past_v, Wv, bv,
 
             if k < NTILES - 1:
                 mx_passes()
-            if ok(k - 1):
+            if ok(k - 1) and k < NTILES:
                 st4p(k - 1)
                 st5a(k - 1, "s")
                 if k == NTILES - 1:
-                    st3(k)
+                    st3(k, 0, 5)
+                    st3(k, 5, 9, half_s[:])
                 st4n(k - 1)
                 st5n(k - 1, "s")
+            if k == NTILES:
+                st4p(k - 1, 0, 2)
+                st5a(k - 1, "s", 0, 2)
+                st4n(k - 1)
+                st5n(k - 1, "s")
+                st4p(k - 1, 2, 4)
+                st5a(k - 1, "s", 2, 4)
             if k >= NTILES - 1:
                 mx_passes()
             if 1 <= k < NT:

@@ -27,7 +27,7 @@ LASTPV = 65
 QE = "ss"
 XQ = 2
 A = {"qk0": -4, "qk1": -3, "w0": -2, "w1": -1, "quant_w": 1, "proj0": 4, "proj1": 5, "y_evac": 6, "quant_va": 6, "quant_vb": 7, "pv0": 10, "pv1": 11, "quant_n": 8, "quant_t1": 4, "recip": 11, "finish": 12, "v0": 0, "v1": 1, "v2": 2, "v3": 3}
-F = {("v0", 0): 2, ("v1", 0): 2, ("w0", 0): 0, ("w1", 0): 0, ("quant_w", 0): 3, ("quant_w", 15): 61, ("proj0", 15): 61, ("proj1", 15): 62, ("y_evac", 15): -9, ("quant_va", 15): 64, ("quant_vb", 15): 63, ("pv0", 14): 64, ("pv1", 14): 64, ("recip", 14): 64, ("finish", 14): 66, ("quant_t1", 15): 63}
+F = {("v0", 0): 2, ("v1", 0): 2, ("w0", 0): -9, ("w1", 0): -9, ("quant_w", 0): 3, ("quant_w", 15): 61, ("proj0", 15): 61, ("proj1", 15): 62, ("y_evac", 15): -9, ("quant_va", 15): 64, ("quant_vb", 15): 63, ("pv0", 14): 64, ("pv1", 14): 64, ("recip", 14): 64, ("finish", 14): 66, ("quant_t1", 15): 63}
 
 
 def tile_flashattentionmodule_pa_kernel(tc, x, q, k_new, past_k, past_v, Wv, bv, out):
@@ -419,12 +419,14 @@ def tile_flashattentionmodule_pa_kernel(tc, x, q, k_new, past_k, past_v, Wv, bv,
             qk_tr(0, j0, 4, tg)
             qk_ev(0, j0, 4, e)
         x_tr(0, 0, "tN")
+        x_tr(0, 1, "yo")
         st1(0, 0)
         st1(0, 1)
         x_ev(0, 0, "s")
-        x_tr(0, 1, "yo")
         x_ev(0, 1, "s")
         st1(0, 2)
+        prep_w(0, 0, "s", "tr")
+        prep_w(0, 1, "s", "tr")
         for k in range(NTILES + 12):
             h, it = divmod(k, NT)
             for hh in heads_at(k - 1, "quant_vb"):
@@ -474,8 +476,10 @@ def tile_flashattentionmodule_pa_kernel(tc, x, q, k_new, past_k, past_v, Wv, bv,
                     if hh < H - 2:
                         quant_v(hh, 1)
                 for hh in heads_at(k, "recip"):
-                    if hh < H - 1:
+                    if hh == H - 2:
                         finish_b(hh, 0, NT)
+                    elif hh % 2 == 0 and hh < H - 2:
+                        finish_b(hh, 0, 2 * NT)
                 quant_new()
 
             if k < NTILES - 1:

import math
from contextlib import ExitStack

import concourse.mybir as mybir
from concourse.masks import make_identity

F32 = mybir.dt.float32
BF16 = mybir.dt.bfloat16
U32 = mybir.dt.uint32
U8 = mybir.dt.uint8
I32 = mybir.dt.int32
FP8X4 = mybir.dt.float8_e4m3fn_x4
ALU = mybir.AluOpType
ACTF = mybir.ActivationFunctionType
AX = mybir.AxisListType

P = 128
S, PAST, D, H, HD = 512, 1024, 2048, 16, 128
NT = S // P
SCALE = 1.0 / math.sqrt(HD)
MASKED = -1.0e30
FLOPS = 2 * S * D * D + 2 * 2 * H * S * (PAST + S) * HD

TBUFS = {"tr": 3, "tN": 1, "yo": 1}
LAG = 4
LASTPV = 65
QE = "ss"
XQ = 2
A = {"qk0": -4, "qk1": -3, "w0": -2, "w1": -1, "quant_w": 1, "proj0": 4, "proj1": 5, "y_evac": 6, "quant_va": 6, "quant_vb": 7, "pv0": 10, "pv1": 11, "quant_n": 8, "quant_t1": 4, "recip": 11, "finish": 12, "v0": 0, "v1": 1, "v2": 2, "v3": 3}
F = {("v0", 0): 2, ("v1", 0): 2, ("w0", 0): -9, ("w1", 0): -9, ("quant_w", 0): 3, ("quant_w", 15): 61, ("proj0", 15): 61, ("proj1", 15): 62, ("y_evac", 15): -9, ("quant_va", 15): 64, ("quant_vb", 15): 63, ("pv0", 14): 64, ("pv1", 14): 64, ("recip", 14): 64, ("finish", 14): 66, ("quant_t1", 15): 63}


def tile_flashattentionmodule_pa_kernel(tc, x, q, k_new, past_k, past_v, Wv, bv, out):
    nc = tc.nc
    with ExitStack() as ctx:
        const = ctx.enter_context(tc.tile_pool(name="const", bufs=1))
        ld = ctx.enter_context(tc.tile_pool(name="ld", bufs=3))
        hd = ctx.enter_context(tc.tile_pool(name="hd", bufs=2))
        tl = ctx.enter_context(tc.tile_pool(name="tl", bufs=4))
        ps_s = ctx.enter_context(tc.psum_pool(name="ps_s", bufs=3))
        ps_t = ctx.enter_context(tc.psum_pool(name="ps_t", bufs=1))
        ps_o = ctx.enter_context(tc.psum_pool(name="ps_o", bufs=1))
        ctx.enter_context(tc.manual_schedule())

        NTILES = H * NT
        Q_SB, KN_SB, PK_SB, PV_SB, W_SB = {}, {}, {}, {}, {}
        QKT, WG, WC, WS, VG, VC, VS, EC, ES, Y_PS = {}, {}, {}, {}, {}, {}, {}, {}, {}, {}
        S_PS, S_SB, TP_PS, TN_PS, ETG, ETN = {}, {}, {}, {}, {}, {}
        ET1, C1, S1 = {}, {}, {}

        def load_q(h):
            Q_SB[h] = ld.tile([P, NT, HD], BF16, name="q_sb", tag="q_sb")
            nc.sync.dma_start(out=Q_SB[h][:], in_=q[0, h].rearrange("(a p) d -> p a d", p=P))

        def load_kn(h):
            KN_SB[h] = ld.tile([P, NT, HD], BF16, name="kn_sb", tag="kn_sb")
            nc.sync.dma_start(out=KN_SB[h][:].rearrange("p (u e) d -> p u e d", u=2), in_=k_new[0, h].rearrange("(u p e) d -> p u e d", u=2, e=2))

        def load_qk(h):
            load_q(h)
            load_kn(h)
            load_pk(h, 0, 8)

        def load_pk(h, lo, hi):
            if lo == 0:
                PK_SB[h] = ld.tile([P, 8, HD], BF16, name="pk_sb", tag="pk_sb")
            nc.sync.dma_start(out=PK_SB[h][:, lo:hi, :], in_=past_k[0, h].rearrange("(p r) d -> p r d", r=8)[:, lo:hi, :])

        def load_wv(h):
            W_SB[h] = ld.tile([P, D], BF16, name="w_sb", tag="w_sb", bufs=4)
            nc.sync.dma_start(out=W_SB[h][:], in_=Wv[h * HD:(h + 1) * HD, :])

        def load_pv(h):
            PV_SB[h] = ld.tile([P, 8, HD], BF16, name="pv_sb", tag="pv_sb")
            nc.sync.dma_start(out=PV_SB[h][:], in_=past_v[0, h].rearrange("(p r) d -> p r d", r=8))

        load_q(0)
        load_pk(0, 0, 4)
        load_pk(0, 4, 8)
        load_kn(0)
        x_sb = const.tile([P, NT, D], BF16, name="x_sb")

        def load_x(a):
            nc.sync.dma_start(out=x_sb[:, a, :], in_=x[0].rearrange("(p t) k -> t p k", t=4)[a])

        for i in range(2):
            nc.sync.dma_start(out=x_sb[:, 0, i * 1024:(i + 1) * 1024],
                              in_=x[0].rearrange("(p t) k -> t p k", t=4)[0][:, i * 1024:(i + 1) * 1024])
        load_wv(0)
        load_qk(1)
        load_x(1)
        load_x(2)
        load_x(3)
        load_pv(0)
        load_wv(1)
        load_pv(1)
        load_wv(2)
        bvb = const.tile([P, D], BF16, name="bvb")
        nc.sync.dma_start(out=bvb[:], in_=bv.partition_broadcast(P))

        warm = const.tile([P, 2], F32, name="warm")
        nc.vector.memset(warm[:, 0:1], 0.0)
        nc.scalar.activation(out=warm[:, 1:2], in_=warm[:, 0:1], func=ACTF.Exp)
        EB = [const.tile([P, 2560], BF16, name="eb%d" % i, align_bytes=64) for i in range(2)]
        ec1 = const.tile([P, 2560], BF16, name="ec1", align_bytes=64)
        e3 = const.tile([P, 1536], BF16, name="e3", align_bytes=64)
        VN, V2, V0, V1 = [], [], [], []
        for name, lst, cnt in (("vn", VN, 3), ("v2_", V2, 2), ("v0_", V0, 2), ("v1_", V1, 2)):
            for i in range(cnt):
                vt = const.tile([P, 5 * HD], U8, name=name + str(i), align_bytes=64)
                nc.vector.memset(vt[:].bitcast(U32), 0)
                lst.append(vt)
        ident_bf = const.tile([P, P], BF16, name="ident_bf")
        make_identity(nc, ident_bf[:])
        ident_f = const.tile([P, P], F32, name="ident_f")
        make_identity(nc, ident_f[:])
        mask_f = const.tile([P, P], F32, name="mask_f")
        nc.gpsimd.memset(mask_f[:], 0.0)
        nc.gpsimd.affine_select(out=mask_f[:], in_=mask_f[:], compare_op=ALU.is_ge, fill=MASKED, base=0,
                                pattern=[[-1, P]], channel_multiplier=1)
        mask_bf = const.tile([P, P], BF16, name="mask_bf")
        nc.vector.tensor_copy(out=mask_bf[:].rearrange("i (e w) -> i e w", e=2), in_=mask_f[:].rearrange("i (w e) -> i e w", e=2))
        mn3 = const.tile([P, NTILES * 4], F32, name="mn3")
        nm = const.tile([P, NTILES], F32, name="nm")
        nm_g = const.tile([P, 2], F32, name="nm_g")
        sums = const.tile([P, NTILES], F32, name="sums")
        half_s = const.tile([P, 1], F32, name="half_s")
        half_v = const.tile([P, 1], F32, name="half_v")
        rinv = const.tile([P, NTILES], F32, name="rinv")
        xg = const.tile([P, 4 * S * 4], BF16, name="xg", align_bytes=64)
        x_codes = const.tile([P, 4 * S], U32, name="x_codes", align_bytes=64)
        x_scales = const.tile([P, 4 * S], U8, name="x_scales", align_bytes=64)

        def evac(eng_name, out_ap, in_ap):
            if eng_name == "v":
                nc.vector.tensor_copy(out=out_ap, in_=in_ap)
            else:
                nc.scalar.copy(out=out_ap, in_=in_ap)

        TX = {}

        def x_tr(a, gp, tg):
            xw = x_sb[:, a, :].bitcast(F32)
            tx = (ps_o if tg == "yo" else ps_t).tile([P, 4, P], F32, name="tx", tag=tg, bufs=TBUFS[tg])
            for j in range(4):
                wb = gp * 4 + j
                nc.tensor.transpose(tx[:, j, :], xw[:, wb * P:(wb + 1) * P], ident_f[:])
            TX[(a, gp)] = tx

        def x_ev(a, gp, e):
            xgw = xg[:].bitcast(F32).rearrange("p (a g k u) -> p a g k u", a=NT, g=4, u=2)
            evac(e, xgw[:, a, 2 * gp:2 * gp + 2, :, :], TX[(a, gp)][:].rearrange("p (g u) k -> p g k u", u=2))

        def x_quant(a):
            nc.vector.quantize_mx(out=x_codes[:, a * 512:(a + 1) * 512].bitcast(FP8X4),
                                  scales=x_scales[:, a * 512:(a + 1) * 512],
                                  in_=xg[:, a * 2048:(a + 1) * 2048])

        TQ = {}

        def qk_tr(h, j0, n, tg):
            if j0 == 0:
                QKT[h] = hd.tile([P, 16 * P], BF16, name="qkT", tag="qkT", bufs=3)
            tq = (ps_o if tg == "yo" else ps_t).tile([P, n, P], BF16, name="tq", tag=tg, bufs=TBUFS[tg])
            for j in range(n):
                dst = tq[:, j, :]
                i = j0 + j
                if i < 4:
                    src = Q_SB[h][:, i, :]
                else:
                    src = KN_SB[h][:, i - 4, :] if i < 8 else PK_SB[h][:, i - 8, :]
                    b, par = divmod(j, 2)
                    dst = tq[:].rearrange("d j i -> d (j i)").rearrange("d (b h e l) -> d b h e l", b=n // 2, h=2, e=2)[:, b, :, par, :]
                nc.tensor.transpose(dst, src, ident_bf[:])
            TQ[(h, j0)] = tq

        def qk_ev(h, j0, n, e):
            evac(e, QKT[h][:, j0 * P:(j0 + n) * P], TQ[(h, j0)][:].rearrange("p j i -> p (j i)"))

        TW = {}

        def prep_w(h, gp, e, tg="tr"):
            w_tr(h, gp, tg)
            w_ev(h, gp, e)

        def w_tr(h, gp, tg):
            if gp == 0:
                WG[h] = hd.tile([P, 4 * HD * 4], BF16, name="wg", tag="wg", align_bytes=64, bufs=4)
            ww = W_SB[h][:].bitcast(F32)
            tw = (ps_o if tg == "yo" else ps_t).tile([P, 4, P], F32, name="tw", tag=tg, bufs=TBUFS[tg])
            for j in range(4):
                wb = gp * 4 + j
                nc.tensor.transpose(tw[:, j, :], ww[:, wb * P:(wb + 1) * P], ident_f[:])
            TW[(h, gp)] = tw

        def w_ev(h, gp, e):
            tw = TW[(h, gp)]
            wgw = WG[h][:].bitcast(F32).rearrange("p (g o u) -> p g o u", g=4, u=2)
            evac(e, wgw[:, 2 * gp:2 * gp + 2, :, :], tw[:].rearrange("p (g u) o -> p g o u", u=2))

        def quant_w(h):
            WC[h] = hd.tile([P, 4 * HD], U32, name="wc", tag="wc", align_bytes=64, bufs=3)
            WS[h] = hd.tile([P, 4 * HD], U8, name="ws", tag="ws", align_bytes=64, bufs=3)
            nc.vector.quantize_mx(out=WC[h][:].bitcast(FP8X4), scales=WS[h][:], in_=WG[h][:])

        def regroup_v(h, piece):
            if piece == 0:
                VG[h] = hd.tile([P, 3 * HD * 4], BF16, name="vg", tag="vg", align_bytes=64, bufs=3)
            g, half = divmod(piece, 2)
            dst = VG[h][:, g * 512 + half * 256:g * 512 + half * 256 + 256].rearrange("p (d t) -> p d t", t=4)
            src = PV_SB[h][:, 4 * g:4 * g + 4, half * 64:half * 64 + 64].rearrange("p t d -> p d t")
            nc.gpsimd.tensor_scalar(out=dst, in0=src, scalar1=1.0, scalar2=0.0, op0=ALU.mult, op1=ALU.add)

        def proj(h, half):
            if half == 0:
                Y_PS[h] = (ps_t if h == H - 1 else ps_o).tile([P, NT, HD], F32, name="y_ps", tag="tr" if h == H - 1 else "yo", bufs=3 if h == H - 1 else 1)
            for jt in range(2 * half, 2 * half + 2):
                for g in range(4):
                    nc.tensor.matmul_mx(
                        out=Y_PS[h][:, jt, :],
                        lhsT=x_codes[:, (jt * 4 + g) * P:(jt * 4 + g + 1) * P].bitcast(FP8X4),
                        lhsT_scale=x_scales[:, (jt * 4 + g) * P:(jt * 4 + g + 1) * P],
                        rhs=WC[h][:, g * HD:(g + 1) * HD].bitcast(FP8X4),
                        rhs_scale=WS[h][:, g * HD:(g + 1) * HD],
                        start=(g == 0), stop=(g == 3))

        def y_evac(h):
            dst = VG[h][:, 2 * HD * 4:3 * HD * 4].rearrange("p (d t) -> p d t", t=4)
            nc.vector.tensor_tensor(out=dst, in0=Y_PS[h][:].rearrange("p t d -> p d t"),
                                    in1=bvb[:, h * HD:(h + 1) * HD].unsqueeze(2).to_broadcast([P, HD, 4]), op=ALU.add)

        def quant_v(h, part):
            if part == 0:
                VC[h] = hd.tile([P, 2 * HD], U32, name="vc", tag="vc", align_bytes=64, bufs=3)
                VS[h] = hd.tile([P, 2 * HD], U8, name="vs", tag="vs", align_bytes=64, bufs=3)
                nc.vector.quantize_mx(out=VC[h][:].bitcast(FP8X4), scales=VS[h][:], in_=VG[h][:, 0:1024])
            else:
                vn = VN[h % 3]
                nc.vector.quantize_mx(out=vn[:, 0:512].bitcast(FP8X4), scales=vn[:, 512:640], in_=VG[h][:, 1024:1536])

        def spread_v(h):
            r = 64 * (h % 2)
            vn = VN[h % 3]
            nc.sync.dma_start(out=V1[h % 2][r:r + 64, :].bitcast(I32), in_=vn[0:64, :].bitcast(I32))
            nc.sync.dma_start(out=V0[h % 2][96:128, :].bitcast(I32), in_=vn[0:32, :].bitcast(I32))
            nc.sync.dma_start(out=V2[h % 2][0:96, :].bitcast(I32), in_=vn[0:96, :].bitcast(I32))

        def where(n):
            h, j = divmod(n, NT)
            return h, ((1, 3, 2, 0)[j] if h == H - 1 else j)

        def flipped(n):
            h, it = where(n)
            return it == 0 or it == 1 and h % 2 == 1

        def e_row(n):
            h, it = where(n)
            return ec1 if it == 1 else EB[h % 2] if it % 2 == 0 else e3

        def e_first(n):
            return 0 if not flipped(n) else 1408 if where(n)[1] == 0 else 1280

        def e_past(n):
            return 1536 if flipped(n) else 0

        def widths(it):
            return [512, 512, P * (it + 1)]

        def st1(n, part):
            h, it = where(n)
            kt = QKT[h]
            lhsT = kt[:, it * P:(it + 1) * P]
            if part == 0:
                S_PS[n] = []
            ps = ps_s.tile([P, 512], F32, name="ps", tag="s")
            S_PS[n].append(ps)
            if part < 2:
                nc.tensor.matmul(out=ps[:], lhsT=lhsT, rhs=kt[:, 1024 + 512 * part:1536 + 512 * part], start=True, stop=True)
            else:
                w = P * (it + 1)
                nc.tensor.matmul(out=ps[:, 0:w], lhsT=lhsT, rhs=kt[:, 512:512 + w], start=True, stop=False)
                nc.tensor.matmul(out=ps[:, w - P:w], lhsT=ident_bf[:], rhs=mask_bf[:], start=False, stop=True)

        def st2(n, part):
            h, it = where(n)
            c = h * NT + it
            if part == 0:
                S_SB[n] = tl.tile([P, 1536], F32, name="s_sb", tag="s_sb")
            w = widths(it)[part]
            nw = P * (it + 1)
            o = (nw, nw + 512, 0)[part] if flipped(n) else 512 * part
            chained = n >= 2
            nc.vector.tensor_scalar(out=S_SB[n][:, o:o + w], in0=S_PS[n][part][:, 0:w], scalar1=-SCALE,
                                    scalar2=mn3[:, 4 * c + part - 1:4 * c + part] if chained and part > 0 else None,
                                    op0=ALU.mult, op1=ALU.min,
                                    accum_out=nm[:, c:c + 1] if chained and part == 2 else mn3[:, 4 * c + part:4 * c + part + 1])
            if part == 2 and not chained:
                nc.gpsimd.tensor_scalar(out=nm_g[:, n:n + 1], in0=mn3[:, 4 * c:4 * c + 1], scalar1=mn3[:, 4 * c + 1:4 * c + 2],
                                        scalar2=mn3[:, 4 * c + 2:4 * c + 3], op0=ALU.min, op1=ALU.min)

        def st3(n, lo=0, hi=None, total=None):
            h, it = where(n)
            c = h * NT + it
            hi = hi or 9 + it
            b = hi - lo
            o = e_first(n) + lo * P
            nc.scalar.activation(out=e_row(n)[:, o:o + b * P].rearrange("q (b l e) -> q b l e", b=b, e=2),
                                 in_=S_SB[n][:, lo * P:hi * P].rearrange("q (b e l) -> q b l e", b=b, e=2),
                                 func=ACTF.Exp, bias=nm_g[:, n:n + 1] if n < 2 else nm[:, c:c + 1], scale=-1.0,
                                 accum_out=sums[:, c:c + 1] if total is None else total)

        def st4p(n, lo=0, hi=4):
            words = e_row(n)[:, e_past(n):e_past(n) + 1024].bitcast(F32)
            TP_PS[(n, lo)] = ps_t.tile([P, hi - lo, P], F32, name="tP", tag="tr", bufs=3)
            for c in range(lo, hi):
                nc.tensor.transpose(TP_PS[(n, lo)][:, c - lo, :], words[:, c * P:(c + 1) * P], ident_f[:])

        def new_op(n):
            h, it = where(n)
            if it == 3:
                return 2
            if it == 1:
                return 0 if h % 2 == 1 else None
            return 1 if it == (0 if h == H - 1 else 2) else None

        def st4n(n):
            h, it = where(n)
            j = new_op(n)
            if j is None:
                return
            if (h, j > 0) not in TN_PS:
                TN_PS[(h, j > 0)] = ps_t.tile([P, 2, 2, P], F32, name="tN", tag="tN", bufs=1)
            words = e_row(n)[:, 1024:1536].bitcast(F32)
            for u in range(2):
                nc.tensor.transpose(TN_PS[(h, j > 0)][:, max(j - 1, 0), u, :], words[:, u:256:2], ident_f[:])

        def st5a(n, e, lo=0, hi=4):
            if n % 2 == 0:
                ETG[n // 2] = tl.tile([P, 2048], BF16, name="etg", tag="etg", align_bytes=64)
            o = n % 2 * 1024 + 256 * lo
            evac(e, ETG[n // 2][:, o:o + 256 * (hi - lo)].bitcast(F32).rearrange("p (g i u) -> p g i u", g=(hi - lo) // 2, u=2),
                 TP_PS[(n, lo)][:].rearrange("p (g u) i -> p g i u", u=2))

        def st5n(n, e):
            h, it = where(n)
            j = new_op(n)
            if j == 0:
                ET1[h // 2] = hd.tile([P, 512], BF16, name="et1", tag="et1", align_bytes=64)
                evac(e, ET1[h // 2][:].bitcast(F32).rearrange("p (i u) -> p i u", u=2), TN_PS[(h, False)][:, 0, :, :].rearrange("p u i -> p i u"))
                return
            if h not in ETN:
                ETN[h] = hd.tile([P, 1024], BF16, name="etn", tag="etn", align_bytes=64)
            for lo, hi in ([(j - 1, j)] if j and h == H - 1 else [(0, 2)] if j == 2 else []):
                evac(e, ETN[h][:, 512 * lo:512 * hi].bitcast(F32).rearrange("p (j i u) -> p j i u", j=hi - lo, u=2),
                     TN_PS[(h, True)][:, lo:hi, :, :].rearrange("p j u i -> p j i u"))

        def st6n(h, lo, hi):
            o, e = 1024 + P * lo, 1024 + P * hi
            nc.vector.quantize_mx(out=EC[h][:, o:e].bitcast(FP8X4), scales=ES[h][:, o:e], in_=ETN[h][:, 512 * lo:512 * hi])

        def st6t1(m):
            C1[m] = hd.tile([P, P], U32, name="c1", tag="c1", align_bytes=64)
            S1[m] = hd.tile([P, P], U8, name="s1", tag="s1", align_bytes=64)
            nc.vector.quantize_mx(out=C1[m][:].bitcast(FP8X4), scales=S1[m][:], in_=ET1[m][:])

        def st6p(m, lo=0, hi=2048):
            h, j = divmod(2 * m, NT)
            if j == 0:
                EC[h] = hd.tile([P, NT * 256 + 256], U32, name="ec", tag="ec", align_bytes=64, bufs=3)
                ES[h] = hd.tile([P, NT * 256 + 256], U8, name="es", tag="es", align_bytes=64, bufs=3)
            o, e = j * 256 + lo // 4, j * 256 + hi // 4
            nc.vector.quantize_mx(out=EC[h][:, o:e].bitcast(FP8X4), scales=ES[h][:, o:e], in_=ETG[m][:, lo:hi])

        O_PS = {}
        SLOT = {h: {where(h * NT + j)[1]: j for j in range(NT)} for h in range(H)}

        def pv(h, its, first):
            if h == H - 1:
                O_PS[h] = ps_s.tile([P, NT, HD], F32, name="o_ps", tag="s")
            elif first:
                O_PS[h] = ps_o.tile([P, NT, HD], F32, name="o_ps", tag="yo", bufs=1)
            for it in its:
                j = SLOT[h][it]
                vn = (V0[h % 2], V1[h % 2], V2[h % 2], VN[h % 3])[it]
                for g in range(3):
                    ec, es = EC[h], ES[h]
                    o = j * 256 + g * P if g < 2 else 1024 + (it == 3) * P
                    if g == 2 and it == 1:
                        ec, es, o = C1[h // 2], S1[h // 2], 0
                    nc.tensor.matmul_mx(out=O_PS[h][:, it, :],
                                        lhsT=ec[:, o:o + P].bitcast(FP8X4), lhsT_scale=es[:, o:o + P],
                                        rhs=(VC[h][:, g * HD:(g + 1) * HD] if g < 2 else vn[:, 0:512]).bitcast(FP8X4),
                                        rhs_scale=VS[h][:, g * HD:(g + 1) * HD] if g < 2 else vn[:, 512:640],
                                        start=(g == 0), stop=(g == 2))

        def finish_b(h, lo, hi):
            c = h * NT
            nc.vector.reciprocal(out=rinv[:, c + lo:c + hi], in_=sums[:, c + lo:c + hi])

        def finish_c(h, its, e="v"):
            c = h * NT
            o_sb = hd.tile([P, NT, HD], F32, name="o_sb", tag="o_sb", bufs=4)
            n = len(range(NT)[its])
            if e == "v":
                nc.vector.tensor_tensor(out=o_sb[:, its, :], in0=O_PS[h][:, its, :],
                                        in1=rinv[:, c:c + NT][:, its].unsqueeze(2).to_broadcast([P, n, HD]), op=ALU.mult)
            else:
                for it in range(NT)[its]:
                    nc.scalar.activation(out=o_sb[:, it, :], in_=O_PS[h][:, it, :], func=ACTF.Copy, scale=rinv[:, c + it:c + it + 1])
            nc.sync.dma_start(out=out[0].rearrange("(a p) c -> p a c", p=P)[:, its, h * HD:(h + 1) * HD], in_=o_sb[:, its, :])

        def ok(n):
            return 0 <= n < NTILES

        def heads_at(k, task):
            return [hh for hh in range(H) if F.get((task, hh), NT * hh + A[task]) == k]

        for j0, tg, e in ((0, "tr", "s"), (8, "tr", "v"), (12, "yo", "s"), (4, "tr", "v")):
            qk_tr(0, j0, 4, tg)
            qk_ev(0, j0, 4, e)
        x_tr(0, 0, "tN")
        x_tr(0, 1, "yo")
        st1(0, 0)
        st1(0, 1)
        x_ev(0, 0, "s")
        x_ev(0, 1, "s")
        st1(0, 2)
        prep_w(0, 0, "s", "tr")
        prep_w(0, 1, "s", "tr")
        for k in range(NTILES + 12):
            h, it = divmod(k, NT)
            for hh in heads_at(k - 1, "quant_vb"):
                spread_v(hh)
            if it == 0:
                if h + 2 < H:
                    load_qk(h + 2)
                if h + 3 < H:
                    load_wv(h + 3)
                if h + 2 < H:
                    load_pv(h + 2)
            def quant_past():
                n = k - LAG
                if ok(n) and n % 2 == 1 and n < NTILES - 1:
                    st6p(n // 2)
                if k == LASTPV + 1:
                    for lo, hi in ((0, 1024), (1024, 1536)):
                        st6p(NTILES // 2 - 1, lo, hi)

            def quant_new():
                for hh in heads_at(k, "quant_n"):
                    if hh < H - 1:
                        st6n(hh, 0, 2)
                if k == LASTPV:
                    st6n(H - 1, 1, 2)
                if k == LASTPV + 1:
                    st6n(H - 1, 0, 1)
                    st6p(NTILES // 2 - 1, 1536, 2048)
                for hh in heads_at(k, "quant_t1"):
                    if hh % 2 == 1:
                        st6t1(hh // 2)

            def fill_a():
                for hh in heads_at(k, "finish"):
                    if hh < H - 2:
                        finish_c(hh, slice(0, NT))
                quant_past()
                for hh in heads_at(k, "quant_va"):
                    quant_v(hh, 0)

            def fill_b():
                for hh in heads_at(k, "quant_w"):
                    quant_w(hh)
                for hh in heads_at(k, "y_evac"):
                    y_evac(hh)
                for hh in heads_at(k, "quant_vb"):
                    if hh < H - 2:
                        quant_v(hh, 1)
                for hh in heads_at(k, "recip"):
                    if hh == H - 2:
                        finish_b(hh, 0, NT)
                    elif hh % 2 == 0 and hh < H - 2:
                        finish_b(hh, 0, 2 * NT)
                quant_new()

            if k < NTILES - 1:
                st2(k, 0)
                if 0 <= k - XQ < NT:
                    x_quant(k - XQ)
                fill_a()
                st2(k, 1)
                if 1 <= k - 1 < NT:
                    x_ev(k - 1, 1, "v")
                fill_b()
                st2(k, 2)
            elif k == NTILES - 1:
                st2(k, 0)
                quant_v(H - 2, 1)
                y_evac(H - 1)
                st2(k, 1)
                quant_v(H - 1, 1)
                st2(k, 2)
                fill_a()
                fill_b()
            else:
                if k == LASTPV:
                    finish_b(H - 1, 1, NT)
                if k == LASTPV + 1:
                    nc.vector.tensor_tensor(out=half_v[:], in0=half_s[:], in1=sums[:, (H - 1) * NT:(H - 1) * NT + 1], op=ALU.add)
                fill_a()
                fill_b()
                if k == LASTPV + 1:
                    nc.vector.reciprocal(out=rinv[:, (H - 1) * NT:(H - 1) * NT + 1], in_=half_v[:])
                if k == LASTPV + 2:
                    finish_c(H - 1, slice(0, NT, 2))
            for piece in range(4):
                for hh in heads_at(k, "v%d" % piece):
                    regroup_v(hh, piece)
            if ok(k + 1):
                st1(k + 1, 0)
                st1(k + 1, 1)
                if k == 0:
                    st1(k + 1, 2)
            if k < NTILES - 1:
                st3(k)

            def mx_passes():
                if k == LASTPV:
                    finish_c(H - 2, slice(0, NT), "s")
                    pv(H - 1, [1, 3], True)
                if k == LASTPV + 1:
                    finish_c(H - 1, slice(1, NT, 2), "s")
                    pv(H - 1, [2, 0], False)
                for half in range(2):
                    for hh in heads_at(k, "pv%d" % half):
                        if hh < H - 1:
                            pv(hh, [2 * half, 2 * half + 1], half == 0)
                    for hh in heads_at(k, "proj%d" % half):
                        proj(hh, half)

            if k < NTILES - 1:
                mx_passes()
            if ok(k - 1) and k < NTILES:
                st4p(k - 1)
                st5a(k - 1, "s")
                if k == NTILES - 1:
                    st3(k, 0, 5)
                    st3(k, 5, 9, half_s[:])
                st4n(k - 1)
                st5n(k - 1, "s")
            if k == NTILES:
                st4p(k - 1, 0, 2)
                st5a(k - 1, "s", 0, 2)
                st4n(k - 1)
                st5n(k - 1, "s")
                st4p(k - 1, 2, 4)
                st5a(k - 1, "s", 2, 4)
            if k >= NTILES - 1:
                mx_passes()
            if 1 <= k < NT:
                x_tr(k, 0, "tr")
                x_ev(k, 0, "s")
                x_tr(k, 1, "yo")
            for part in range(2):
                for hh in heads_at(k, "w%d" % part):
                    prep_w(hh, part, "s", "tr")
                for hh in heads_at(k, "qk%d" % part):
                    if hh > 0:
                        qk_tr(hh, 8 * part, 8, "tr")
                        qk_ev(hh, 8 * part, 8, "s")
            if ok(k + 1) and k > 0:
                st1(k + 1, 2)
